import numpy as np
import ml_dtypes


def mxq(x, axis, fmt="e4m3"):
    dtype, down = {"e4m3": (ml_dtypes.float8_e4m3fn, 7), "e5m2": (ml_dtypes.float8_e5m2, 14)}[fmt]
    v = np.moveaxis(np.asarray(x, np.float32).astype(ml_dtypes.bfloat16).astype(np.float64), axis, -1)
    blocks = v.reshape(v.shape[:-1] + (-1, 32))
    amax = np.abs(blocks).max(-1, keepdims=True)
    byte = np.maximum(np.where(amax > 0, np.frexp(amax)[1] - 1 + 127, 0) - down, 1)
    scale = np.exp2(byte - 127.0)
    codes = (blocks / scale).astype(np.float32).astype(dtype).astype(np.float64)
    return np.moveaxis((codes * scale).reshape(v.shape), -1, axis)


WIDE = False


def mx_kscale(k):
    if not WIDE:
        return np.ones(k)
    levels = np.array([10, -10, 5, -5, 0])
    if k % 512:
        return np.exp2(np.random.permutation(np.resize(levels, k // 32))).repeat(32)
    a = np.empty((k // 512, 16))
    for p in range(k // 512):
        a[p, :8] = np.random.permutation(np.resize(levels, 8))
        for g in range(8):
            far = levels[np.abs(levels - a[p, g]) >= 10]
            a[p, g + 8] = far[np.random.randint(len(far))]
    return np.exp2(a.ravel()).repeat(32)


BF16 = ml_dtypes.bfloat16


def bf(x):
    return np.asarray(x, np.float32).astype(BF16)


def f64(x):
    return np.asarray(x).astype(np.float64)


E2M1 = np.array([0.0, 0.5, 1.0, 1.5, 2.0, 3.0, 4.0, 6.0, -0.0, -0.5, -1.0, -1.5, -2.0, -3.0, -4.0, -6.0])


def pack_weight(w, fmt):
    k, n = w.shape
    w = f64(bf(w)).reshape(k // 32, 32, n)
    amax = np.abs(w).max(1)
    if fmt == "e4m3":
        byte = np.frexp(amax)[1] - 1 + 127 - 7
    else:
        mant, ex = np.frexp(amax / 6.0)
        byte = np.where(mant > 0.5, ex, ex - 1) + 127
    byte = np.clip(np.where(amax > 0, byte, 1), 1, 254)
    scaled = (w * np.exp2(127.0 - byte)[:, None, :]).reshape(k, n).astype(np.float32)
    by_word = np.ascontiguousarray(scaled.reshape(k // 512, 128, 4, n).transpose(0, 1, 3, 2))
    if fmt == "e4m3":
        words = by_word.astype(ml_dtypes.float8_e4m3fn).view(np.uint8)
    else:
        c = by_word.astype(ml_dtypes.float4_e2m1fn).view(np.uint8) & 0xF
        words = c[..., 0::2] | (c[..., 1::2] << 4)
    return np.ascontiguousarray(words), np.ascontiguousarray(byte.astype(np.uint8).reshape(k // 512, 16, n))


def unpack_weight(words, scales, fmt):
    g, p, n, _ = words.shape
    if fmt == "e4m3":
        vals = np.ascontiguousarray(words).view(ml_dtypes.float8_e4m3fn).astype(np.float64)
    else:
        nib = np.empty((g, p, n, 4), np.uint8)
        nib[..., 0::2] = words & 0xF
        nib[..., 1::2] = words >> 4
        vals = E2M1[nib]
    vals = vals * np.repeat(np.exp2(scales.astype(np.float64) - 127.0), 8, axis=1)[..., None]
    return vals.transpose(0, 1, 3, 2).reshape(g * 512, n)


B, IN, M, OUT = 1024, 1024, 512, 512
F = 2 * M
EPS = 1e-12


def draw0():
    s, t = mx_kscale(IN), mx_kscale(F)
    x = bf(np.random.standard_normal((B, IN)) * s)
    W1_words, W1_scales = pack_weight(np.random.standard_normal((IN, F)) / np.sqrt(IN) / s[:, None] * t, "e4m3")
    b1 = bf(np.random.standard_normal(F) * 0.1 * t)
    W2_words, W2_scales = pack_weight(np.random.standard_normal((F, M)) / np.sqrt(F) / t[:, None], "e4m3")
    b2 = bf(np.random.standard_normal(M) * 0.3)
    return {"x": x,
            "W1_words": W1_words, "W1_scales": W1_scales,
            "b1": b1,
            "W2_words": W2_words, "W2_scales": W2_scales,
            "b2": b2}


def core(x, W1_words, W1_scales, b1, W2_words, W2_scales, b2):
    h = np.maximum((mxq(f64(x), 1, "e4m3") @ unpack_weight(W1_words, W1_scales, "e4m3")) + f64(b1), 0.0)
    v = (mxq(h, 1, "e4m3") @ unpack_weight(W2_words, W2_scales, "e4m3")) + f64(b2)
    norm = np.sqrt(np.sum(v * v, axis=-1, keepdims=True))
    return v / np.maximum(norm, EPS)


def e4m3fn_bytes(y):
    return np.clip(np.asarray(y, np.float64), -448.0, 448.0).astype(np.float32).astype(ml_dtypes.float8_e4m3fn).view(np.uint8)


def e4m3fn_values(b):
    return np.asarray(b, np.uint8).view(ml_dtypes.float8_e4m3fn).astype(np.float64)


def setup_inputs():
    d = draw0()
    x0 = np.asarray(d['x']).astype(np.float64)
    s = (np.max(np.abs(x0), axis=(0,), keepdims=True) / 448.0).astype(np.float32)
    out = {}
    for k, v in d.items():
        if k == 'x':
            out['x_bytes'] = e4m3fn_bytes(x0 / s.astype(np.float64))
            out['x_scale'] = s
        else:
            out[k] = v
    return out


def reference(x_bytes, x_scale, W1_words, W1_scales, b1, W2_words, W2_scales, b2):
    return core(e4m3fn_values(x_bytes) * x_scale.astype(np.float64), W1_words, W1_scales, b1, W2_words, W2_scales, b2)

@@ -1,0 +1,296 @@
+from contextlib import ExitStack
+
+import concourse.mybir as mybir
+from concourse.masks import make_identity
+
+FLOPS = 2 * 1024 * 1024 * 1024 + 2 * 1024 * 1024 * 512
+
+F32 = mybir.dt.float32
+BF16 = mybir.dt.bfloat16
+U32 = mybir.dt.uint32
+I32 = mybir.dt.int32
+U8 = mybir.dt.uint8
+FP8 = mybir.dt.float8_e4m3fn
+FP8X4 = mybir.dt.float8_e4m3fn_x4
+ACT = mybir.ActivationFunctionType
+ALU = mybir.AluOpType
+
+P = 128
+K = 1024
+NOUT = 512
+CHUNKS = ((0, 1), (128, 2), (384, 2), (640, 2), (896, 1))
+S_WEAVE = ((0,0),(0,0),(0,0),(0,0),(0,0))
+FIN = ("G", "GG", "GG", "GG", "V")
+NCH = len(CHUNKS)
+
+
+def tile_geometricmanifoldnetwork_pa_w8_kernel(
+    tc, x_bytes, x_scale, W1_words, W1_scales, b1, W2_words, W2_scales, b2, out
+):
+    nc = tc.nc
+    with ExitStack() as ctx:
+        keep = ctx.enter_context(tc.tile_pool(name="keep", bufs=1))
+        work = ctx.enter_context(tc.tile_pool(name="work", bufs=3))
+        psx = ctx.enter_context(tc.psum_pool(name="psx", bufs=1))
+        psh = ctx.enter_context(tc.psum_pool(name="psh", bufs=4))
+        psy = ctx.enter_context(tc.psum_pool(name="psy", bufs=2))
+        ctx.enter_context(tc.manual_schedule())
+
+        s1raw = keep.tile([P, K], U8, name="s1raw", align_bytes=64)
+        s1 = keep.tile([P, K], U8, name="s1", align_bytes=64)
+        s2 = keep.tile([P, NOUT], U8, name="s2", align_bytes=64)
+        nc.vector.memset(s1raw[:].bitcast(I32), 0)
+        nc.vector.memset(s2[:].bitcast(I32), 0)
+        half = keep.tile([P, 2], F32, name="half")
+        nc.vector.memset(half[:], -0.5)
+        warm = keep.tile([P, 2], BF16, name="warm")
+        nc.scalar.activation(out=warm[:], in_=half[:], func=ACT.Relu)
+        ident = keep.tile([P, P], F32, name="ident", align_bytes=64)
+        make_identity(nc, ident[:])
+
+        xbytes = []
+        for c, (t0, J) in enumerate(CHUNKS):
+            xbytes.append(keep.tile([P, J, K], U8, name="xbytes%d" % c, align_bytes=64))
+
+        def load_x(c):
+            t0, J = CHUNKS[c]
+            nc.sync.dma_start(out=xbytes[c][:], in_=x_bytes[t0 : t0 + P * J, :].rearrange("(p j) k -> p j k", j=J))
+
+        w1raw = [keep.tile([P, 2, 512], I32, name="w1raw%d" % t, align_bytes=64) for t in range(2)]
+        w1 = [keep.tile([P, 2, 512], U32, name="w1_%d" % t, align_bytes=64) for t in range(2)]
+        w2 = keep.tile([P, 2, 512], U32, name="w2", align_bytes=64)
+
+        xsc = keep.tile([P, 2, 2, 2], F32, name="xsc")
+        nc.scalar.dma_start(
+            out=xsc[:].rearrange("p g u e -> p g (u e)"),
+            in_=x_scale.rearrange("o (g p t) -> p (o g) t", g=2, t=4),
+        )
+        b1t = keep.tile([P, 2, 4], BF16, name="b1t")
+        nc.scalar.dma_start(out=b1t[:], in_=b1.rearrange("(g p t) -> p g t", g=2, t=4))
+
+        load_x(0)
+        load_x(1)
+        for q in range(4):
+            nc.sync.dma_start(
+                out=s1raw[32 * q : 32 * q + 8, :].bitcast(I32),
+                in_=W1_scales[:, 4 * q : 4 * q + 4, :].bitcast(I32),
+            )
+        w1i = W1_words.rearrange("g p n t -> p g (n t)").bitcast(I32)
+        for t in range(2):
+            nc.sync.dma_start(out=w1raw[t][:], in_=w1i[:, :, 512 * t : 512 * t + 512])
+        load_x(2)
+        nc.sync.dma_start(out=w2[:].bitcast(I32), in_=W2_words.rearrange("g p n t -> p g (n t)").bitcast(I32))
+        for q in range(4):
+            nc.sync.dma_start(
+                out=s2[32 * q : 32 * q + 8, :].bitcast(I32),
+                in_=W2_scales[:, 4 * q : 4 * q + 4, :].bitcast(I32),
+            )
+        load_x(3)
+        load_x(4)
+        b2t = keep.tile([P, NOUT], BF16, name="b2t")
+        nc.sync.dma_start(out=b2t[:], in_=b2.partition_broadcast(P))
+
+        xv = [keep.tile([P, J, K], BF16, name="xv%d" % c, align_bytes=64) for c, (t0, J) in enumerate(CHUNKS)]
+        xt = {}
+        grp = {}
+        xq = {}
+        xs = {}
+        ph = {}
+        hp = {}
+        hg = {}
+        hq = {}
+        hs = {}
+        py = {}
+        v = {}
+        ssq = {}
+
+        def cast(c, j):
+            nc.scalar.copy(out=xv[c][:, j, :], in_=xbytes[c][:, j, :].bitcast(FP8))
+
+        def turn(c):
+            J = CHUNKS[c][1]
+            for g in range(2):
+                xt[c, g] = psx.tile([P, 2, P * J], F32, name="xt%d" % g)
+            words = xv[c][:].bitcast(F32)
+            for j in range(J):
+                for g in range(2):
+                    for u in range(2):
+                        nc.tensor.transpose(
+                            xt[c, g][:, u, P * j : P * j + P],
+                            words[:, j, 256 * g + u : 256 * (g + 1) : 2],
+                            ident[:],
+                        )
+
+        def scale_x(c, g):
+            n = P * CHUNKS[c][1]
+            if g == 0:
+                grp[c] = work.tile([P, 2, n, 4], BF16, name="grp", align_bytes=64)
+            nc.vector.tensor_tensor(
+                out=grp[c][:, g, :, :].rearrange("p n (u e) -> p n u e", e=2),
+                in0=xt[c, g][:].bitcast(BF16).rearrange("p u (n e) -> p n u e", e=2),
+                in1=xsc[:, g, :, :].unsqueeze(1).to_broadcast([P, n, 2, 2]),
+                op=ALU.mult,
+            )
+
+        def quant_x(c):
+            n = P * CHUNKS[c][1]
+            xq[c] = work.tile([P, 2, n], U32, name="xq", align_bytes=64)
+            xs[c] = work.tile([P, 2, n], U8, name="xs", align_bytes=64)
+            nc.vector.quantize_mx(
+                out=xq[c][:].rearrange("p g n -> p (g n)").bitcast(FP8X4),
+                scales=xs[c][:].rearrange("p g n -> p (g n)"),
+                in_=grp[c][:].rearrange("p g n t -> p (g n t)"),
+            )
+
+        def stage1(c, T):
+            n = P * CHUNKS[c][1]
+            for t in range(4):
+                if t % 2 == 0:
+                    ph[c, T, t // 2] = psh.tile([P, 2, n], F32, name="ph")
+                cols = slice(128 * t, 128 * t + 128)
+                for g in range(2):
+                    nc.tensor.matmul_mx(
+                        out=ph[c, T, t // 2][:, t % 2, :],
+                        lhsT=w1[T][:, g, cols].bitcast(FP8X4),
+                        lhsT_scale=s1[4 * g :, 512 * T + 128 * t : 512 * T + 128 * t + 128],
+                        rhs=xq[c][:, g, :].bitcast(FP8X4),
+                        rhs_scale=xs[c][:, g, :],
+                        start=(g == 0),
+                        stop=(g == 1),
+                    )
+
+        def exit_h(c, T):
+            n = P * CHUNKS[c][1]
+            hp[c, T] = work.tile([P, 4, n], BF16, name="hp", align_bytes=64)
+            for t in range(4):
+                nc.scalar.activation(
+                    out=hp[c, T][:, t, :],
+                    in_=ph[c, T, t // 2][:, t % 2, :],
+                    func=ACT.Relu,
+                    bias=b1t[:, T, t : t + 1],
+                )
+
+        def weave_h(c, T):
+            n = P * CHUNKS[c][1]
+            hg[c, T] = work.tile([P, n, 4], BF16, name="hg", align_bytes=64)
+            cut = n - S_WEAVE[c][T]
+            for copy, cols in ((nc.vector.tensor_copy, slice(0, cut)), (nc.scalar.copy, slice(cut, n))):
+                if cols.start < cols.stop:
+                    copy(
+                        out=hg[c, T][:, cols, :].rearrange("p (c i) t -> p c t i", i=4),
+                        in_=hp[c, T][:, :, cols].rearrange("p t (c i) -> p c t i", i=4),
+                    )
+
+        def quant_h(c, T):
+            n = P * CHUNKS[c][1]
+            if T == 0:
+                hq[c] = work.tile([P, 2, n], U32, name="hq", align_bytes=64)
+                hs[c] = work.tile([P, 2, n], U8, name="hs", align_bytes=64)
+            nc.vector.quantize_mx(
+                out=hq[c][:, T, :].bitcast(FP8X4),
+                scales=hs[c][:, T, :],
+                in_=hg[c, T][:].rearrange("p n t -> p (n t)"),
+            )
+
+        def stage2(c):
+            for j in range(CHUNKS[c][1]):
+                py[c, j] = psy.tile([P, NOUT], F32, name="py")
+                for T in range(2):
+                    nc.tensor.matmul_mx(
+                        out=py[c, j][:],
+                        lhsT=hq[c][:, T, P * j : P * j + P].bitcast(FP8X4),
+                        lhsT_scale=hs[c][:, T, P * j : P * j + P],
+                        rhs=w2[:, T, :].bitcast(FP8X4),
+                        rhs_scale=s2[4 * T :, :],
+                        start=(T == 0),
+                        stop=(T == 1),
+                    )
+
+        def bias_v(c, j):
+            J = CHUNKS[c][1]
+            if j == 0:
+                v[c] = work.tile([P, J, NOUT], F32, name="v", align_bytes=64)
+                ssq[c] = work.tile([P, 2], F32, name="ssq")
+            nc.vector.tensor_tensor(out=v[c][:, j, :], in0=py[c, j][:], in1=b2t[:], op=ALU.add)
+
+        def square_v(c, j):
+            junk = work.tile([P, NOUT], BF16, name="junk", align_bytes=64)
+            nc.scalar.activation(out=junk[:], in_=v[c][:, j, :], func=ACT.Square, accum_out=ssq[c][:, j : j + 1])
+
+        def finish_v(c):
+            t0, J = CHUNKS[c]
+            clamped = work.tile([P, 2], F32, name="clamped")
+            r = work.tile([P, 2], F32, name="r")
+            o = work.tile([P, J, NOUT], F32, name="o", align_bytes=64)
+            nc.gpsimd.tensor_scalar(
+                out=clamped[:, 0:J], in0=ssq[c][:, 0:J], scalar1=1e-24, scalar2=None, op0=ALU.max
+            )
+            nc.gpsimd.tensor_tensor(out=r[:, 0:J], in0=clamped[:, 0:J], in1=half[:, 0:J], op=ALU.pow)
+            for j in range(J):
+                if FIN[c][j] == "S":
+                    nc.scalar.activation(out=o[:, j, :], in_=v[c][:, j, :], func=ACT.Copy, scale=r[:, j : j + 1])
+                elif FIN[c][j] == "V":
+                    nc.vector.tensor_scalar(
+                        out=o[:, j, :], in0=v[c][:, j, :], scalar1=r[:, j : j + 1], scalar2=None, op0=ALU.mult
+                    )
+                else:
+                    nc.gpsimd.tensor_scalar(
+                        out=o[:, j, :], in0=v[c][:, j, :], scalar1=r[:, j : j + 1], scalar2=0.0,
+                        op0=ALU.mult, op1=ALU.add,
+                    )
+            nc.sync.dma_start(out=out[t0 : t0 + P * J, :].rearrange("(p j) o -> p j o", j=J), in_=o[:])
+
+        def permute_w1(T):
+            nc.vector.tensor_copy(
+                out=w1[T][:].bitcast(I32).rearrange("p g (t m) -> p g m t", t=4),
+                in_=w1raw[T][:].rearrange("p g (m t) -> p g m t", t=4),
+            )
+
+        def live(c):
+            return 0 <= c < NCH
+
+        nc.scalar.copy(out=xv[0][:, 0, 0:512], in_=xbytes[0][:, 0, 0:512].bitcast(FP8))
+        nc.vector.tensor_copy(out=xv[0][:, 0, 512:1024], in_=xbytes[0][:, 0, 512:1024].bitcast(FP8))
+        turn(0)
+        cast(1, 0)
+        nc.vector.tensor_copy(out=xv[1][:, 1, :], in_=xbytes[1][:, 1, :].bitcast(FP8))
+
+        for s in range(NCH + 2):
+            a, b, c = s, s - 1, s - 2
+            if live(a):
+                scale_x(a, 0)
+                scale_x(a, 1)
+            if s == 0:
+                nc.vector.tensor_copy(
+                    out=s1[:].rearrange("p (a t m) -> p a t m", a=2, t=4),
+                    in_=s1raw[:].rearrange("p (a m t) -> p a t m", a=2, t=4),
+                )
+                permute_w1(0)
+            if live(b):
+                stage1(b, 0)
+                exit_h(b, 0)
+            if live(c):
+                stage2(c)
+            if live(a):
+                quant_x(a)
+            if live(b):
+                weave_h(b, 0)
+                stage1(b, 1)
+                exit_h(b, 1)
+            if live(c):
+                for j in range(CHUNKS[c][1]):
+                    bias_v(c, j)
+                    square_v(c, j)
+            if s == 0:
+                permute_w1(1)
+            if live(a + 2):
+                for j in range(CHUNKS[a + 2][1]):
+                    cast(a + 2, j)
+            if live(a + 1):
+                turn(a + 1)
+            if live(b):
+                weave_h(b, 1)
+                quant_h(b, 0)
+                quant_h(b, 1)
+            if live(c):
+                finish_v(c)

@@ -19,8 +19,8 @@ P = 128
 K = 1024
 NOUT = 512
 CHUNKS = ((0, 1), (128, 2), (384, 2), (640, 2), (896, 1))
-S_WEAVE = ((0,0),(0,0),(0,0),(0,0),(0,0))
-FIN = ("G", "GG", "GG", "GG", "V")
+WEAVE = "VVVVVVVVVV"
+EPS2 = 1e-24
 NCH = len(CHUNKS)
 
 
@@ -31,7 +31,7 @@ def tile_geometricmanifoldnetwork_pa_w8_kernel(
     with ExitStack() as ctx:
         keep = ctx.enter_context(tc.tile_pool(name="keep", bufs=1))
         work = ctx.enter_context(tc.tile_pool(name="work", bufs=3))
-        psx = ctx.enter_context(tc.psum_pool(name="psx", bufs=1))
+        psx = ctx.enter_context(tc.psum_pool(name="psx", bufs=2))
         psh = ctx.enter_context(tc.psum_pool(name="psh", bufs=4))
         psy = ctx.enter_context(tc.psum_pool(name="psy", bufs=2))
         ctx.enter_context(tc.manual_schedule())
@@ -39,12 +39,17 @@ def tile_geometricmanifoldnetwork_pa_w8_kernel(
         s1raw = keep.tile([P, K], U8, name="s1raw", align_bytes=64)
         s1 = keep.tile([P, K], U8, name="s1", align_bytes=64)
         s2 = keep.tile([P, NOUT], U8, name="s2", align_bytes=64)
+        xsc = keep.tile([P, 2, 2, 2], F32, name="xsc")
+        nc.scalar.dma_start(
+            out=xsc[:].rearrange("p g u e -> p g (u e)"),
+            in_=x_scale.rearrange("o (g p t) -> p (o g) t", g=2, t=4),
+        )
         nc.vector.memset(s1raw[:].bitcast(I32), 0)
         nc.vector.memset(s2[:].bitcast(I32), 0)
-        half = keep.tile([P, 2], F32, name="half")
-        nc.vector.memset(half[:], -0.5)
-        warm = keep.tile([P, 2], BF16, name="warm")
-        nc.scalar.activation(out=warm[:], in_=half[:], func=ACT.Relu)
+        one = keep.tile([P, 2], F32, name="one")
+        nc.vector.memset(one[:], 1.0)
+        warm = keep.tile([P, 2], F32, name="warm")
+        nc.scalar.activation(out=warm[:], in_=one[:], func=ACT.Abs_reciprocal_sqrt)
         ident = keep.tile([P, P], F32, name="ident", align_bytes=64)
         make_identity(nc, ident[:])
 
@@ -59,14 +64,9 @@ def tile_geometricmanifoldnetwork_pa_w8_kernel(
         w1raw = [keep.tile([P, 2, 512], I32, name="w1raw%d" % t, align_bytes=64) for t in range(2)]
         w1 = [keep.tile([P, 2, 512], U32, name="w1_%d" % t, align_bytes=64) for t in range(2)]
         w2 = keep.tile([P, 2, 512], U32, name="w2", align_bytes=64)
-
-        xsc = keep.tile([P, 2, 2, 2], F32, name="xsc")
-        nc.scalar.dma_start(
-            out=xsc[:].rearrange("p g u e -> p g (u e)"),
-            in_=x_scale.rearrange("o (g p t) -> p (o g) t", g=2, t=4),
-        )
         b1t = keep.tile([P, 2, 4], BF16, name="b1t")
-        nc.scalar.dma_start(out=b1t[:], in_=b1.rearrange("(g p t) -> p g t", g=2, t=4))
+        b2t = keep.tile([P, NOUT], BF16, name="b2t")
+        w1i = W1_words.rearrange("g p n t -> p g (n t)").bitcast(I32)
 
         load_x(0)
         load_x(1)
@@ -75,20 +75,19 @@ def tile_geometricmanifoldnetwork_pa_w8_kernel(
                 out=s1raw[32 * q : 32 * q + 8, :].bitcast(I32),
                 in_=W1_scales[:, 4 * q : 4 * q + 4, :].bitcast(I32),
             )
-        w1i = W1_words.rearrange("g p n t -> p g (n t)").bitcast(I32)
-        for t in range(2):
-            nc.sync.dma_start(out=w1raw[t][:], in_=w1i[:, :, 512 * t : 512 * t + 512])
         load_x(2)
+        nc.sync.dma_start(out=w1raw[0][:], in_=w1i[:, :, 0:512])
+        nc.sync.dma_start(out=b1t[:], in_=b1.rearrange("(g p t) -> p g t", g=2, t=4))
+        nc.sync.dma_start(out=w1raw[1][:], in_=w1i[:, :, 512:1024])
+        load_x(3)
+        load_x(4)
         nc.sync.dma_start(out=w2[:].bitcast(I32), in_=W2_words.rearrange("g p n t -> p g (n t)").bitcast(I32))
+        nc.sync.dma_start(out=b2t[:], in_=b2.partition_broadcast(P))
         for q in range(4):
             nc.sync.dma_start(
                 out=s2[32 * q : 32 * q + 8, :].bitcast(I32),
                 in_=W2_scales[:, 4 * q : 4 * q + 4, :].bitcast(I32),
             )
-        load_x(3)
-        load_x(4)
-        b2t = keep.tile([P, NOUT], BF16, name="b2t")
-        nc.sync.dma_start(out=b2t[:], in_=b2.partition_broadcast(P))
 
         xv = [keep.tile([P, J, K], BF16, name="xv%d" % c, align_bytes=64) for c, (t0, J) in enumerate(CHUNKS)]
         xt = {}
@@ -103,43 +102,48 @@ def tile_geometricmanifoldnetwork_pa_w8_kernel(
         py = {}
         v = {}
         ssq = {}
+        pw = {}
+        over = {}
+        r = {}
 
-        def cast(c, j):
-            nc.scalar.copy(out=xv[c][:, j, :], in_=xbytes[c][:, j, :].bitcast(FP8))
+        def cast(c, j, on_vector=False):
+            copy = nc.vector.tensor_copy if on_vector else nc.scalar.copy
+            copy(out=xv[c][:, j, :], in_=xbytes[c][:, j, :].bitcast(FP8))
 
-        def turn(c):
+        def turn(c, g):
             J = CHUNKS[c][1]
-            for g in range(2):
-                xt[c, g] = psx.tile([P, 2, P * J], F32, name="xt%d" % g)
+            if J == 2:
+                xt[c, g] = psx.tile([P, 2, 2 * P], F32, name="xt")[:]
+            elif g == 0:
+                both = (psy if c == 0 else psx).tile([P, 2, 2, P], F32, name="py" if c == 0 else "xt")
+                xt[c, 0], xt[c, 1] = both[:, 0, :, :], both[:, 1, :, :]
             words = xv[c][:].bitcast(F32)
             for j in range(J):
-                for g in range(2):
-                    for u in range(2):
-                        nc.tensor.transpose(
-                            xt[c, g][:, u, P * j : P * j + P],
-                            words[:, j, 256 * g + u : 256 * (g + 1) : 2],
-                            ident[:],
-                        )
+                for u in range(2):
+                    nc.tensor.transpose(
+                        xt[c, g][:, u, P * j : P * j + P],
+                        words[:, j, 256 * g + u : 256 * (g + 1) : 2],
+                        ident[:],
+                    )
 
         def scale_x(c, g):
             n = P * CHUNKS[c][1]
-            if g == 0:
-                grp[c] = work.tile([P, 2, n, 4], BF16, name="grp", align_bytes=64)
+            grp[c, g] = work.tile([P, n, 4], BF16, name="grp", align_bytes=64)
             nc.vector.tensor_tensor(
-                out=grp[c][:, g, :, :].rearrange("p n (u e) -> p n u e", e=2),
-                in0=xt[c, g][:].bitcast(BF16).rearrange("p u (n e) -> p n u e", e=2),
+                out=grp[c, g][:].rearrange("p n (u e) -> p n u e", e=2),
+                in0=xt[c, g].bitcast(BF16).rearrange("p u (n e) -> p n u e", e=2),
                 in1=xsc[:, g, :, :].unsqueeze(1).to_broadcast([P, n, 2, 2]),
                 op=ALU.mult,
             )
 
-        def quant_x(c):
+        def quant_x(c, g):
             n = P * CHUNKS[c][1]
-            xq[c] = work.tile([P, 2, n], U32, name="xq", align_bytes=64)
-            xs[c] = work.tile([P, 2, n], U8, name="xs", align_bytes=64)
+            xq[c, g] = work.tile([P, n], U32, name="xq", align_bytes=64, bufs=6)
+            xs[c, g] = work.tile([P, n], U8, name="xs", align_bytes=64, bufs=6)
             nc.vector.quantize_mx(
-                out=xq[c][:].rearrange("p g n -> p (g n)").bitcast(FP8X4),
-                scales=xs[c][:].rearrange("p g n -> p (g n)"),
-                in_=grp[c][:].rearrange("p g n t -> p (g n t)"),
+                out=xq[c, g][:].bitcast(FP8X4),
+                scales=xs[c, g][:],
+                in_=grp[c, g][:].rearrange("p n t -> p (n t)"),
             )
 
         def stage1(c, T):
@@ -153,18 +157,24 @@ def tile_geometricmanifoldnetwork_pa_w8_kernel(
                         out=ph[c, T, t // 2][:, t % 2, :],
                         lhsT=w1[T][:, g, cols].bitcast(FP8X4),
                         lhsT_scale=s1[4 * g :, 512 * T + 128 * t : 512 * T + 128 * t + 128],
-                        rhs=xq[c][:, g, :].bitcast(FP8X4),
-                        rhs_scale=xs[c][:, g, :],
+                        rhs=xq[c, g][:].bitcast(FP8X4),
+                        rhs_scale=xs[c, g][:],
                         start=(g == 0),
                         stop=(g == 1),
                     )
 
-        def exit_h(c, T):
+        def exit_h(c, T, ts):
             n = P * CHUNKS[c][1]
-            hp[c, T] = work.tile([P, 4, n], BF16, name="hp", align_bytes=64)
-            for t in range(4):
+            pairs = WEAVE[2 * c + T] == "B"
+            if ts[0] == 0:
+                hp[c, T] = work.tile([P, 4, n], BF16, name="hp", align_bytes=64, bufs=5)
+            for t in ts:
+                if pairs:
+                    plane = hp[c, T][:].rearrange("p (u a) n -> p u (a n)", u=2)[:, t // 2, t % 2 : 2 * n : 2]
+                else:
+                    plane = hp[c, T][:, t, :]
                 nc.scalar.activation(
-                    out=hp[c, T][:, t, :],
+                    out=plane,
                     in_=ph[c, T, t // 2][:, t % 2, :],
                     func=ACT.Relu,
                     bias=b1t[:, T, t : t + 1],
@@ -172,14 +182,17 @@ def tile_geometricmanifoldnetwork_pa_w8_kernel(
 
         def weave_h(c, T):
             n = P * CHUNKS[c][1]
-            hg[c, T] = work.tile([P, n, 4], BF16, name="hg", align_bytes=64)
-            cut = n - S_WEAVE[c][T]
-            for copy, cols in ((nc.vector.tensor_copy, slice(0, cut)), (nc.scalar.copy, slice(cut, n))):
-                if cols.start < cols.stop:
-                    copy(
-                        out=hg[c, T][:, cols, :].rearrange("p (c i) t -> p c t i", i=4),
-                        in_=hp[c, T][:, :, cols].rearrange("p t (c i) -> p c t i", i=4),
-                    )
+            walk_out, walk_in = "p (c i) t -> p c t i", "p t (c i) -> p c t i"
+            hg[c, T] = work.tile([P, n, 4], BF16, name="hg", align_bytes=64, bufs=4)
+            how = WEAVE[2 * c + T]
+            if how == "B":
+                nc.vector.tensor_copy(
+                    out=hg[c, T][:].rearrange("p n t -> p (n t)").bitcast(F32).rearrange("p (c i u) -> p c u i", i=4, u=2),
+                    in_=hp[c, T][:].rearrange("p t n -> p (t n)").bitcast(F32).rearrange("p (u c i) -> p c u i", i=4, u=2),
+                )
+            else:
+                copy = nc.vector.tensor_copy if how == "V" else nc.scalar.copy
+                copy(out=hg[c, T][:].rearrange(walk_out, i=4), in_=hp[c, T][:].rearrange(walk_in, i=4))
 
         def quant_h(c, T):
             n = P * CHUNKS[c][1]
@@ -192,105 +205,176 @@ def tile_geometricmanifoldnetwork_pa_w8_kernel(
                 in_=hg[c, T][:].rearrange("p n t -> p (n t)"),
             )
 
-        def stage2(c):
-            for j in range(CHUNKS[c][1]):
-                py[c, j] = psy.tile([P, NOUT], F32, name="py")
-                for T in range(2):
-                    nc.tensor.matmul_mx(
-                        out=py[c, j][:],
-                        lhsT=hq[c][:, T, P * j : P * j + P].bitcast(FP8X4),
-                        lhsT_scale=hs[c][:, T, P * j : P * j + P],
-                        rhs=w2[:, T, :].bitcast(FP8X4),
-                        rhs_scale=s2[4 * T :, :],
-                        start=(T == 0),
-                        stop=(T == 1),
-                    )
+        def stage2(c, j):
+            late = TILES.index((c, j)) in (5, 6)
+            py[c, j] = psx.tile([P, NOUT], F32, name="xt") if late else psy.tile([P, NOUT], F32, name="py")
+            for T in range(2):
+                nc.tensor.matmul_mx(
+                    out=py[c, j][:],
+                    lhsT=hq[c][:, T, P * j : P * j + P].bitcast(FP8X4),
+                    lhsT_scale=hs[c][:, T, P * j : P * j + P],
+                    rhs=w2[:, T, :].bitcast(FP8X4),
+                    rhs_scale=s2[4 * T :, :],
+                    start=(T == 0),
+                    stop=(T == 1),
+                )
 
         def bias_v(c, j):
-            J = CHUNKS[c][1]
-            if j == 0:
-                v[c] = work.tile([P, J, NOUT], F32, name="v", align_bytes=64)
-                ssq[c] = work.tile([P, 2], F32, name="ssq")
-            nc.vector.tensor_tensor(out=v[c][:, j, :], in0=py[c, j][:], in1=b2t[:], op=ALU.add)
+            v[c, j] = work.tile([P, NOUT], F32, name="v", align_bytes=64, bufs=8)
+            nc.vector.tensor_tensor(out=v[c, j][:], in0=py[c, j][:], in1=b2t[:], op=ALU.add)
 
         def square_v(c, j):
             junk = work.tile([P, NOUT], BF16, name="junk", align_bytes=64)
-            nc.scalar.activation(out=junk[:], in_=v[c][:, j, :], func=ACT.Square, accum_out=ssq[c][:, j : j + 1])
+            ssq[c, j] = work.tile([P, 1], F32, name="ssq")
+            nc.scalar.activation(out=junk[:], in_=v[c, j][:], func=ACT.Square, accum_out=ssq[c, j][:])
 
-        def finish_v(c):
+        def clamp_v(c, j):
+            over[c, j] = work.tile([P, 1], F32, name="over")
+            nc.scalar.activation(out=over[c, j][:], in_=ssq[c, j][:], func=ACT.Relu, bias=-EPS2)
+
+        def root_v(c, j):
+            r[c, j] = work.tile([P, 1], F32, name="r")
+            nc.scalar.activation(out=r[c, j][:], in_=over[c, j][:], func=ACT.Abs_reciprocal_sqrt, bias=EPS2)
+
+        def finish_v(c, j, on_vector):
             t0, J = CHUNKS[c]
-            clamped = work.tile([P, 2], F32, name="clamped")
-            r = work.tile([P, 2], F32, name="r")
-            o = work.tile([P, J, NOUT], F32, name="o", align_bytes=64)
-            nc.gpsimd.tensor_scalar(
-                out=clamped[:, 0:J], in0=ssq[c][:, 0:J], scalar1=1e-24, scalar2=None, op0=ALU.max
-            )
-            nc.gpsimd.tensor_tensor(out=r[:, 0:J], in0=clamped[:, 0:J], in1=half[:, 0:J], op=ALU.pow)
-            for j in range(J):
-                if FIN[c][j] == "S":
-                    nc.scalar.activation(out=o[:, j, :], in_=v[c][:, j, :], func=ACT.Copy, scale=r[:, j : j + 1])
-                elif FIN[c][j] == "V":
-                    nc.vector.tensor_scalar(
-                        out=o[:, j, :], in0=v[c][:, j, :], scalar1=r[:, j : j + 1], scalar2=None, op0=ALU.mult
-                    )
-                else:
-                    nc.gpsimd.tensor_scalar(
-                        out=o[:, j, :], in0=v[c][:, j, :], scalar1=r[:, j : j + 1], scalar2=0.0,
-                        op0=ALU.mult, op1=ALU.add,
-                    )
-            nc.sync.dma_start(out=out[t0 : t0 + P * J, :].rearrange("(p j) o -> p j o", j=J), in_=o[:])
+            o = work.tile([P, NOUT], F32, name="o", align_bytes=64, bufs=8)
+            if on_vector:
+                nc.vector.tensor_scalar(
+                    out=o[:], in0=v[c, j][:], scalar1=r[c, j][:], scalar2=None, op0=ALU.mult
+                )
+            else:
+                nc.scalar.activation(out=o[:], in_=v[c, j][:], func=ACT.Copy, scale=r[c, j][:])
+            nc.sync.dma_start(out=out[t0 : t0 + P * J, :].rearrange("(p j) o -> p j o", j=J)[:, j, :], in_=o[:])
 
         def permute_w1(T):
             nc.vector.tensor_copy(
-                out=w1[T][:].bitcast(I32).rearrange("p g (t m) -> p g m t", t=4),
-                in_=w1raw[T][:].rearrange("p g (m t) -> p g m t", t=4),
+                out=w1[T][:].bitcast(I32).rearrange("p g (t m) -> p g t m", t=4),
+                in_=w1raw[T][:].rearrange("p g (m t) -> p g t m", t=4),
+            )
+
+        def permute_s1(T):
+            cols = slice(512 * T, 512 * T + 512)
+            nc.vector.tensor_copy(
+                out=s1[:, cols].rearrange("p (t m) -> p t m", t=4),
+                in_=s1raw[:, cols].rearrange("p (m t) -> p t m", t=4),
             )
 
         def live(c):
             return 0 <= c < NCH
 
-        nc.scalar.copy(out=xv[0][:, 0, 0:512], in_=xbytes[0][:, 0, 0:512].bitcast(FP8))
-        nc.vector.tensor_copy(out=xv[0][:, 0, 512:1024], in_=xbytes[0][:, 0, 512:1024].bitcast(FP8))
-        turn(0)
+        def tiles(c):
+            return range(CHUNKS[c][1]) if live(c) else range(0)
+
+        TILES = [(c, j) for c in range(NCH) for j in range(CHUNKS[c][1])]
+
+        UNITS = [[(0, 0), (0, 1)]] + [[(c, T)] for c in range(1, NCH - 1) for T in range(2)] + [[(NCH - 1, 0), (NCH - 1, 1)]]
+
+        def units(f, i, *more):
+            if 0 <= i < len(UNITS):
+                for cT in UNITS[i]:
+                    f(*cT, *more)
+
+        def tile(f, i, *more):
+            if 0 <= i < len(TILES):
+                f(*TILES[i], *more)
+
+        nc.scalar.copy(out=xv[0][:, 0, 0:384], in_=xbytes[0][:, 0, 0:384].bitcast(FP8))
+        nc.vector.tensor_copy(out=xv[0][:, 0, 384:1024], in_=xbytes[0][:, 0, 384:1024].bitcast(FP8))
+        turn(0, 0)
+        turn(0, 1)
         cast(1, 0)
         nc.vector.tensor_copy(out=xv[1][:, 1, :], in_=xbytes[1][:, 1, :].bitcast(FP8))
+        turn(1, 0)
+        turn(1, 1)
+        cast(2, 0)
+        cast(2, 1)
+        permute_s1(0)
+        permute_s1(1)
+        scale_x(0, 0)
+        scale_x(0, 1)
+        quant_x(0, 0)
+        permute_w1(0)
+        quant_x(0, 1)
+        stage1(0, 0)
+        scale_x(1, 0)
+        permute_w1(1)
+        stage1(0, 1)
+        turn(2, 0)
+        scale_x(1, 1)
+        quant_x(1, 0)
+        tile(cast, 5)
 
-        for s in range(NCH + 2):
-            a, b, c = s, s - 1, s - 2
-            if live(a):
-                scale_x(a, 0)
-                scale_x(a, 1)
-            if s == 0:
-                nc.vector.tensor_copy(
-                    out=s1[:].rearrange("p (a t m) -> p a t m", a=2, t=4),
-                    in_=s1raw[:].rearrange("p (a m t) -> p a t m", a=2, t=4),
-                )
-                permute_w1(0)
-            if live(b):
-                stage1(b, 0)
-                exit_h(b, 0)
-            if live(c):
-                stage2(c)
-            if live(a):
-                quant_x(a)
-            if live(b):
-                weave_h(b, 0)
-                stage1(b, 1)
-                exit_h(b, 1)
-            if live(c):
-                for j in range(CHUNKS[c][1]):
-                    bias_v(c, j)
-                    square_v(c, j)
-            if s == 0:
-                permute_w1(1)
-            if live(a + 2):
-                for j in range(CHUNKS[a + 2][1]):
-                    cast(a + 2, j)
-            if live(a + 1):
-                turn(a + 1)
-            if live(b):
-                weave_h(b, 1)
-                quant_h(b, 0)
-                quant_h(b, 1)
-            if live(c):
-                finish_v(c)
+        def relu(c, T):
+            exit_h(c, T, (0, 1, 2, 3))
+
+        for i in range(4):
+            units(turn, i + 4)
+            units(relu, i)
+            tile(square_v, i - 3)
+            tile(cast, i + 6)
+            units(weave_h, i - 1)
+            units(quant_x, i + 2)
+            if i % 2 == 1:
+                units(stage1, i + 1)
+            units(quant_h, i - 1)
+            tile(stage2, i - 2)
+            if i % 2 == 0:
+                units(stage1, i + 1)
+            units(scale_x, i + 3)
+            tile(bias_v, i - 2)
+        tile(clamp_v, 0)
+        units(relu, 4)
+        tile(root_v, 0)
+        units(quant_x, 6)
+        tile(stage2, 2)
+        units(stage1, 5)
+        units(scale_x, 7)
+        tile(square_v, 1)
+        tile(finish_v, 0, False)
+        tile(clamp_v, 1)
+        units(weave_h, 3)
+        units(quant_x, 7)
+        units(quant_h, 3)
+        units(relu, 5)
+        tile(root_v, 1)
+        units(stage1, 6)
+        units(relu, 6)
+        units(stage1, 7)
+        tile(finish_v, 1, False)
+        relu(4, 0)
+        units(weave_h, 4)
+        tile(bias_v, 2)
+        units(quant_h, 4)
+        tile(stage2, 3)
+        tile(stage2, 4)
+        relu(4, 1)
+        units(weave_h, 5)
+        units(weave_h, 6)
+        units(quant_h, 5)
+        tile(bias_v, 3)
+        units(quant_h, 6)
+        tile(stage2, 5)
+        tile(stage2, 6)
+        tile(bias_v, 4)
+        units(weave_h, 7)
+        tile(bias_v, 5)
+        units(quant_h, 7)
+        tile(stage2, 7)
+        tile(bias_v, 6)
+        tile(square_v, 2)
+        tile(square_v, 3)
+        tile(clamp_v, 2)
+        tile(square_v, 4)
+        tile(root_v, 2)
+        tile(clamp_v, 3)
+        tile(finish_v, 2, False)
+        tile(root_v, 3)
+        tile(clamp_v, 4)
+        tile(finish_v, 3, True)
+        tile(bias_v, 7)
+        for i in range(5, 9):
+            tile(square_v, i)
+            tile(root_v, i - 1)
+            tile(clamp_v, i)
+            tile(finish_v, i - 1, True)

@@ -19,9 +19,11 @@ P = 128
 K = 1024
 NOUT = 512
 CHUNKS = ((0, 1), (128, 2), (384, 2), (640, 2), (896, 1))
-WEAVE = "VVVVVVVVVV"
-EPS2 = 1e-24
 NCH = len(CHUNKS)
+TILES = [(c, j) for c in range(NCH) for j in range(CHUNKS[c][1])]
+UNITS = [(0, (0, 1))] + [(c, (h,)) for c in range(1, NCH - 1) for h in range(2)] + [(NCH - 1, (0, 1))]
+PAIRS = (0, 1)
+EPS2 = 1e-24
 
 
 def tile_geometricmanifoldnetwork_pa_w8_kernel(
@@ -39,11 +41,8 @@ def tile_geometricmanifoldnetwork_pa_w8_kernel(
         s1raw = keep.tile([P, K], U8, name="s1raw", align_bytes=64)
         s1 = keep.tile([P, K], U8, name="s1", align_bytes=64)
         s2 = keep.tile([P, NOUT], U8, name="s2", align_bytes=64)
-        xsc = keep.tile([P, 2, 2, 2], F32, name="xsc")
-        nc.scalar.dma_start(
-            out=xsc[:].rearrange("p g u e -> p g (u e)"),
-            in_=x_scale.rearrange("o (g p t) -> p (o g) t", g=2, t=4),
-        )
+        xsc = keep.tile([P, 2, 4], F32, name="xsc")
+        nc.scalar.dma_start(out=xsc[:], in_=x_scale.rearrange("o (g p t) -> p (o g) t", g=2, t=4))
         nc.vector.memset(s1raw[:].bitcast(I32), 0)
         nc.vector.memset(s2[:].bitcast(I32), 0)
         one = keep.tile([P, 2], F32, name="one")
@@ -53,102 +52,86 @@ def tile_geometricmanifoldnetwork_pa_w8_kernel(
         ident = keep.tile([P, P], F32, name="ident", align_bytes=64)
         make_identity(nc, ident[:])
 
-        xbytes = []
-        for c, (t0, J) in enumerate(CHUNKS):
-            xbytes.append(keep.tile([P, J, K], U8, name="xbytes%d" % c, align_bytes=64))
-
-        def load_x(c):
-            t0, J = CHUNKS[c]
-            nc.sync.dma_start(out=xbytes[c][:], in_=x_bytes[t0 : t0 + P * J, :].rearrange("(p j) k -> p j k", j=J))
-
-        w1raw = [keep.tile([P, 2, 512], I32, name="w1raw%d" % t, align_bytes=64) for t in range(2)]
-        w1 = [keep.tile([P, 2, 512], U32, name="w1_%d" % t, align_bytes=64) for t in range(2)]
+        xbytes = [keep.tile([P, J, K], U8, name="xbytes%d" % c, align_bytes=64) for c, (t0, J) in enumerate(CHUNKS)]
+        w1raw = [keep.tile([P, 2, 512], I32, name="w1raw%d" % T, align_bytes=64) for T in range(2)]
+        w1 = [keep.tile([P, 2, 512], U32, name="w1_%d" % T, align_bytes=64) for T in range(2)]
         w2 = keep.tile([P, 2, 512], U32, name="w2", align_bytes=64)
         b1t = keep.tile([P, 2, 4], BF16, name="b1t")
         b2t = keep.tile([P, NOUT], BF16, name="b2t")
         w1i = W1_words.rearrange("g p n t -> p g (n t)").bitcast(I32)
 
+        def load_x(c):
+            t0, J = CHUNKS[c]
+            nc.sync.dma_start(out=xbytes[c][:], in_=x_bytes[t0 : t0 + P * J, :].rearrange("(p j) k -> p j k", j=J))
+
+        def load_w1(T):
+            nc.sync.dma_start(out=w1raw[T][:], in_=w1i[:, :, 512 * T : 512 * T + 512])
+
+        def load_scales(dst, src):
+            for q in range(4):
+                nc.sync.dma_start(out=dst[32 * q : 32 * q + 8, :].bitcast(I32), in_=src[:, 4 * q : 4 * q + 4, :].bitcast(I32))
+
         load_x(0)
         load_x(1)
-        for q in range(4):
-            nc.sync.dma_start(
-                out=s1raw[32 * q : 32 * q + 8, :].bitcast(I32),
-                in_=W1_scales[:, 4 * q : 4 * q + 4, :].bitcast(I32),
-            )
+        load_scales(s1raw, W1_scales)
         load_x(2)
-        nc.sync.dma_start(out=w1raw[0][:], in_=w1i[:, :, 0:512])
-        nc.sync.dma_start(out=b1t[:], in_=b1.rearrange("(g p t) -> p g t", g=2, t=4))
-        nc.sync.dma_start(out=w1raw[1][:], in_=w1i[:, :, 512:1024])
+        load_w1(0)
         load_x(3)
+        nc.sync.dma_start(out=b1t[:], in_=b1.rearrange("(g p t) -> p g t", g=2, t=4))
+        load_w1(1)
         load_x(4)
         nc.sync.dma_start(out=w2[:].bitcast(I32), in_=W2_words.rearrange("g p n t -> p g (n t)").bitcast(I32))
         nc.sync.dma_start(out=b2t[:], in_=b2.partition_broadcast(P))
-        for q in range(4):
-            nc.sync.dma_start(
-                out=s2[32 * q : 32 * q + 8, :].bitcast(I32),
-                in_=W2_scales[:, 4 * q : 4 * q + 4, :].bitcast(I32),
-            )
+        load_scales(s2, W2_scales)
 
-        xv = [keep.tile([P, J, K], BF16, name="xv%d" % c, align_bytes=64) for c, (t0, J) in enumerate(CHUNKS)]
-        xt = {}
-        grp = {}
-        xq = {}
-        xs = {}
-        ph = {}
-        hp = {}
-        hg = {}
-        hq = {}
-        hs = {}
-        py = {}
-        v = {}
-        ssq = {}
-        pw = {}
-        over = {}
-        r = {}
+        xv, xt, grp, xq, xs, ph, hp, hg, hq, hs, py, v, ssq, over, r = ({} for i in range(15))
 
-        def cast(c, j, on_vector=False):
+        def cast(c, j, on_vector=False, cols=slice(0, K)):
+            if (c, j) not in xv:
+                xv[c, j] = keep.tile([P, K], BF16, name="xv%d_%d" % (c, j), align_bytes=64)
             copy = nc.vector.tensor_copy if on_vector else nc.scalar.copy
-            copy(out=xv[c][:, j, :], in_=xbytes[c][:, j, :].bitcast(FP8))
+            copy(out=xv[c, j][:, cols], in_=xbytes[c][:, j, cols].bitcast(FP8))
 
-        def turn(c, g):
+        def turn(c, gs):
             J = CHUNKS[c][1]
-            if J == 2:
-                xt[c, g] = psx.tile([P, 2, 2 * P], F32, name="xt")[:]
-            elif g == 0:
-                both = (psy if c == 0 else psx).tile([P, 2, 2, P], F32, name="py" if c == 0 else "xt")
-                xt[c, 0], xt[c, 1] = both[:, 0, :, :], both[:, 1, :, :]
-            words = xv[c][:].bitcast(F32)
-            for j in range(J):
-                for u in range(2):
-                    nc.tensor.transpose(
-                        xt[c, g][:, u, P * j : P * j + P],
-                        words[:, j, 256 * g + u : 256 * (g + 1) : 2],
-                        ident[:],
-                    )
+            pool, tag = (psy, "py") if c == 0 else (psx, "xt")
+            bank = pool.tile([P, 2, len(gs), P * J], F32, name=tag)
+            xt[c, gs] = bank
+            for a, g in enumerate(gs):
+                for j in range(J):
+                    words = xv[c, j][:].bitcast(F32)
+                    for u in range(2):
+                        nc.tensor.transpose(
+                            bank[:, u, a, P * j : P * j + P], words[:, 256 * g + u : 256 * (g + 1) : 2], ident[:]
+                        )
 
-        def scale_x(c, g):
+        def scale_x(c, gs):
             n = P * CHUNKS[c][1]
-            grp[c, g] = work.tile([P, n, 4], BF16, name="grp", align_bytes=64)
-            nc.vector.tensor_tensor(
-                out=grp[c, g][:].rearrange("p n (u e) -> p n u e", e=2),
-                in0=xt[c, g].bitcast(BF16).rearrange("p u (n e) -> p n u e", e=2),
-                in1=xsc[:, g, :, :].unsqueeze(1).to_broadcast([P, n, 2, 2]),
-                op=ALU.mult,
-            )
+            if gs[0] == 0:
+                grp[c] = work.tile([P, 2, n, 4], BF16, name="grp", align_bytes=64)
+            for a, g in enumerate(gs):
+                nc.vector.tensor_tensor(
+                    out=grp[c][:, g, :, :].rearrange("p n (u e) -> p n u e", e=2),
+                    in0=xt[c, gs][:, :, a, :].bitcast(BF16).rearrange("p u (n e) -> p n u e", e=2),
+                    in1=xsc[:, g, :].rearrange("p (u e) -> p u e", e=2).unsqueeze(1).to_broadcast([P, n, 2, 2]),
+                    op=ALU.mult,
+                )
 
-        def quant_x(c, g):
+        def quant_x(c, gs):
             n = P * CHUNKS[c][1]
-            xq[c, g] = work.tile([P, n], U32, name="xq", align_bytes=64, bufs=6)
-            xs[c, g] = work.tile([P, n], U8, name="xs", align_bytes=64, bufs=6)
+            if gs[0] == 0:
+                xq[c] = work.tile([P, 2, n], U32, name="xq", align_bytes=64)
+                xs[c] = work.tile([P, 2, n], U8, name="xs", align_bytes=64)
+            part = slice(gs[0], gs[-1] + 1)
             nc.vector.quantize_mx(
-                out=xq[c, g][:].bitcast(FP8X4),
-                scales=xs[c, g][:],
-                in_=grp[c, g][:].rearrange("p n t -> p (n t)"),
+                out=xq[c][:, part, :].rearrange("p g n -> p (g n)").bitcast(FP8X4),
+                scales=xs[c][:, part, :].rearrange("p g n -> p (g n)"),
+                in_=grp[c][:, part, :, :].rearrange("p g n t -> p (g n t)"),
             )
 
-        def stage1(c, T):
+        def stage1(c, Ts):
             n = P * CHUNKS[c][1]
-            for t in range(4):
+            for T, t in [(T, t) for T in Ts for t in range(4)]:
                 if t % 2 == 0:
                     ph[c, T, t // 2] = psh.tile([P, 2, n], F32, name="ph")
                 cols = slice(128 * t, 128 * t + 128)
@@ -157,52 +140,51 @@ def tile_geometricmanifoldnetwork_pa_w8_kernel(
                         out=ph[c, T, t // 2][:, t % 2, :],
                         lhsT=w1[T][:, g, cols].bitcast(FP8X4),
                         lhsT_scale=s1[4 * g :, 512 * T + 128 * t : 512 * T + 128 * t + 128],
-                        rhs=xq[c, g][:].bitcast(FP8X4),
-                        rhs_scale=xs[c, g][:],
+                        rhs=xq[c][:, g, :].bitcast(FP8X4),
+                        rhs_scale=xs[c][:, g, :],
                         start=(g == 0),
                         stop=(g == 1),
                     )
 
-        def exit_h(c, T, ts):
+        def relu(c, Ts):
             n = P * CHUNKS[c][1]
-            pairs = WEAVE[2 * c + T] == "B"
-            if ts[0] == 0:
-                hp[c, T] = work.tile([P, 4, n], BF16, name="hp", align_bytes=64, bufs=5)
-            for t in ts:
-                if pairs:
-                    plane = hp[c, T][:].rearrange("p (u a) n -> p u (a n)", u=2)[:, t // 2, t % 2 : 2 * n : 2]
+            if Ts[0] == 0:
+                hp[c] = work.tile([P, 2, 4 * n], BF16, name="hp", align_bytes=64)
+            for T, t in [(T, t) for T in Ts for t in range(4)]:
+                if c in PAIRS:
+                    plane = hp[c][:, T, 2 * n * (t // 2) + t % 2 : 2 * n * (t // 2 + 1) : 2]
                 else:
-                    plane = hp[c, T][:, t, :]
+                    plane = hp[c][:, T, n * t : n * t + n]
                 nc.scalar.activation(
-                    out=plane,
-                    in_=ph[c, T, t // 2][:, t % 2, :],
-                    func=ACT.Relu,
-                    bias=b1t[:, T, t : t + 1],
+                    out=plane, in_=ph[c, T, t // 2][:, t % 2, :], func=ACT.Relu, bias=b1t[:, T, t : t + 1]
                 )
 
-        def weave_h(c, T):
+        def weave_h(c, Ts):
             n = P * CHUNKS[c][1]
-            walk_out, walk_in = "p (c i) t -> p c t i", "p t (c i) -> p c t i"
-            hg[c, T] = work.tile([P, n, 4], BF16, name="hg", align_bytes=64, bufs=4)
-            how = WEAVE[2 * c + T]
-            if how == "B":
+            if Ts[0] == 0:
+                hg[c] = work.tile([P, 2, 4 * n], BF16, name="hg", align_bytes=64)
+            part = slice(Ts[0], Ts[-1] + 1)
+            if c in PAIRS:
                 nc.vector.tensor_copy(
-                    out=hg[c, T][:].rearrange("p n t -> p (n t)").bitcast(F32).rearrange("p (c i u) -> p c u i", i=4, u=2),
-                    in_=hp[c, T][:].rearrange("p t n -> p (t n)").bitcast(F32).rearrange("p (u c i) -> p c u i", i=4, u=2),
+                    out=hg[c][:, part, :].bitcast(F32).rearrange("p T (c i u) -> p T c u i", i=4, u=2),
+                    in_=hp[c][:, part, :].bitcast(F32).rearrange("p T (u c i) -> p T c u i", i=4, u=2),
                 )
             else:
-                copy = nc.vector.tensor_copy if how == "V" else nc.scalar.copy
-                copy(out=hg[c, T][:].rearrange(walk_out, i=4), in_=hp[c, T][:].rearrange(walk_in, i=4))
+                nc.vector.tensor_copy(
+                    out=hg[c][:, part, :].rearrange("p T (c i t) -> p T c t i", i=4, t=4),
+                    in_=hp[c][:, part, :].rearrange("p T (t c i) -> p T c t i", i=4, t=4),
+                )
 
-        def quant_h(c, T):
+        def quant_h(c, Ts):
             n = P * CHUNKS[c][1]
-            if T == 0:
+            if Ts[0] == 0:
                 hq[c] = work.tile([P, 2, n], U32, name="hq", align_bytes=64)
                 hs[c] = work.tile([P, 2, n], U8, name="hs", align_bytes=64)
+            part = slice(Ts[0], Ts[-1] + 1)
             nc.vector.quantize_mx(
-                out=hq[c][:, T, :].bitcast(FP8X4),
-                scales=hs[c][:, T, :],
-                in_=hg[c, T][:].rearrange("p n t -> p (n t)"),
+                out=hq[c][:, part, :].rearrange("p T n -> p (T n)").bitcast(FP8X4),
+                scales=hs[c][:, part, :].rearrange("p T n -> p (T n)"),
+                in_=hg[c][:, part, :].rearrange("p T n -> p (T n)"),
             )
 
         def stage2(c, j):
@@ -240,79 +222,106 @@ def tile_geometricmanifoldnetwork_pa_w8_kernel(
             t0, J = CHUNKS[c]
             o = work.tile([P, NOUT], F32, name="o", align_bytes=64, bufs=8)
             if on_vector:
-                nc.vector.tensor_scalar(
-                    out=o[:], in0=v[c, j][:], scalar1=r[c, j][:], scalar2=None, op0=ALU.mult
-                )
+                nc.vector.tensor_scalar(out=o[:], in0=v[c, j][:], scalar1=r[c, j][:], scalar2=None, op0=ALU.mult)
             else:
                 nc.scalar.activation(out=o[:], in_=v[c, j][:], func=ACT.Copy, scale=r[c, j][:])
             nc.sync.dma_start(out=out[t0 : t0 + P * J, :].rearrange("(p j) o -> p j o", j=J)[:, j, :], in_=o[:])
 
+        def last_tile(stage):
+            c = NCH - 1
+            t0 = CHUNKS[c][0]
+            halves = (slice(0, 256), slice(256, NOUT))
+            if stage == 0:
+                for a, cols in enumerate(halves):
+                    py[c, a] = psy.tile([P, 256], F32, name="py")
+                    for T in range(2):
+                        nc.tensor.matmul_mx(
+                            out=py[c, a][:],
+                            lhsT=hq[c][:, T, :].bitcast(FP8X4),
+                            lhsT_scale=hs[c][:, T, :],
+                            rhs=w2[:, T, cols].bitcast(FP8X4),
+                            rhs_scale=s2[4 * T :, cols],
+                            start=(T == 0),
+                            stop=(T == 1),
+                        )
+            if stage == 1:
+                for a, cols in enumerate(halves):
+                    v[c, a] = work.tile([P, 256], F32, name="vhalf", align_bytes=64)
+                    ssq[c, a] = work.tile([P, 1], F32, name="ssqhalf")
+                    nc.vector.tensor_tensor(out=v[c, a][:], in0=py[c, a][:], in1=b2t[:, cols], op=ALU.add)
+            if stage == 2:
+                junk = work.tile([P, 256], BF16, name="junk_s", align_bytes=64)
+                nc.scalar.activation(out=junk[:], in_=v[c, 0][:], func=ACT.Square, accum_out=ssq[c, 0][:])
+            if stage == 3:
+                junk = work.tile([P, 256], BF16, name="junk_v", align_bytes=64)
+                nc.vector.scalar_tensor_tensor(
+                    out=junk[:], in0=v[c, 1][:], scalar=1.0, in1=v[c, 1][:], op0=ALU.mult, op1=ALU.mult,
+                    accum_out=ssq[c, 1][:],
+                )
+            if stage == 4:
+                over[c, 0] = work.tile([P, 1], F32, name="over")
+                nc.vector.tensor_scalar(
+                    out=over[c, 0][:], in0=ssq[c, 0][:], scalar1=ssq[c, 1][:], scalar2=EPS2, op0=ALU.add, op1=ALU.max
+                )
+            if stage == 5:
+                r[c, 0] = work.tile([P, 1], F32, name="r")
+                nc.scalar.activation(out=r[c, 0][:], in_=over[c, 0][:], func=ACT.Abs_reciprocal_sqrt)
+            if stage == 6:
+                o = work.tile([P, NOUT], F32, name="o", align_bytes=64, bufs=8)
+                for a, cols in enumerate(halves):
+                    nc.vector.tensor_scalar(out=o[:, cols], in0=v[c, a][:], scalar1=r[c, 0][:], scalar2=None, op0=ALU.mult)
+                    nc.sync.dma_start(out=out[t0 : t0 + P, cols], in_=o[:, cols])
+
         def permute_w1(T):
             nc.vector.tensor_copy(
-                out=w1[T][:].bitcast(I32).rearrange("p g (t m) -> p g t m", t=4),
-                in_=w1raw[T][:].rearrange("p g (m t) -> p g t m", t=4),
+                out=w1[T][:].bitcast(I32).rearrange("p g (t c i) -> p g c t i", t=4, i=4),
+                in_=w1raw[T][:].rearrange("p g (c i t) -> p g c t i", t=4, i=4),
             )
 
-        def permute_s1(T):
-            cols = slice(512 * T, 512 * T + 512)
+        def permute_s1():
             nc.vector.tensor_copy(
-                out=s1[:, cols].rearrange("p (t m) -> p t m", t=4),
-                in_=s1raw[:, cols].rearrange("p (m t) -> p t m", t=4),
+                out=s1[:].rearrange("p (T t c i) -> p T c t i", T=2, t=4, i=16),
+                in_=s1raw[:].rearrange("p (T c i t) -> p T c t i", T=2, t=4, i=16),
             )
-
-        def live(c):
-            return 0 <= c < NCH
-
-        def tiles(c):
-            return range(CHUNKS[c][1]) if live(c) else range(0)
-
-        TILES = [(c, j) for c in range(NCH) for j in range(CHUNKS[c][1])]
-
-        UNITS = [[(0, 0), (0, 1)]] + [[(c, T)] for c in range(1, NCH - 1) for T in range(2)] + [[(NCH - 1, 0), (NCH - 1, 1)]]
-
-        def units(f, i, *more):
-            if 0 <= i < len(UNITS):
-                for cT in UNITS[i]:
-                    f(*cT, *more)
 
         def tile(f, i, *more):
             if 0 <= i < len(TILES):
                 f(*TILES[i], *more)
 
-        nc.scalar.copy(out=xv[0][:, 0, 0:384], in_=xbytes[0][:, 0, 0:384].bitcast(FP8))
-        nc.vector.tensor_copy(out=xv[0][:, 0, 384:1024], in_=xbytes[0][:, 0, 384:1024].bitcast(FP8))
-        turn(0, 0)
-        turn(0, 1)
-        cast(1, 0)
-        nc.vector.tensor_copy(out=xv[1][:, 1, :], in_=xbytes[1][:, 1, :].bitcast(FP8))
-        turn(1, 0)
-        turn(1, 1)
-        cast(2, 0)
-        cast(2, 1)
-        permute_s1(0)
-        permute_s1(1)
-        scale_x(0, 0)
-        scale_x(0, 1)
-        quant_x(0, 0)
-        permute_w1(0)
-        quant_x(0, 1)
-        stage1(0, 0)
-        scale_x(1, 0)
-        permute_w1(1)
-        stage1(0, 1)
-        turn(2, 0)
-        scale_x(1, 1)
-        quant_x(1, 0)
-        tile(cast, 5)
+        def units(f, i):
+            if 0 <= i < len(UNITS):
+                f(*UNITS[i])
 
-        def relu(c, T):
-            exit_h(c, T, (0, 1, 2, 3))
+        cast(0, 0, True, slice(0, 512))
+        cast(0, 0, False, slice(512, K))
+        turn(0, (0,))
+        turn(0, (1,))
+        tile(cast, 1)
+        tile(cast, 2, True)
+        units(turn, 1)
+        units(turn, 2)
+        tile(cast, 3)
+        tile(cast, 4)
+        scale_x(0, (0,))
+        scale_x(0, (1,))
+        permute_s1()
+        units(quant_x, 0)
+        permute_w1(0)
+        stage1(0, (0,))
+        units(scale_x, 1)
+        permute_w1(1)
+        stage1(0, (1,))
+        units(turn, 3)
+        units(scale_x, 2)
+        units(quant_x, 1)
+        tile(cast, 5)
+        tile(cast, 6)
 
         for i in range(4):
             units(turn, i + 4)
             units(relu, i)
             tile(square_v, i - 3)
-            tile(cast, i + 6)
+            tile(cast, i + 7)
             units(weave_h, i - 1)
             units(quant_x, i + 2)
             if i % 2 == 1:
@@ -342,13 +351,13 @@ def tile_geometricmanifoldnetwork_pa_w8_kernel(
         units(relu, 6)
         units(stage1, 7)
         tile(finish_v, 1, False)
-        relu(4, 0)
+        relu(4, (0,))
         units(weave_h, 4)
         tile(bias_v, 2)
         units(quant_h, 4)
         tile(stage2, 3)
         tile(stage2, 4)
-        relu(4, 1)
+        relu(4, (1,))
         units(weave_h, 5)
         units(weave_h, 6)
         units(quant_h, 5)
@@ -360,7 +369,7 @@ def tile_geometricmanifoldnetwork_pa_w8_kernel(
         units(weave_h, 7)
         tile(bias_v, 5)
         units(quant_h, 7)
-        tile(stage2, 7)
+        last_tile(0)
         tile(bias_v, 6)
         tile(square_v, 2)
         tile(square_v, 3)
@@ -372,9 +381,19 @@ def tile_geometricmanifoldnetwork_pa_w8_kernel(
         tile(root_v, 3)
         tile(clamp_v, 4)
         tile(finish_v, 3, True)
-        tile(bias_v, 7)
-        for i in range(5, 9):
-            tile(square_v, i)
-            tile(root_v, i - 1)
-            tile(clamp_v, i)
-            tile(finish_v, i - 1, True)
+        last_tile(1)
+        tile(square_v, 5)
+        tile(root_v, 4)
+        tile(clamp_v, 5)
+        tile(finish_v, 4, True)
+        last_tile(3)
+        tile(square_v, 6)
+        tile(root_v, 5)
+        last_tile(2)
+        tile(clamp_v, 6)
+        tile(finish_v, 5, True)
+        last_tile(4)
+        tile(root_v, 6)
+        last_tile(5)
+        tile(finish_v, 6, True)
+        last_tile(6)

@@ -95,27 +95,27 @@ def tile_geometricmanifoldnetwork_pa_w8_kernel(
         def turn(c, gs):
             J = CHUNKS[c][1]
             pool, tag = (psy, "py") if c == 0 else (psx, "xt")
-            bank = pool.tile([P, 2, len(gs), P * J], F32, name=tag)
+            bank = pool.tile([P, len(gs), P * J, 2], F32, name=tag)
             xt[c, gs] = bank
             for a, g in enumerate(gs):
                 for j in range(J):
                     words = xv[c, j][:].bitcast(F32)
                     for u in range(2):
                         nc.tensor.transpose(
-                            bank[:, u, a, P * j : P * j + P], words[:, 256 * g + u : 256 * (g + 1) : 2], ident[:]
+                            bank[:, a, P * j : P * j + P, u], words[:, 256 * g + u : 256 * (g + 1) : 2], ident[:]
                         )
 
         def scale_x(c, gs):
             n = P * CHUNKS[c][1]
             if gs[0] == 0:
                 grp[c] = work.tile([P, 2, n, 4], BF16, name="grp", align_bytes=64)
-            for a, g in enumerate(gs):
-                nc.vector.tensor_tensor(
-                    out=grp[c][:, g, :, :].rearrange("p n (u e) -> p n u e", e=2),
-                    in0=xt[c, gs][:, :, a, :].bitcast(BF16).rearrange("p u (n e) -> p n u e", e=2),
-                    in1=xsc[:, g, :].rearrange("p (u e) -> p u e", e=2).unsqueeze(1).to_broadcast([P, n, 2, 2]),
-                    op=ALU.mult,
-                )
+            part = slice(gs[0], gs[-1] + 1)
+            nc.vector.tensor_tensor(
+                out=grp[c][:, part, :, :],
+                in0=xt[c, gs][:].bitcast(BF16),
+                in1=xsc[:, part, :].unsqueeze(2).to_broadcast([P, len(gs), n, 4]),
+                op=ALU.mult,
+            )
 
         def quant_x(c, gs):
             n = P * CHUNKS[c][1]

@@ -17,13 +17,16 @@ ALU = mybir.AluOpType
 
 P = 128
 K = 1024
+HALF = 512
 NOUT = 512
-CHUNKS = ((0, 1), (128, 2), (384, 2), (640, 2), (896, 1))
-NCH = len(CHUNKS)
-TILES = [(c, j) for c in range(NCH) for j in range(CHUNKS[c][1])]
-UNITS = [(0, (0, 1))] + [(c, (h,)) for c in range(1, NCH - 1) for h in range(2)] + [(NCH - 1, (0, 1))]
-PAIRS = (0, 1)
 EPS2 = 1e-24
+CHUNKS = ((0, 1), (128, 2), (384, 2), (640, 2), (896, 1))
+LAST = len(CHUNKS) - 1
+TILES = [(c, j) for c in range(len(CHUNKS)) for j in range(CHUNKS[c][1])]
+UNITS = [(0, (0, 1))] + [(c, (half,)) for c in range(1, LAST) for half in range(2)] + [(LAST, (0, 1))]
+PAIRED_CHUNK = 0
+TILES_IN_TURN_BANKS = TILES[5:7]
+COLUMN_HALVES = (slice(0, NOUT // 2), slice(NOUT // 2, NOUT))
 
 
 def tile_geometricmanifoldnetwork_pa_w8_kernel(
@@ -53,9 +56,9 @@ def tile_geometricmanifoldnetwork_pa_w8_kernel(
         make_identity(nc, ident[:])
 
         xbytes = [keep.tile([P, J, K], U8, name="xbytes%d" % c, align_bytes=64) for c, (t0, J) in enumerate(CHUNKS)]
-        w1raw = [keep.tile([P, 2, 512], I32, name="w1raw%d" % T, align_bytes=64) for T in range(2)]
-        w1 = [keep.tile([P, 2, 512], U32, name="w1_%d" % T, align_bytes=64) for T in range(2)]
-        w2 = keep.tile([P, 2, 512], U32, name="w2", align_bytes=64)
+        w1raw = [keep.tile([P, 2, HALF], I32, name="w1raw%d" % T, align_bytes=64) for T in range(2)]
+        w1 = [keep.tile([P, 2, HALF], U32, name="w1_%d" % T, align_bytes=64) for T in range(2)]
+        w2 = keep.tile([P, 2, NOUT], U32, name="w2", align_bytes=64)
         b1t = keep.tile([P, 2, 4], BF16, name="b1t")
         b2t = keep.tile([P, NOUT], BF16, name="b2t")
         w1i = W1_words.rearrange("g p n t -> p g (n t)").bitcast(I32)
@@ -65,11 +68,13 @@ def tile_geometricmanifoldnetwork_pa_w8_kernel(
             nc.sync.dma_start(out=xbytes[c][:], in_=x_bytes[t0 : t0 + P * J, :].rearrange("(p j) k -> p j k", j=J))
 
         def load_w1(T):
-            nc.sync.dma_start(out=w1raw[T][:], in_=w1i[:, :, 512 * T : 512 * T + 512])
+            nc.sync.dma_start(out=w1raw[T][:], in_=w1i[:, :, HALF * T : HALF * T + HALF])
 
         def load_scales(dst, src):
-            for q in range(4):
-                nc.sync.dma_start(out=dst[32 * q : 32 * q + 8, :].bitcast(I32), in_=src[:, 4 * q : 4 * q + 4, :].bitcast(I32))
+            for Q in range(4):
+                nc.sync.dma_start(
+                    out=dst[32 * Q : 32 * Q + 8, :].bitcast(I32), in_=src[:, 4 * Q : 4 * Q + 4, :].bitcast(I32)
+                )
 
         load_x(0)
         load_x(1)
@@ -84,13 +89,24 @@ def tile_geometricmanifoldnetwork_pa_w8_kernel(
         nc.sync.dma_start(out=b2t[:], in_=b2.partition_broadcast(P))
         load_scales(s2, W2_scales)
 
-        xv, xt, grp, xq, xs, ph, hp, hg, hq, hs, py, v, ssq, over, r = ({} for i in range(15))
+        xv = [keep.tile([P, J * K], BF16, name="xv%d" % c, align_bytes=64) for c, (t0, J) in enumerate(CHUNKS)]
+        xt, grp, xq, xs, ph, hp, hg, hq, hs, py, v, ssq, over, r = ({} for i in range(14))
 
-        def cast(c, j, on_vector=False, cols=slice(0, K)):
-            if (c, j) not in xv:
-                xv[c, j] = keep.tile([P, K], BF16, name="xv%d_%d" % (c, j), align_bytes=64)
+        def permute_w1(T):
+            nc.vector.tensor_copy(
+                out=w1[T][:].bitcast(I32).rearrange("p g (t c i) -> p g c t i", t=4, i=4),
+                in_=w1raw[T][:].rearrange("p g (c i t) -> p g c t i", t=4, i=4),
+            )
+
+        def permute_s1():
+            nc.vector.tensor_copy(
+                out=s1[:].rearrange("p (T t c i) -> p T c t i", T=2, t=4, i=16),
+                in_=s1raw[:].rearrange("p (T c i t) -> p T c t i", T=2, t=4, i=16),
+            )
+
+        def cast(c, cols, on_vector=False):
             copy = nc.vector.tensor_copy if on_vector else nc.scalar.copy
-            copy(out=xv[c, j][:, cols], in_=xbytes[c][:, j, cols].bitcast(FP8))
+            copy(out=xv[c][:, cols], in_=xbytes[c][:].rearrange("p j k -> p (j k)")[:, cols].bitcast(FP8))
 
         def turn(c, gs):
             J = CHUNKS[c][1]
@@ -99,7 +115,7 @@ def tile_geometricmanifoldnetwork_pa_w8_kernel(
             xt[c, gs] = bank
             for a, g in enumerate(gs):
                 for j in range(J):
-                    words = xv[c, j][:].bitcast(F32)
+                    words = xv[c][:, K * j : K * j + K].bitcast(F32)
                     for u in range(2):
                         nc.tensor.transpose(
                             bank[:, a, P * j : P * j + P, u], words[:, 256 * g + u : 256 * (g + 1) : 2], ident[:]
@@ -134,12 +150,11 @@ def tile_geometricmanifoldnetwork_pa_w8_kernel(
             for T, t in [(T, t) for T in Ts for t in range(4)]:
                 if t % 2 == 0:
                     ph[c, T, t // 2] = psh.tile([P, 2, n], F32, name="ph")
-                cols = slice(128 * t, 128 * t + 128)
                 for g in range(2):
                     nc.tensor.matmul_mx(
                         out=ph[c, T, t // 2][:, t % 2, :],
-                        lhsT=w1[T][:, g, cols].bitcast(FP8X4),
-                        lhsT_scale=s1[4 * g :, 512 * T + 128 * t : 512 * T + 128 * t + 128],
+                        lhsT=w1[T][:, g, P * t : P * t + P].bitcast(FP8X4),
+                        lhsT_scale=s1[4 * g :, HALF * T + P * t : HALF * T + P * t + P],
                         rhs=xq[c][:, g, :].bitcast(FP8X4),
                         rhs_scale=xs[c][:, g, :],
                         start=(g == 0),
@@ -151,12 +166,12 @@ def tile_geometricmanifoldnetwork_pa_w8_kernel(
             if Ts[0] == 0:
                 hp[c] = work.tile([P, 2, 4 * n], BF16, name="hp", align_bytes=64)
             for T, t in [(T, t) for T in Ts for t in range(4)]:
-                if c in PAIRS:
-                    plane = hp[c][:, T, 2 * n * (t // 2) + t % 2 : 2 * n * (t // 2 + 1) : 2]
+                if c == PAIRED_CHUNK:
+                    dst = hp[c][:, T, 2 * n * (t // 2) + t % 2 : 2 * n * (t // 2 + 1) : 2]
                 else:
-                    plane = hp[c][:, T, n * t : n * t + n]
+                    dst = hp[c][:, T, n * t : n * t + n]
                 nc.scalar.activation(
-                    out=plane, in_=ph[c, T, t // 2][:, t % 2, :], func=ACT.Relu, bias=b1t[:, T, t : t + 1]
+                    out=dst, in_=ph[c, T, t // 2][:, t % 2, :], func=ACT.Relu, bias=b1t[:, T, t : t + 1]
                 )
 
         def weave_h(c, Ts):
@@ -164,7 +179,7 @@ def tile_geometricmanifoldnetwork_pa_w8_kernel(
             if Ts[0] == 0:
                 hg[c] = work.tile([P, 2, 4 * n], BF16, name="hg", align_bytes=64)
             part = slice(Ts[0], Ts[-1] + 1)
-            if c in PAIRS:
+            if c == PAIRED_CHUNK:
                 nc.vector.tensor_copy(
                     out=hg[c][:, part, :].bitcast(F32).rearrange("p T (c i u) -> p T c u i", i=4, u=2),
                     in_=hp[c][:, part, :].bitcast(F32).rearrange("p T (u c i) -> p T c u i", i=4, u=2),
@@ -188,8 +203,8 @@ def tile_geometricmanifoldnetwork_pa_w8_kernel(
             )
 
         def stage2(c, j):
-            late = TILES.index((c, j)) in (5, 6)
-            py[c, j] = psx.tile([P, NOUT], F32, name="xt") if late else psy.tile([P, NOUT], F32, name="py")
+            pool, tag = (psx, "xt") if (c, j) in TILES_IN_TURN_BANKS else (psy, "py")
+            py[c, j] = pool.tile([P, NOUT], F32, name=tag)
             for T in range(2):
                 nc.tensor.matmul_mx(
                     out=py[c, j][:],
@@ -202,13 +217,13 @@ def tile_geometricmanifoldnetwork_pa_w8_kernel(
                 )
 
         def bias_v(c, j):
-            v[c, j] = work.tile([P, NOUT], F32, name="v", align_bytes=64, bufs=8)
+            v[c, j] = work.tile([P, NOUT], F32, name="v", align_bytes=64, bufs=len(TILES))
             nc.vector.tensor_tensor(out=v[c, j][:], in0=py[c, j][:], in1=b2t[:], op=ALU.add)
 
         def square_v(c, j):
-            junk = work.tile([P, NOUT], BF16, name="junk", align_bytes=64)
+            squares = work.tile([P, NOUT], BF16, name="squares", align_bytes=64)
             ssq[c, j] = work.tile([P, 1], F32, name="ssq")
-            nc.scalar.activation(out=junk[:], in_=v[c, j][:], func=ACT.Square, accum_out=ssq[c, j][:])
+            nc.scalar.activation(out=squares[:], in_=v[c, j][:], func=ACT.Square, accum_out=ssq[c, j][:])
 
         def clamp_v(c, j):
             over[c, j] = work.tile([P, 1], F32, name="over")
@@ -220,157 +235,159 @@ def tile_geometricmanifoldnetwork_pa_w8_kernel(
 
         def finish_v(c, j, on_vector):
             t0, J = CHUNKS[c]
-            o = work.tile([P, NOUT], F32, name="o", align_bytes=64, bufs=8)
+            o = work.tile([P, NOUT], F32, name="o", align_bytes=64, bufs=len(TILES))
             if on_vector:
                 nc.vector.tensor_scalar(out=o[:], in0=v[c, j][:], scalar1=r[c, j][:], scalar2=None, op0=ALU.mult)
             else:
                 nc.scalar.activation(out=o[:], in_=v[c, j][:], func=ACT.Copy, scale=r[c, j][:])
             nc.sync.dma_start(out=out[t0 : t0 + P * J, :].rearrange("(p j) o -> p j o", j=J)[:, j, :], in_=o[:])
 
-        def last_tile(stage):
-            c = NCH - 1
-            t0 = CHUNKS[c][0]
-            halves = (slice(0, 256), slice(256, NOUT))
-            if stage == 0:
-                for a, cols in enumerate(halves):
-                    py[c, a] = psy.tile([P, 256], F32, name="py")
-                    for T in range(2):
-                        nc.tensor.matmul_mx(
-                            out=py[c, a][:],
-                            lhsT=hq[c][:, T, :].bitcast(FP8X4),
-                            lhsT_scale=hs[c][:, T, :],
-                            rhs=w2[:, T, cols].bitcast(FP8X4),
-                            rhs_scale=s2[4 * T :, cols],
-                            start=(T == 0),
-                            stop=(T == 1),
-                        )
-            if stage == 1:
-                for a, cols in enumerate(halves):
-                    v[c, a] = work.tile([P, 256], F32, name="vhalf", align_bytes=64)
-                    ssq[c, a] = work.tile([P, 1], F32, name="ssqhalf")
-                    nc.vector.tensor_tensor(out=v[c, a][:], in0=py[c, a][:], in1=b2t[:, cols], op=ALU.add)
-            if stage == 2:
-                junk = work.tile([P, 256], BF16, name="junk_s", align_bytes=64)
-                nc.scalar.activation(out=junk[:], in_=v[c, 0][:], func=ACT.Square, accum_out=ssq[c, 0][:])
-            if stage == 3:
-                junk = work.tile([P, 256], BF16, name="junk_v", align_bytes=64)
-                nc.vector.scalar_tensor_tensor(
-                    out=junk[:], in0=v[c, 1][:], scalar=1.0, in1=v[c, 1][:], op0=ALU.mult, op1=ALU.mult,
-                    accum_out=ssq[c, 1][:],
+        end_py, end_v, end_ssq, end_r = {}, {}, {}, {}
+
+        def end_stage2(T):
+            for a, cols in enumerate(COLUMN_HALVES):
+                if T == 0:
+                    end_py[a] = psy.tile([P, NOUT // 2], F32, name="py")
+                nc.tensor.matmul_mx(
+                    out=end_py[a][:],
+                    lhsT=hq[LAST][:, T, :].bitcast(FP8X4),
+                    lhsT_scale=hs[LAST][:, T, :],
+                    rhs=w2[:, T, cols].bitcast(FP8X4),
+                    rhs_scale=s2[4 * T :, cols],
+                    start=(T == 0),
+                    stop=(T == 1),
                 )
-            if stage == 4:
-                over[c, 0] = work.tile([P, 1], F32, name="over")
+
+        def end_bias():
+            for a, cols in enumerate(COLUMN_HALVES):
+                end_v[a] = work.tile([P, NOUT // 2], F32, name="end_v", align_bytes=64)
+                end_ssq[a] = work.tile([P, 1], F32, name="end_ssq")
+                nc.vector.tensor_tensor(out=end_v[a][:], in0=end_py[a][:], in1=b2t[:, cols], op=ALU.add)
+
+        def end_square_on_scalar():
+            squares = work.tile([P, NOUT // 2], BF16, name="end_squares0", align_bytes=64)
+            nc.scalar.activation(out=squares[:], in_=end_v[0][:], func=ACT.Square, accum_out=end_ssq[0][:])
+
+        def end_square_on_vector():
+            squares = work.tile([P, NOUT // 2], BF16, name="end_squares1", align_bytes=64)
+            nc.vector.scalar_tensor_tensor(
+                out=squares[:],
+                in0=end_v[1][:],
+                scalar=1.0,
+                in1=end_v[1][:],
+                op0=ALU.mult,
+                op1=ALU.mult,
+                accum_out=end_ssq[1][:],
+            )
+
+        def end_sum_and_clamp():
+            end_r["clamped"] = work.tile([P, 1], F32, name="over")
+            nc.vector.tensor_scalar(
+                out=end_r["clamped"][:], in0=end_ssq[0][:], scalar1=end_ssq[1][:], scalar2=EPS2, op0=ALU.add, op1=ALU.max
+            )
+
+        def end_root():
+            end_r["root"] = work.tile([P, 1], F32, name="r")
+            nc.scalar.activation(out=end_r["root"][:], in_=end_r["clamped"][:], func=ACT.Abs_reciprocal_sqrt)
+
+        def end_finish():
+            t0 = CHUNKS[LAST][0]
+            o = work.tile([P, NOUT], F32, name="o", align_bytes=64, bufs=len(TILES))
+            for a, cols in enumerate(COLUMN_HALVES):
                 nc.vector.tensor_scalar(
-                    out=over[c, 0][:], in0=ssq[c, 0][:], scalar1=ssq[c, 1][:], scalar2=EPS2, op0=ALU.add, op1=ALU.max
+                    out=o[:, cols], in0=end_v[a][:], scalar1=end_r["root"][:], scalar2=None, op0=ALU.mult
                 )
-            if stage == 5:
-                r[c, 0] = work.tile([P, 1], F32, name="r")
-                nc.scalar.activation(out=r[c, 0][:], in_=over[c, 0][:], func=ACT.Abs_reciprocal_sqrt)
-            if stage == 6:
-                o = work.tile([P, NOUT], F32, name="o", align_bytes=64, bufs=8)
-                for a, cols in enumerate(halves):
-                    nc.vector.tensor_scalar(out=o[:, cols], in0=v[c, a][:], scalar1=r[c, 0][:], scalar2=None, op0=ALU.mult)
-                    nc.sync.dma_start(out=out[t0 : t0 + P, cols], in_=o[:, cols])
-
-        def permute_w1(T):
-            nc.vector.tensor_copy(
-                out=w1[T][:].bitcast(I32).rearrange("p g (t c i) -> p g c t i", t=4, i=4),
-                in_=w1raw[T][:].rearrange("p g (c i t) -> p g c t i", t=4, i=4),
-            )
-
-        def permute_s1():
-            nc.vector.tensor_copy(
-                out=s1[:].rearrange("p (T t c i) -> p T c t i", T=2, t=4, i=16),
-                in_=s1raw[:].rearrange("p (T c i t) -> p T c t i", T=2, t=4, i=16),
-            )
+                nc.sync.dma_start(out=out[t0 : t0 + P, cols], in_=o[:, cols])
 
         def tile(f, i, *more):
             if 0 <= i < len(TILES):
                 f(*TILES[i], *more)
 
-        def units(f, i):
+        def unit(f, i):
             if 0 <= i < len(UNITS):
                 f(*UNITS[i])
 
-        cast(0, 0, True, slice(0, 512))
-        cast(0, 0, False, slice(512, K))
+
+        cast(0, slice(0, HALF), True)
+        cast(0, slice(HALF, K))
         turn(0, (0,))
         turn(0, (1,))
-        tile(cast, 1)
-        tile(cast, 2, True)
-        units(turn, 1)
-        units(turn, 2)
-        tile(cast, 3)
-        tile(cast, 4)
+        cast(1, slice(0, K))
+        cast(1, slice(K, 2 * K), True)
+        unit(turn, 1)
+        unit(turn, 2)
+        cast(2, slice(0, 2 * K))
         scale_x(0, (0,))
         scale_x(0, (1,))
         permute_s1()
-        units(quant_x, 0)
-        permute_w1(0)
-        stage1(0, (0,))
-        units(scale_x, 1)
-        permute_w1(1)
-        stage1(0, (1,))
-        units(turn, 3)
-        units(scale_x, 2)
-        units(quant_x, 1)
-        tile(cast, 5)
-        tile(cast, 6)
+        unit(quant_x, 0)
+        for T in range(2):
+            permute_w1(T)
+            stage1(0, (T,))
+            if T == 1:
+                unit(turn, 3)
+            unit(scale_x, 1 + T)
+        unit(quant_x, 1)
+        cast(3, slice(0, 2 * K))
 
         for i in range(4):
-            units(turn, i + 4)
-            units(relu, i)
+            unit(turn, i + 4)
+            unit(relu, i)
             tile(square_v, i - 3)
-            tile(cast, i + 7)
-            units(weave_h, i - 1)
-            units(quant_x, i + 2)
+            if i == 0:
+                cast(LAST, slice(0, K))
+            unit(weave_h, i - 1)
+            unit(quant_x, i + 2)
             if i % 2 == 1:
-                units(stage1, i + 1)
-            units(quant_h, i - 1)
+                unit(stage1, i + 1)
+            unit(quant_h, i - 1)
             tile(stage2, i - 2)
             if i % 2 == 0:
-                units(stage1, i + 1)
-            units(scale_x, i + 3)
+                unit(stage1, i + 1)
+            unit(scale_x, i + 3)
             tile(bias_v, i - 2)
+
         tile(clamp_v, 0)
-        units(relu, 4)
+        unit(relu, 4)
         tile(root_v, 0)
-        units(quant_x, 6)
+        unit(quant_x, 6)
         tile(stage2, 2)
-        units(stage1, 5)
-        units(scale_x, 7)
+        unit(stage1, 5)
+        unit(scale_x, 7)
+        unit(weave_h, 3)
+        unit(quant_x, 7)
+        unit(quant_h, 3)
         tile(square_v, 1)
         tile(finish_v, 0, False)
         tile(clamp_v, 1)
-        units(weave_h, 3)
-        units(quant_x, 7)
-        units(quant_h, 3)
-        units(relu, 5)
+        unit(relu, 5)
         tile(root_v, 1)
-        units(stage1, 6)
-        units(relu, 6)
-        units(stage1, 7)
+        unit(stage1, 6)
+        unit(relu, 6)
+        unit(stage1, 7)
         tile(finish_v, 1, False)
-        relu(4, (0,))
-        units(weave_h, 4)
+        unit(relu, 7)
+
+        unit(weave_h, 4)
         tile(bias_v, 2)
-        units(quant_h, 4)
+        unit(quant_h, 4)
         tile(stage2, 3)
         tile(stage2, 4)
-        relu(4, (1,))
-        units(weave_h, 5)
-        units(weave_h, 6)
-        units(quant_h, 5)
+        unit(weave_h, 5)
+        unit(weave_h, 6)
+        unit(quant_h, 5)
         tile(bias_v, 3)
-        units(quant_h, 6)
+        unit(quant_h, 6)
         tile(stage2, 5)
         tile(stage2, 6)
         tile(bias_v, 4)
-        units(weave_h, 7)
-        tile(bias_v, 5)
-        units(quant_h, 7)
-        last_tile(0)
-        tile(bias_v, 6)
+        for T in range(2):
+            weave_h(LAST, (T,))
+        for T in range(2):
+            quant_h(LAST, (T,))
+            end_stage2(T)
+            tile(bias_v, 5 + T)
+
         tile(square_v, 2)
         tile(square_v, 3)
         tile(clamp_v, 2)
@@ -381,19 +398,19 @@ def tile_geometricmanifoldnetwork_pa_w8_kernel(
         tile(root_v, 3)
         tile(clamp_v, 4)
         tile(finish_v, 3, True)
-        last_tile(1)
+        end_bias()
         tile(square_v, 5)
         tile(root_v, 4)
         tile(clamp_v, 5)
         tile(finish_v, 4, True)
-        last_tile(3)
+        end_square_on_vector()
         tile(square_v, 6)
         tile(root_v, 5)
-        last_tile(2)
+        end_square_on_scalar()
         tile(clamp_v, 6)
         tile(finish_v, 5, True)
-        last_tile(4)
+        end_sum_and_clamp()
         tile(root_v, 6)
-        last_tile(5)
+        end_root()
         tile(finish_v, 6, True)
-        last_tile(6)
+        end_finish()

@@ -24,7 +24,7 @@ CHUNKS = ((0, 1), (128, 2), (384, 2), (640, 2), (896, 1))
 LAST = len(CHUNKS) - 1
 TILES = [(c, j) for c in range(len(CHUNKS)) for j in range(CHUNKS[c][1])]
 UNITS = [(0, (0, 1))] + [(c, (half,)) for c in range(1, LAST) for half in range(2)] + [(LAST, (0, 1))]
-PAIRED_CHUNK = 0
+PAIRED_CHUNKS = (0, 1)
 TILES_IN_TURN_BANKS = TILES[5:7]
 COLUMN_HALVES = (slice(0, NOUT // 2), slice(NOUT // 2, NOUT))
 
@@ -52,6 +52,8 @@ def tile_geometricmanifoldnetwork_pa_w8_kernel(
         nc.vector.memset(one[:], 1.0)
         warm = keep.tile([P, 2], F32, name="warm")
         nc.scalar.activation(out=warm[:], in_=one[:], func=ACT.Abs_reciprocal_sqrt)
+        zeros = keep.tile([P, HALF], BF16, name="zeros")
+        nc.gpsimd.memset(zeros[:].bitcast(I32), 0)
         ident = keep.tile([P, P], F32, name="ident", align_bytes=64)
         make_identity(nc, ident[:])
 
@@ -166,7 +168,7 @@ def tile_geometricmanifoldnetwork_pa_w8_kernel(
             if Ts[0] == 0:
                 hp[c] = work.tile([P, 2, 4 * n], BF16, name="hp", align_bytes=64)
             for T, t in [(T, t) for T in Ts for t in range(4)]:
-                if c == PAIRED_CHUNK:
+                if c in PAIRED_CHUNKS:
                     dst = hp[c][:, T, 2 * n * (t // 2) + t % 2 : 2 * n * (t // 2 + 1) : 2]
                 else:
                     dst = hp[c][:, T, n * t : n * t + n]
@@ -179,7 +181,7 @@ def tile_geometricmanifoldnetwork_pa_w8_kernel(
             if Ts[0] == 0:
                 hg[c] = work.tile([P, 2, 4 * n], BF16, name="hg", align_bytes=64)
             part = slice(Ts[0], Ts[-1] + 1)
-            if c == PAIRED_CHUNK:
+            if c in PAIRED_CHUNKS:
                 nc.vector.tensor_copy(
                     out=hg[c][:, part, :].bitcast(F32).rearrange("p T (c i u) -> p T c u i", i=4, u=2),
                     in_=hp[c][:, part, :].bitcast(F32).rearrange("p T (u c i) -> p T c u i", i=4, u=2),
@@ -299,6 +301,11 @@ def tile_geometricmanifoldnetwork_pa_w8_kernel(
                 )
                 nc.sync.dma_start(out=out[t0 : t0 + P, cols], in_=o[:, cols])
 
+        def warm_tensor(count):
+            unused = psh.tile([P, HALF], F32, name="ph")
+            for i in range(count):
+                nc.tensor.matmul(unused[:], zeros[:, 0:P], zeros[:], start=True, stop=True)
+
         def tile(f, i, *more):
             if 0 <= i < len(TILES):
                 f(*TILES[i], *more)
@@ -308,24 +315,28 @@ def tile_geometricmanifoldnetwork_pa_w8_kernel(
                 f(*UNITS[i])
 
 
+        warm_tensor(4)
         cast(0, slice(0, HALF), True)
         cast(0, slice(HALF, K))
         turn(0, (0,))
         turn(0, (1,))
+        warm_tensor(2)
         cast(1, slice(0, K))
         cast(1, slice(K, 2 * K), True)
         unit(turn, 1)
         unit(turn, 2)
+        warm_tensor(2)
         cast(2, slice(0, 2 * K))
+        permute_s1()
         scale_x(0, (0,))
         scale_x(0, (1,))
-        permute_s1()
-        unit(quant_x, 0)
         for T in range(2):
             permute_w1(T)
-            stage1(0, (T,))
+            if T == 0:
+                unit(quant_x, 0)
             if T == 1:
                 unit(turn, 3)
+            stage1(0, (T,))
             unit(scale_x, 1 + T)
         unit(quant_x, 1)
         cast(3, slice(0, 2 * K))

@@ -24,7 +24,7 @@ CHUNKS = ((0, 1), (128, 2), (384, 2), (640, 2), (896, 1))
 LAST = len(CHUNKS) - 1
 TILES = [(c, j) for c in range(len(CHUNKS)) for j in range(CHUNKS[c][1])]
 UNITS = [(0, (0, 1))] + [(c, (half,)) for c in range(1, LAST) for half in range(2)] + [(LAST, (0, 1))]
-PAIRED_CHUNKS = (0, 1)
+PAIRED_CHUNKS = (0,)
 TILES_IN_TURN_BANKS = TILES[5:7]
 COLUMN_HALVES = (slice(0, NOUT // 2), slice(NOUT // 2, NOUT))
 
@@ -46,16 +46,17 @@ def tile_geometricmanifoldnetwork_pa_w8_kernel(
         s2 = keep.tile([P, NOUT], U8, name="s2", align_bytes=64)
         xsc = keep.tile([P, 2, 4], F32, name="xsc")
         nc.scalar.dma_start(out=xsc[:], in_=x_scale.rearrange("o (g p t) -> p (o g) t", g=2, t=4))
-        nc.vector.memset(s1raw[:].bitcast(I32), 0)
-        nc.vector.memset(s2[:].bitcast(I32), 0)
         one = keep.tile([P, 2], F32, name="one")
         nc.vector.memset(one[:], 1.0)
         warm = keep.tile([P, 2], F32, name="warm")
         nc.scalar.activation(out=warm[:], in_=one[:], func=ACT.Abs_reciprocal_sqrt)
+        nc.vector.memset(s1raw[:].bitcast(I32), 0)
         zeros = keep.tile([P, HALF], BF16, name="zeros")
-        nc.gpsimd.memset(zeros[:].bitcast(I32), 0)
+        nc.vector.memset(zeros[:].bitcast(I32), 0)
+        nc.vector.memset(s2[:].bitcast(I32), 0)
         ident = keep.tile([P, P], F32, name="ident", align_bytes=64)
-        make_identity(nc, ident[:])
+        nc.vector.memset(ident[:], 0.0)
+        make_identity(nc, ident[:], nomemset=True)
 
         xbytes = [keep.tile([P, J, K], U8, name="xbytes%d" % c, align_bytes=64) for c, (t0, J) in enumerate(CHUNKS)]
         w1raw = [keep.tile([P, 2, HALF], I32, name="w1raw%d" % T, align_bytes=64) for T in range(2)]
@@ -79,13 +80,13 @@ def tile_geometricmanifoldnetwork_pa_w8_kernel(
                 )
 
         load_x(0)
-        load_x(1)
         load_scales(s1raw, W1_scales)
-        load_x(2)
+        load_x(1)
         load_w1(0)
-        load_x(3)
+        load_x(2)
         nc.sync.dma_start(out=b1t[:], in_=b1.rearrange("(g p t) -> p g t", g=2, t=4))
         load_w1(1)
+        load_x(3)
         load_x(4)
         nc.sync.dma_start(out=w2[:].bitcast(I32), in_=W2_words.rearrange("g p n t -> p g (n t)").bitcast(I32))
         nc.sync.dma_start(out=b2t[:], in_=b2.partition_broadcast(P))
@@ -106,9 +107,11 @@ def tile_geometricmanifoldnetwork_pa_w8_kernel(
                 in_=s1raw[:].rearrange("p (T c i t) -> p T c t i", T=2, t=4, i=16),
             )
 
-        def cast(c, cols, on_vector=False):
+        def cast(c, gs, on_vector=False):
             copy = nc.vector.tensor_copy if on_vector else nc.scalar.copy
-            copy(out=xv[c][:, cols], in_=xbytes[c][:].rearrange("p j k -> p (j k)")[:, cols].bitcast(FP8))
+            for j in range(CHUNKS[c][1]):
+                cols = slice(K * j + HALF * gs[0], K * j + HALF * gs[-1] + HALF)
+                copy(out=xv[c][:, cols], in_=xbytes[c][:].rearrange("p j k -> p (j k)")[:, cols].bitcast(FP8))
 
         def turn(c, gs):
             J = CHUNKS[c][1]
@@ -224,24 +227,29 @@ def tile_geometricmanifoldnetwork_pa_w8_kernel(
 
         def square_v(c, j):
             squares = work.tile([P, NOUT], BF16, name="squares", align_bytes=64)
-            ssq[c, j] = work.tile([P, 1], F32, name="ssq")
-            nc.scalar.activation(out=squares[:], in_=v[c, j][:], func=ACT.Square, accum_out=ssq[c, j][:])
+            if j == 0:
+                ssq[c] = work.tile([P, CHUNKS[c][1]], F32, name="ssq")
+            nc.scalar.activation(out=squares[:], in_=v[c, j][:], func=ACT.Square, accum_out=ssq[c][:, j : j + 1])
 
-        def clamp_v(c, j):
-            over[c, j] = work.tile([P, 1], F32, name="over")
-            nc.scalar.activation(out=over[c, j][:], in_=ssq[c, j][:], func=ACT.Relu, bias=-EPS2)
+        def clamp_v(c, js):
+            if js[0] == 0:
+                over[c] = work.tile([P, CHUNKS[c][1]], F32, name="over")
+            part = slice(js[0], js[-1] + 1)
+            nc.scalar.activation(out=over[c][:, part], in_=ssq[c][:, part], func=ACT.Relu, bias=-EPS2)
 
-        def root_v(c, j):
-            r[c, j] = work.tile([P, 1], F32, name="r")
-            nc.scalar.activation(out=r[c, j][:], in_=over[c, j][:], func=ACT.Abs_reciprocal_sqrt, bias=EPS2)
+        def root_v(c, js):
+            if js[0] == 0:
+                r[c] = work.tile([P, CHUNKS[c][1]], F32, name="r")
+            part = slice(js[0], js[-1] + 1)
+            nc.scalar.activation(out=r[c][:, part], in_=over[c][:, part], func=ACT.Abs_reciprocal_sqrt, bias=EPS2)
 
         def finish_v(c, j, on_vector):
             t0, J = CHUNKS[c]
             o = work.tile([P, NOUT], F32, name="o", align_bytes=64, bufs=len(TILES))
             if on_vector:
-                nc.vector.tensor_scalar(out=o[:], in0=v[c, j][:], scalar1=r[c, j][:], scalar2=None, op0=ALU.mult)
+                nc.vector.tensor_scalar(out=o[:], in0=v[c, j][:], scalar1=r[c][:, j : j + 1], scalar2=None, op0=ALU.mult)
             else:
-                nc.scalar.activation(out=o[:], in_=v[c, j][:], func=ACT.Copy, scale=r[c, j][:])
+                nc.scalar.activation(out=o[:], in_=v[c, j][:], func=ACT.Copy, scale=r[c][:, j : j + 1])
             nc.sync.dma_start(out=out[t0 : t0 + P * J, :].rearrange("(p j) o -> p j o", j=J)[:, j, :], in_=o[:])
 
         end_py, end_v, end_ssq, end_r = {}, {}, {}, {}
@@ -315,113 +323,123 @@ def tile_geometricmanifoldnetwork_pa_w8_kernel(
                 f(*UNITS[i])
 
 
-        warm_tensor(4)
-        cast(0, slice(0, HALF), True)
-        cast(0, slice(HALF, K))
+        warm_tensor(3)
+        cast(0, (0,), True)
+        cast(0, (1,), True)
         turn(0, (0,))
         turn(0, (1,))
+        cast(1, (0,))
+        cast(1, (1,))
         warm_tensor(2)
-        cast(1, slice(0, K))
-        cast(1, slice(K, 2 * K), True)
         unit(turn, 1)
         unit(turn, 2)
-        warm_tensor(2)
-        cast(2, slice(0, 2 * K))
         permute_s1()
         scale_x(0, (0,))
         scale_x(0, (1,))
-        for T in range(2):
-            permute_w1(T)
-            if T == 0:
-                unit(quant_x, 0)
-            if T == 1:
-                unit(turn, 3)
-            stage1(0, (T,))
-            unit(scale_x, 1 + T)
+        permute_w1(0)
+        unit(quant_x, 0)
+        warm_tensor(2)
+        stage1(0, (0,))
+        unit(cast, 3)
+        unit(cast, 4)
+        unit(scale_x, 1)
+        unit(turn, 3)
+        permute_w1(1)
+        stage1(0, (1,))
+        unit(relu, 0)
+        unit(scale_x, 2)
+        unit(turn, 4)
         unit(quant_x, 1)
-        cast(3, slice(0, 2 * K))
-
-        for i in range(4):
-            unit(turn, i + 4)
-            unit(relu, i)
-            tile(square_v, i - 3)
-            if i == 0:
-                cast(LAST, slice(0, K))
-            unit(weave_h, i - 1)
-            unit(quant_x, i + 2)
-            if i % 2 == 1:
-                unit(stage1, i + 1)
-            unit(quant_h, i - 1)
-            tile(stage2, i - 2)
-            if i % 2 == 0:
-                unit(stage1, i + 1)
-            unit(scale_x, i + 3)
-            tile(bias_v, i - 2)
-
-        tile(clamp_v, 0)
-        unit(relu, 4)
-        tile(root_v, 0)
+        unit(quant_x, 2)
+        unit(stage1, 1)
+        unit(scale_x, 3)
+        unit(weave_h, 0)
+        unit(cast, 5)
+        unit(turn, 5)
+        unit(relu, 1)
+        unit(stage1, 2)
+        unit(scale_x, 4)
+        unit(quant_h, 0)
+        unit(quant_x, 3)
+        unit(quant_x, 4)
+        tile(stage2, 0)
+        unit(cast, 6)
+        unit(turn, 6)
+        unit(relu, 2)
+        unit(stage1, 3)
+        unit(weave_h, 1)
+        unit(scale_x, 5)
+        unit(quant_h, 1)
+        tile(bias_v, 0)
+        unit(cast, 7)
+        unit(relu, 3)
+        unit(stage1, 4)
+        unit(turn, 7)
+        unit(weave_h, 2)
+        unit(scale_x, 6)
+        unit(quant_h, 2)
+        unit(quant_x, 5)
         unit(quant_x, 6)
+        tile(stage2, 1)
         tile(stage2, 2)
+        tile(square_v, 0)
+        unit(relu, 4)
+        clamp_v(0, (0,))
         unit(stage1, 5)
         unit(scale_x, 7)
         unit(weave_h, 3)
         unit(quant_x, 7)
         unit(quant_h, 3)
-        tile(square_v, 1)
-        tile(finish_v, 0, False)
-        tile(clamp_v, 1)
+        tile(bias_v, 1)
         unit(relu, 5)
-        tile(root_v, 1)
+        root_v(0, (0,))
         unit(stage1, 6)
-        unit(relu, 6)
-        unit(stage1, 7)
-        tile(finish_v, 1, False)
-        unit(relu, 7)
-
         unit(weave_h, 4)
         tile(bias_v, 2)
         unit(quant_h, 4)
+        unit(relu, 6)
+        unit(stage1, 7)
         tile(stage2, 3)
         tile(stage2, 4)
+        tile(finish_v, 0, False)
+        tile(square_v, 1)
+        tile(square_v, 2)
+        unit(relu, 7)
+        clamp_v(1, (0, 1))
         unit(weave_h, 5)
         unit(weave_h, 6)
         unit(quant_h, 5)
         tile(bias_v, 3)
         unit(quant_h, 6)
+        tile(bias_v, 4)
         tile(stage2, 5)
         tile(stage2, 6)
-        tile(bias_v, 4)
+        tile(square_v, 3)
+        root_v(1, (0, 1))
+        tile(square_v, 4)
         for T in range(2):
             weave_h(LAST, (T,))
         for T in range(2):
             quant_h(LAST, (T,))
             end_stage2(T)
             tile(bias_v, 5 + T)
-
-        tile(square_v, 2)
-        tile(square_v, 3)
-        tile(clamp_v, 2)
-        tile(square_v, 4)
-        tile(root_v, 2)
-        tile(clamp_v, 3)
-        tile(finish_v, 2, False)
-        tile(root_v, 3)
-        tile(clamp_v, 4)
-        tile(finish_v, 3, True)
-        end_bias()
+        tile(finish_v, 1, False)
+        clamp_v(2, (0, 1))
         tile(square_v, 5)
-        tile(root_v, 4)
-        tile(clamp_v, 5)
-        tile(finish_v, 4, True)
-        end_square_on_vector()
+        root_v(2, (0, 1))
+        tile(finish_v, 2, True)
+        end_bias()
         tile(square_v, 6)
-        tile(root_v, 5)
+        clamp_v(3, (0,))
+        tile(finish_v, 3, True)
+        end_square_on_vector()
         end_square_on_scalar()
-        tile(clamp_v, 6)
-        tile(finish_v, 5, True)
+        root_v(3, (0,))
+        clamp_v(3, (1,))
+        tile(finish_v, 4, True)
         end_sum_and_clamp()
-        tile(root_v, 6)
+        root_v(3, (1,))
         end_root()
+        tile(finish_v, 5, True)
         tile(finish_v, 6, True)
         end_finish()

@@ -24,7 +24,7 @@ CHUNKS = ((0, 1), (128, 2), (384, 2), (640, 2), (896, 1))
 LAST = len(CHUNKS) - 1
 TILES = [(c, j) for c in range(len(CHUNKS)) for j in range(CHUNKS[c][1])]
 UNITS = [(0, (0, 1))] + [(c, (half,)) for c in range(1, LAST) for half in range(2)] + [(LAST, (0, 1))]
-PAIRED_CHUNKS = (0,)
+PAIRED_CHUNKS = (0, 1, 2)
 TILES_IN_TURN_BANKS = TILES[5:7]
 COLUMN_HALVES = (slice(0, NOUT // 2), slice(NOUT // 2, NOUT))
 
@@ -152,12 +152,14 @@ def tile_geometricmanifoldnetwork_pa_w8_kernel(
 
         def stage1(c, Ts):
             n = P * CHUNKS[c][1]
+            per_bank = HALF // n
             for T, t in [(T, t) for T in Ts for t in range(4)]:
-                if t % 2 == 0:
-                    ph[c, T, t // 2] = psh.tile([P, 2, n], F32, name="ph")
+                if t % per_bank == 0:
+                    bank = psh.tile([P, per_bank, n], F32, name="ph")
+                ph[c, T, t] = bank[:, t % per_bank, :]
                 for g in range(2):
                     nc.tensor.matmul_mx(
-                        out=ph[c, T, t // 2][:, t % 2, :],
+                        out=ph[c, T, t],
                         lhsT=w1[T][:, g, P * t : P * t + P].bitcast(FP8X4),
                         lhsT_scale=s1[4 * g :, HALF * T + P * t : HALF * T + P * t + P],
                         rhs=xq[c][:, g, :].bitcast(FP8X4),
@@ -176,7 +178,7 @@ def tile_geometricmanifoldnetwork_pa_w8_kernel(
                 else:
                     dst = hp[c][:, T, n * t : n * t + n]
                 nc.scalar.activation(
-                    out=dst, in_=ph[c, T, t // 2][:, t % 2, :], func=ACT.Relu, bias=b1t[:, T, t : t + 1]
+                    out=dst, in_=ph[c, T, t], func=ACT.Relu, bias=b1t[:, T, t : t + 1]
                 )
 
         def weave_h(c, Ts):
@@ -323,6 +325,7 @@ def tile_geometricmanifoldnetwork_pa_w8_kernel(
                 f(*UNITS[i])
 
 
+        BOTH = (0, 1)
         warm_tensor(3)
         cast(0, (0,), True)
         cast(0, (1,), True)
@@ -340,13 +343,14 @@ def tile_geometricmanifoldnetwork_pa_w8_kernel(
         unit(quant_x, 0)
         warm_tensor(2)
         stage1(0, (0,))
-        unit(cast, 3)
-        unit(cast, 4)
+        cast(2, BOTH)
         unit(scale_x, 1)
         unit(turn, 3)
         permute_w1(1)
         stage1(0, (1,))
-        unit(relu, 0)
+        relu(0, (0,))
+        cast(3, BOTH)
+        relu(0, (1,))
         unit(scale_x, 2)
         unit(turn, 4)
         unit(quant_x, 1)
@@ -354,22 +358,18 @@ def tile_geometricmanifoldnetwork_pa_w8_kernel(
         unit(stage1, 1)
         unit(scale_x, 3)
         unit(weave_h, 0)
-        unit(cast, 5)
         unit(turn, 5)
         unit(relu, 1)
         unit(stage1, 2)
         unit(scale_x, 4)
         unit(quant_h, 0)
-        unit(quant_x, 3)
-        unit(quant_x, 4)
+        quant_x(2, BOTH)
         tile(stage2, 0)
-        unit(cast, 6)
         unit(turn, 6)
         unit(relu, 2)
         unit(stage1, 3)
         unit(weave_h, 1)
         unit(scale_x, 5)
-        unit(quant_h, 1)
         tile(bias_v, 0)
         unit(cast, 7)
         unit(relu, 3)
@@ -377,9 +377,8 @@ def tile_geometricmanifoldnetwork_pa_w8_kernel(
         unit(turn, 7)
         unit(weave_h, 2)
         unit(scale_x, 6)
-        unit(quant_h, 2)
-        unit(quant_x, 5)
-        unit(quant_x, 6)
+        quant_h(1, BOTH)
+        quant_x(3, BOTH)
         tile(stage2, 1)
         tile(stage2, 2)
         tile(square_v, 0)
@@ -389,14 +388,13 @@ def tile_geometricmanifoldnetwork_pa_w8_kernel(
         unit(scale_x, 7)
         unit(weave_h, 3)
         unit(quant_x, 7)
-        unit(quant_h, 3)
         tile(bias_v, 1)
         unit(relu, 5)
         root_v(0, (0,))
         unit(stage1, 6)
         unit(weave_h, 4)
         tile(bias_v, 2)
-        unit(quant_h, 4)
+        quant_h(2, BOTH)
         unit(relu, 6)
         unit(stage1, 7)
         tile(stage2, 3)
@@ -425,9 +423,9 @@ def tile_geometricmanifoldnetwork_pa_w8_kernel(
             tile(bias_v, 5 + T)
         tile(finish_v, 1, False)
         clamp_v(2, (0, 1))
-        tile(square_v, 5)
+        tile(finish_v, 2, False)
         root_v(2, (0, 1))
-        tile(finish_v, 2, True)
+        tile(square_v, 5)
         end_bias()
         tile(square_v, 6)
         clamp_v(3, (0,))
@@ -441,5 +439,5 @@ def tile_geometricmanifoldnetwork_pa_w8_kernel(
         root_v(3, (1,))
         end_root()
         tile(finish_v, 5, True)
-        tile(finish_v, 6, True)
+        tile(finish_v, 6, False)
         end_finish()

@@ -21,12 +21,9 @@ HALF = 512
 NOUT = 512
 EPS2 = 1e-24
 CHUNKS = ((0, 1), (128, 2), (384, 2), (640, 2), (896, 1))
-LAST = len(CHUNKS) - 1
 TILES = [(c, j) for c in range(len(CHUNKS)) for j in range(CHUNKS[c][1])]
-UNITS = [(0, (0, 1))] + [(c, (half,)) for c in range(1, LAST) for half in range(2)] + [(LAST, (0, 1))]
-PAIRED_CHUNKS = (0, 1, 2)
-TILES_IN_TURN_BANKS = TILES[5:7]
-COLUMN_HALVES = (slice(0, NOUT // 2), slice(NOUT // 2, NOUT))
+BOTH = (0, 1)
+PAIRED = ((0, 0), (0, 1), (1, 0), (1, 1), (2, 0), (2, 1))
 
 
 def tile_geometricmanifoldnetwork_pa_w8_kernel(
@@ -39,6 +36,7 @@ def tile_geometricmanifoldnetwork_pa_w8_kernel(
         psx = ctx.enter_context(tc.psum_pool(name="psx", bufs=2))
         psh = ctx.enter_context(tc.psum_pool(name="psh", bufs=4))
         psy = ctx.enter_context(tc.psum_pool(name="psy", bufs=2))
+        PS = {"xt": psx, "ph": psh, "py": psy}
         ctx.enter_context(tc.manual_schedule())
 
         s1raw = keep.tile([P, K], U8, name="s1raw", align_bytes=64)
@@ -93,10 +91,10 @@ def tile_geometricmanifoldnetwork_pa_w8_kernel(
         load_scales(s2, W2_scales)
 
         xv = [keep.tile([P, J * K], BF16, name="xv%d" % c, align_bytes=64) for c, (t0, J) in enumerate(CHUNKS)]
-        xt, grp, xq, xs, ph, hp, hg, hq, hs, py, v, ssq, over, r = ({} for i in range(14))
+        xt, grp, xq, xs, ph, hp, hg, hq, hs, py, v, ssq, over, r, pw, xp = ({} for i in range(16))
 
-        def permute_w1(T):
-            nc.vector.tensor_copy(
+        def permute_w1(T, eng=None):
+            (eng or nc.vector).tensor_copy(
                 out=w1[T][:].bitcast(I32).rearrange("p g (t c i) -> p g c t i", t=4, i=4),
                 in_=w1raw[T][:].rearrange("p g (c i t) -> p g c t i", t=4, i=4),
             )
@@ -107,53 +105,52 @@ def tile_geometricmanifoldnetwork_pa_w8_kernel(
                 in_=s1raw[:].rearrange("p (T c i t) -> p T c t i", T=2, t=4, i=16),
             )
 
-        def cast(c, gs, on_vector=False):
+        def cast(c, j, gs=BOTH, on_vector=False):
             copy = nc.vector.tensor_copy if on_vector else nc.scalar.copy
-            for j in range(CHUNKS[c][1]):
-                cols = slice(K * j + HALF * gs[0], K * j + HALF * gs[-1] + HALF)
-                copy(out=xv[c][:, cols], in_=xbytes[c][:].rearrange("p j k -> p (j k)")[:, cols].bitcast(FP8))
+            cols = slice(K * j + HALF * gs[0], K * j + HALF * gs[-1] + HALF)
+            copy(out=xv[c][:, cols], in_=xbytes[c][:].rearrange("p j k -> p (j k)")[:, cols].bitcast(FP8))
 
-        def turn(c, gs):
-            J = CHUNKS[c][1]
-            pool, tag = (psy, "py") if c == 0 else (psx, "xt")
-            bank = pool.tile([P, len(gs), P * J, 2], F32, name=tag)
-            xt[c, gs] = bank
+        def turn(c, q, gs, pool="xt"):
+            js = (2 * q, 2 * q + 1) if CHUNKS[c][1] > 1 else (0,)
+            bank = PS[pool].tile([P, len(gs), P * len(js), 2], F32, name=pool)
+            xt[c, q, gs] = bank
             for a, g in enumerate(gs):
-                for j in range(J):
+                for b, j in enumerate(js):
                     words = xv[c][:, K * j : K * j + K].bitcast(F32)
                     for u in range(2):
                         nc.tensor.transpose(
-                            bank[:, a, P * j : P * j + P, u], words[:, 256 * g + u : 256 * (g + 1) : 2], ident[:]
+                            bank[:, a, P * b : P * b + P, u], words[:, 256 * g + u : 256 * (g + 1) : 2], ident[:]
                         )
 
-        def scale_x(c, gs):
+        def need(d, c, shape, dtype, name, bufs=3):
+            if c not in d:
+                d[c] = work.tile(shape, dtype, name=name, align_bytes=64, bufs=bufs)
+            return d[c]
+
+        def scale_x(c, q, gs):
             n = P * CHUNKS[c][1]
-            if gs[0] == 0:
-                grp[c] = work.tile([P, 2, n, 4], BF16, name="grp", align_bytes=64)
+            m = min(n, 256)
             part = slice(gs[0], gs[-1] + 1)
             nc.vector.tensor_tensor(
-                out=grp[c][:, part, :, :],
-                in0=xt[c, gs][:].bitcast(BF16),
-                in1=xsc[:, part, :].unsqueeze(2).to_broadcast([P, len(gs), n, 4]),
+                out=need(grp, c, [P, 2, n, 4], BF16, "grp", 2)[:, part, m * q : m * q + m, :],
+                in0=xt[c, q, gs][:].bitcast(BF16),
+                in1=xsc[:, part, :].unsqueeze(2).to_broadcast([P, len(gs), m, 4]),
                 op=ALU.mult,
             )
 
         def quant_x(c, gs):
             n = P * CHUNKS[c][1]
-            if gs[0] == 0:
-                xq[c] = work.tile([P, 2, n], U32, name="xq", align_bytes=64)
-                xs[c] = work.tile([P, 2, n], U8, name="xs", align_bytes=64)
             part = slice(gs[0], gs[-1] + 1)
             nc.vector.quantize_mx(
-                out=xq[c][:, part, :].rearrange("p g n -> p (g n)").bitcast(FP8X4),
-                scales=xs[c][:, part, :].rearrange("p g n -> p (g n)"),
+                out=need(xq, c, [P, 2, n], U32, "xq")[:, part, :].rearrange("p g n -> p (g n)").bitcast(FP8X4),
+                scales=need(xs, c, [P, 2, n], U8, "xs")[:, part, :].rearrange("p g n -> p (g n)"),
                 in_=grp[c][:, part, :, :].rearrange("p g n t -> p (g n t)"),
             )
 
-        def stage1(c, Ts):
+        def stage1(c, T, ts=range(4)):
             n = P * CHUNKS[c][1]
             per_bank = HALF // n
-            for T, t in [(T, t) for T in Ts for t in range(4)]:
+            for t in ts:
                 if t % per_bank == 0:
                     bank = psh.tile([P, per_bank, n], F32, name="ph")
                 ph[c, T, t] = bank[:, t % per_bank, :]
@@ -168,53 +165,46 @@ def tile_geometricmanifoldnetwork_pa_w8_kernel(
                         stop=(g == 1),
                     )
 
-        def relu(c, Ts):
+        def relu(c, T, ts=range(4)):
             n = P * CHUNKS[c][1]
-            if Ts[0] == 0:
-                hp[c] = work.tile([P, 2, 4 * n], BF16, name="hp", align_bytes=64)
-            for T, t in [(T, t) for T in Ts for t in range(4)]:
-                if c in PAIRED_CHUNKS:
-                    dst = hp[c][:, T, 2 * n * (t // 2) + t % 2 : 2 * n * (t // 2 + 1) : 2]
+            planes = need(hp, c, [P, 2, 4 * n], BF16, "hp", 2)
+            for t in ts:
+                if (c, T) in PAIRED:
+                    dst = planes[:, T, 2 * n * (t // 2) + t % 2 : 2 * n * (t // 2 + 1) : 2]
                 else:
-                    dst = hp[c][:, T, n * t : n * t + n]
-                nc.scalar.activation(
-                    out=dst, in_=ph[c, T, t], func=ACT.Relu, bias=b1t[:, T, t : t + 1]
-                )
+                    dst = planes[:, T, n * t : n * t + n]
+                nc.scalar.activation(out=dst, in_=ph[c, T, t], func=ACT.Relu, bias=b1t[:, T, t : t + 1])
 
         def weave_h(c, Ts):
             n = P * CHUNKS[c][1]
-            if Ts[0] == 0:
-                hg[c] = work.tile([P, 2, 4 * n], BF16, name="hg", align_bytes=64)
+            dst = need(hg, c, [P, 2, 4 * n], BF16, "hg", 2)
             part = slice(Ts[0], Ts[-1] + 1)
-            if c in PAIRED_CHUNKS:
+            if (c, Ts[0]) in PAIRED:
                 nc.vector.tensor_copy(
-                    out=hg[c][:, part, :].bitcast(F32).rearrange("p T (c i u) -> p T c u i", i=4, u=2),
+                    out=dst[:, part, :].bitcast(F32).rearrange("p T (c i u) -> p T c u i", i=4, u=2),
                     in_=hp[c][:, part, :].bitcast(F32).rearrange("p T (u c i) -> p T c u i", i=4, u=2),
                 )
             else:
                 nc.vector.tensor_copy(
-                    out=hg[c][:, part, :].rearrange("p T (c i t) -> p T c t i", i=4, t=4),
+                    out=dst[:, part, :].rearrange("p T (c i t) -> p T c t i", i=4, t=4),
                     in_=hp[c][:, part, :].rearrange("p T (t c i) -> p T c t i", i=4, t=4),
                 )
 
         def quant_h(c, Ts):
             n = P * CHUNKS[c][1]
-            if Ts[0] == 0:
-                hq[c] = work.tile([P, 2, n], U32, name="hq", align_bytes=64)
-                hs[c] = work.tile([P, 2, n], U8, name="hs", align_bytes=64)
             part = slice(Ts[0], Ts[-1] + 1)
             nc.vector.quantize_mx(
-                out=hq[c][:, part, :].rearrange("p T n -> p (T n)").bitcast(FP8X4),
-                scales=hs[c][:, part, :].rearrange("p T n -> p (T n)"),
+                out=need(hq, c, [P, 2, n], U32, "hq")[:, part, :].rearrange("p T n -> p (T n)").bitcast(FP8X4),
+                scales=need(hs, c, [P, 2, n], U8, "hs")[:, part, :].rearrange("p T n -> p (T n)"),
                 in_=hg[c][:, part, :].rearrange("p T n -> p (T n)"),
             )
 
-        def stage2(c, j):
-            pool, tag = (psx, "xt") if (c, j) in TILES_IN_TURN_BANKS else (psy, "py")
-            py[c, j] = pool.tile([P, NOUT], F32, name=tag)
+        def stage2(i, pool="py"):
+            c, j = TILES[i]
+            py[i] = PS[pool].tile([P, NOUT], F32, name=pool)
             for T in range(2):
                 nc.tensor.matmul_mx(
-                    out=py[c, j][:],
+                    out=py[i][:],
                     lhsT=hq[c][:, T, P * j : P * j + P].bitcast(FP8X4),
                     lhsT_scale=hs[c][:, T, P * j : P * j + P],
                     rhs=w2[:, T, :].bitcast(FP8X4),
@@ -223,221 +213,211 @@ def tile_geometricmanifoldnetwork_pa_w8_kernel(
                     stop=(T == 1),
                 )
 
-        def bias_v(c, j):
-            v[c, j] = work.tile([P, NOUT], F32, name="v", align_bytes=64, bufs=len(TILES))
-            nc.vector.tensor_tensor(out=v[c, j][:], in0=py[c, j][:], in1=b2t[:], op=ALU.add)
+        ssq = keep.tile([P, len(TILES) + 1], F32, name="ssq")
+        over = keep.tile([P, len(TILES)], F32, name="over")
+        r = keep.tile([P, len(TILES)], F32, name="r")
 
-        def square_v(c, j):
+        def bias_v(i):
+            v[i] = work.tile([P, NOUT], F32, name="v", align_bytes=64, bufs=len(TILES))
+            nc.vector.tensor_tensor(out=v[i][:], in0=py[i][:], in1=b2t[:], op=ALU.add)
+
+        def square_v(i):
             squares = work.tile([P, NOUT], BF16, name="squares", align_bytes=64)
-            if j == 0:
-                ssq[c] = work.tile([P, CHUNKS[c][1]], F32, name="ssq")
-            nc.scalar.activation(out=squares[:], in_=v[c, j][:], func=ACT.Square, accum_out=ssq[c][:, j : j + 1])
+            nc.scalar.activation(out=squares[:], in_=v[i][:], func=ACT.Square, accum_out=ssq[:, i : i + 1])
 
-        def clamp_v(c, js):
-            if js[0] == 0:
-                over[c] = work.tile([P, CHUNKS[c][1]], F32, name="over")
-            part = slice(js[0], js[-1] + 1)
-            nc.scalar.activation(out=over[c][:, part], in_=ssq[c][:, part], func=ACT.Relu, bias=-EPS2)
+        def clamp_v(a, b):
+            nc.scalar.activation(out=over[:, a:b], in_=ssq[:, a:b], func=ACT.Relu, bias=-EPS2)
 
-        def root_v(c, js):
-            if js[0] == 0:
-                r[c] = work.tile([P, CHUNKS[c][1]], F32, name="r")
-            part = slice(js[0], js[-1] + 1)
-            nc.scalar.activation(out=r[c][:, part], in_=over[c][:, part], func=ACT.Abs_reciprocal_sqrt, bias=EPS2)
+        def root_v(a, b):
+            nc.scalar.activation(out=r[:, a:b], in_=over[:, a:b], func=ACT.Abs_reciprocal_sqrt, bias=EPS2)
 
-        def finish_v(c, j, on_vector):
+        def finish_v(i, on_vector, parts=1):
+            c, j = TILES[i]
             t0, J = CHUNKS[c]
             o = work.tile([P, NOUT], F32, name="o", align_bytes=64, bufs=len(TILES))
-            if on_vector:
-                nc.vector.tensor_scalar(out=o[:], in0=v[c, j][:], scalar1=r[c][:, j : j + 1], scalar2=None, op0=ALU.mult)
-            else:
-                nc.scalar.activation(out=o[:], in_=v[c, j][:], func=ACT.Copy, scale=r[c][:, j : j + 1])
-            nc.sync.dma_start(out=out[t0 : t0 + P * J, :].rearrange("(p j) o -> p j o", j=J)[:, j, :], in_=o[:])
+            for a in range(parts):
+                cols = slice(NOUT // parts * a, NOUT // parts * (a + 1))
+                if on_vector == "G":
+                    nc.gpsimd.tensor_scalar(
+                        out=o[:, cols], in0=v[i][:, cols], scalar1=r[:, i : i + 1], scalar2=0.0, op0=ALU.mult, op1=ALU.add
+                    )
+                elif on_vector:
+                    nc.vector.tensor_scalar(
+                        out=o[:, cols], in0=v[i][:, cols], scalar1=r[:, i : i + 1], scalar2=None, op0=ALU.mult
+                    )
+                else:
+                    nc.scalar.activation(out=o[:, cols], in_=v[i][:, cols], func=ACT.Copy, scale=r[:, i : i + 1])
+                nc.sync.dma_start(
+                    out=out[t0 : t0 + P * J, :].rearrange("(p j) o -> p j o", j=J)[:, j, cols], in_=o[:, cols]
+                )
 
-        end_py, end_v, end_ssq, end_r = {}, {}, {}, {}
+        end_py = {}
+        LASTT = len(TILES) - 1
 
         def end_stage2(T):
-            for a, cols in enumerate(COLUMN_HALVES):
+            c = len(CHUNKS) - 1
+            for a in range(2):
                 if T == 0:
                     end_py[a] = psy.tile([P, NOUT // 2], F32, name="py")
+                cols = slice(256 * a, 256 * a + 256)
                 nc.tensor.matmul_mx(
                     out=end_py[a][:],
-                    lhsT=hq[LAST][:, T, :].bitcast(FP8X4),
-                    lhsT_scale=hs[LAST][:, T, :],
+                    lhsT=hq[c][:, T, :].bitcast(FP8X4),
+                    lhsT_scale=hs[c][:, T, :],
                     rhs=w2[:, T, cols].bitcast(FP8X4),
                     rhs_scale=s2[4 * T :, cols],
                     start=(T == 0),
                     stop=(T == 1),
                 )
 
-        def end_bias():
-            for a, cols in enumerate(COLUMN_HALVES):
-                end_v[a] = work.tile([P, NOUT // 2], F32, name="end_v", align_bytes=64)
-                end_ssq[a] = work.tile([P, 1], F32, name="end_ssq")
-                nc.vector.tensor_tensor(out=end_v[a][:], in0=end_py[a][:], in1=b2t[:, cols], op=ALU.add)
+        def end_bias(a):
+            cols = slice(256 * a, 256 * a + 256)
+            nc.vector.tensor_tensor(out=need(v, LASTT, [P, NOUT], F32, "v", len(TILES))[:, cols], in0=end_py[a][:], in1=b2t[:, cols], op=ALU.add)
 
-        def end_square_on_scalar():
-            squares = work.tile([P, NOUT // 2], BF16, name="end_squares0", align_bytes=64)
-            nc.scalar.activation(out=squares[:], in_=end_v[0][:], func=ACT.Square, accum_out=end_ssq[0][:])
+        def end_square(a, on_vector):
+            cols = slice(256 * a, 256 * a + 256)
+            squares = work.tile([P, NOUT // 2], BF16, name="end_squares%d" % a, align_bytes=64)
+            acc = need(end_py, ("s", a), [P, 1], F32, "end_ssq%d" % a, 1)
+            if on_vector:
+                nc.vector.scalar_tensor_tensor(
+                    out=squares[:], in0=v[LASTT][:, cols], scalar=1.0, in1=v[LASTT][:, cols], op0=ALU.mult, op1=ALU.mult, accum_out=acc[:]
+                )
+            else:
+                nc.scalar.activation(out=squares[:], in_=v[LASTT][:, cols], func=ACT.Square, accum_out=acc[:])
 
-        def end_square_on_vector():
-            squares = work.tile([P, NOUT // 2], BF16, name="end_squares1", align_bytes=64)
-            nc.vector.scalar_tensor_tensor(
-                out=squares[:],
-                in0=end_v[1][:],
-                scalar=1.0,
-                in1=end_v[1][:],
-                op0=ALU.mult,
-                op1=ALU.mult,
-                accum_out=end_ssq[1][:],
-            )
-
-        def end_sum_and_clamp():
-            end_r["clamped"] = work.tile([P, 1], F32, name="over")
+        def end_clamp():
             nc.vector.tensor_scalar(
-                out=end_r["clamped"][:], in0=end_ssq[0][:], scalar1=end_ssq[1][:], scalar2=EPS2, op0=ALU.add, op1=ALU.max
+                out=need(end_py, "c", [P, 1], F32, "end_c", 1)[:], in0=end_py["s", 0][:], scalar1=end_py["s", 1][:], scalar2=EPS2, op0=ALU.add, op1=ALU.max
             )
 
         def end_root():
-            end_r["root"] = work.tile([P, 1], F32, name="r")
-            nc.scalar.activation(out=end_r["root"][:], in_=end_r["clamped"][:], func=ACT.Abs_reciprocal_sqrt)
-
-        def end_finish():
-            t0 = CHUNKS[LAST][0]
-            o = work.tile([P, NOUT], F32, name="o", align_bytes=64, bufs=len(TILES))
-            for a, cols in enumerate(COLUMN_HALVES):
-                nc.vector.tensor_scalar(
-                    out=o[:, cols], in0=end_v[a][:], scalar1=end_r["root"][:], scalar2=None, op0=ALU.mult
-                )
-                nc.sync.dma_start(out=out[t0 : t0 + P, cols], in_=o[:, cols])
+            nc.scalar.activation(out=r[:, LASTT : LASTT + 1], in_=end_py["c"][:], func=ACT.Abs_reciprocal_sqrt)
 
         def warm_tensor(count):
             unused = psh.tile([P, HALF], F32, name="ph")
             for i in range(count):
                 nc.tensor.matmul(unused[:], zeros[:, 0:P], zeros[:], start=True, stop=True)
 
-        def tile(f, i, *more):
-            if 0 <= i < len(TILES):
-                f(*TILES[i], *more)
-
-        def unit(f, i):
-            if 0 <= i < len(UNITS):
-                f(*UNITS[i])
-
-
-        BOTH = (0, 1)
         warm_tensor(3)
-        cast(0, (0,), True)
-        cast(0, (1,), True)
-        turn(0, (0,))
-        turn(0, (1,))
-        cast(1, (0,))
-        cast(1, (1,))
+        cast(0, 0, (0,), True)
+        cast(0, 0, (1,), True)
+        turn(0, 0, (0,), "py")
+        turn(0, 0, (1,), "py")
+        cast(1, 0, (0,))
+        cast(1, 1, (0,))
+        cast(1, 0, (1,))
+        cast(1, 1, (1,))
+        turn(1, 0, (0,))
+        turn(1, 0, (1,))
         warm_tensor(2)
-        unit(turn, 1)
-        unit(turn, 2)
         permute_s1()
-        scale_x(0, (0,))
-        scale_x(0, (1,))
+        scale_x(0, 0, (0,))
+        scale_x(0, 0, (1,))
         permute_w1(0)
-        unit(quant_x, 0)
-        warm_tensor(2)
-        stage1(0, (0,))
-        cast(2, BOTH)
-        unit(scale_x, 1)
-        unit(turn, 3)
+        quant_x(0, BOTH)
+        stage1(0, 0)
+        cast(2, 0)
+        cast(2, 1)
+        cast(3, 0)
+        cast(3, 1)
+        scale_x(1, 0, (0,))
+        turn(2, 0, (0,))
         permute_w1(1)
-        stage1(0, (1,))
-        relu(0, (0,))
-        cast(3, BOTH)
-        relu(0, (1,))
-        unit(scale_x, 2)
-        unit(turn, 4)
-        unit(quant_x, 1)
-        unit(quant_x, 2)
-        unit(stage1, 1)
-        unit(scale_x, 3)
-        unit(weave_h, 0)
-        unit(turn, 5)
-        unit(relu, 1)
-        unit(stage1, 2)
-        unit(scale_x, 4)
-        unit(quant_h, 0)
+        stage1(0, 1)
+        relu(0, 0)
+        relu(0, 1)
+        cast(4, 0)
+        scale_x(1, 0, (1,))
+        warm_tensor(2)
+        turn(2, 0, (1,))
+        quant_x(1, (0,))
+        quant_x(1, (1,))
+        stage1(1, 0)
+        stage1(1, 1)
+        scale_x(2, 0, (0,))
+        turn(3, 0, (0,))
+        weave_h(0, BOTH)
+        relu(1, 0)
+        scale_x(2, 0, (1,))
+        turn(3, 0, (1,))
+        quant_h(0, BOTH)
         quant_x(2, BOTH)
-        tile(stage2, 0)
-        unit(turn, 6)
-        unit(relu, 2)
-        unit(stage1, 3)
-        unit(weave_h, 1)
-        unit(scale_x, 5)
-        tile(bias_v, 0)
-        unit(cast, 7)
-        unit(relu, 3)
-        unit(stage1, 4)
-        unit(turn, 7)
-        unit(weave_h, 2)
-        unit(scale_x, 6)
+        stage2(0)
+        relu(1, 1)
+        stage1(2, 0)
+        scale_x(3, 0, (0,))
+        turn(4, 0, BOTH)
+        weave_h(1, (0,))
+        bias_v(0)
+        weave_h(1, (1,))
+        relu(2, 0)
+        stage1(2, 1)
+        square_v(0)
+        relu(2, 1)
+        scale_x(3, 0, (1,))
         quant_h(1, BOTH)
         quant_x(3, BOTH)
-        tile(stage2, 1)
-        tile(stage2, 2)
-        tile(square_v, 0)
-        unit(relu, 4)
-        clamp_v(0, (0,))
-        unit(stage1, 5)
-        unit(scale_x, 7)
-        unit(weave_h, 3)
-        unit(quant_x, 7)
-        tile(bias_v, 1)
-        unit(relu, 5)
-        root_v(0, (0,))
-        unit(stage1, 6)
-        unit(weave_h, 4)
-        tile(bias_v, 2)
+        stage2(1)
+        stage1(3, 0)
+        stage1(3, 1)
+        stage2(2)
+        scale_x(4, 0, BOTH)
+        weave_h(2, (0,))
+        quant_x(4, BOTH)
+        weave_h(2, (1,))
+        bias_v(1)
         quant_h(2, BOTH)
-        unit(relu, 6)
-        unit(stage1, 7)
-        tile(stage2, 3)
-        tile(stage2, 4)
-        tile(finish_v, 0, False)
-        tile(square_v, 1)
-        tile(square_v, 2)
-        unit(relu, 7)
-        clamp_v(1, (0, 1))
-        unit(weave_h, 5)
-        unit(weave_h, 6)
-        unit(quant_h, 5)
-        tile(bias_v, 3)
-        unit(quant_h, 6)
-        tile(bias_v, 4)
-        tile(stage2, 5)
-        tile(stage2, 6)
-        tile(square_v, 3)
-        root_v(1, (0, 1))
-        tile(square_v, 4)
-        for T in range(2):
-            weave_h(LAST, (T,))
-        for T in range(2):
-            quant_h(LAST, (T,))
-            end_stage2(T)
-            tile(bias_v, 5 + T)
-        tile(finish_v, 1, False)
-        clamp_v(2, (0, 1))
-        tile(finish_v, 2, False)
-        root_v(2, (0, 1))
-        tile(square_v, 5)
-        end_bias()
-        tile(square_v, 6)
-        clamp_v(3, (0,))
-        tile(finish_v, 3, True)
-        end_square_on_vector()
-        end_square_on_scalar()
-        root_v(3, (0,))
-        clamp_v(3, (1,))
-        tile(finish_v, 4, True)
-        end_sum_and_clamp()
-        root_v(3, (1,))
+        bias_v(2)
+        relu(3, 0)
+        clamp_v(0, 1)
+        relu(3, 1)
+        root_v(0, 1)
+        stage1(4, 0)
+        stage1(4, 1)
+        stage2(3)
+        stage2(4)
+        square_v(1)
+        square_v(2)
+        relu(4, 0)
+        relu(4, 1)
+        weave_h(3, (0,))
+        weave_h(3, (1,))
+        quant_h(3, (0,))
+        bias_v(3)
+        quant_h(3, (1,))
+        bias_v(4)
+        stage2(5, "xt")
+        stage2(6, "xt")
+        clamp_v(1, 3)
+        square_v(3)
+        root_v(1, 3)
+        square_v(4)
+        weave_h(4, BOTH)
+        finish_v(0, True)
+        quant_h(4, (0,))
+        end_stage2(0)
+        quant_h(4, (1,))
+        end_stage2(1)
+        bias_v(5)
+        bias_v(6)
+        finish_v(1, False)
+        clamp_v(3, 5)
+        finish_v(2, False)
+        root_v(3, 5)
+        square_v(5)
+        end_bias(0)
+        end_bias(1)
+        square_v(6)
+        finish_v(3, True)
+        end_square(1, True)
+        clamp_v(5, 6)
+        end_square(0, False)
+        root_v(5, 6)
+        clamp_v(6, 7)
+        finish_v(4, True)
+        end_clamp()
+        root_v(6, 7)
         end_root()
-        tile(finish_v, 5, True)
-        tile(finish_v, 6, False)
-        end_finish()
+        finish_v(5, True)
+        finish_v(7, True, 2)
+        finish_v(6, False)

@@ -95,14 +95,14 @@ def tile_geometricmanifoldnetwork_pa_w8_kernel(
 
         def permute_w1(T, eng=None):
             (eng or nc.vector).tensor_copy(
-                out=w1[T][:].bitcast(I32).rearrange("p g (t c i) -> p g c t i", t=4, i=4),
-                in_=w1raw[T][:].rearrange("p g (c i t) -> p g c t i", t=4, i=4),
+                out=w1[T][:].bitcast(I32).rearrange("p g (t c i) -> p g c t i", t=4, i=2),
+                in_=w1raw[T][:].rearrange("p g (c i t) -> p g c t i", t=4, i=2),
             )
 
         def permute_s1():
             nc.vector.tensor_copy(
-                out=s1[:].rearrange("p (T t c i) -> p T c t i", T=2, t=4, i=16),
-                in_=s1raw[:].rearrange("p (T c i t) -> p T c t i", T=2, t=4, i=16),
+                out=s1[:].rearrange("p (T t c i) -> p T c t i", T=2, t=4, i=8),
+                in_=s1raw[:].rearrange("p (T c i t) -> p T c t i", T=2, t=4, i=8),
             )
 
         def cast(c, j, gs=BOTH, on_vector=False):
@@ -181,8 +181,8 @@ def tile_geometricmanifoldnetwork_pa_w8_kernel(
             part = slice(Ts[0], Ts[-1] + 1)
             if (c, Ts[0]) in PAIRED:
                 nc.vector.tensor_copy(
-                    out=dst[:, part, :].bitcast(F32).rearrange("p T (c i u) -> p T c u i", i=4, u=2),
-                    in_=hp[c][:, part, :].bitcast(F32).rearrange("p T (u c i) -> p T c u i", i=4, u=2),
+                    out=dst[:, part, :].bitcast(F32).rearrange("p T (n u) -> p T n u", u=2),
+                    in_=hp[c][:, part, :].bitcast(F32).rearrange("p T (u n) -> p T n u", u=2),
                 )
             else:
                 nc.vector.tensor_copy(

@@ -49,8 +49,6 @@ def tile_geometricmanifoldnetwork_pa_w8_kernel(
         warm = keep.tile([P, 2], F32, name="warm")
         nc.scalar.activation(out=warm[:], in_=one[:], func=ACT.Abs_reciprocal_sqrt)
         nc.vector.memset(s1raw[:].bitcast(I32), 0)
-        zeros = keep.tile([P, HALF], BF16, name="zeros")
-        nc.vector.memset(zeros[:].bitcast(I32), 0)
         nc.vector.memset(s2[:].bitcast(I32), 0)
         ident = keep.tile([P, P], F32, name="ident", align_bytes=64)
         nc.vector.memset(ident[:], 0.0)
@@ -293,12 +291,6 @@ def tile_geometricmanifoldnetwork_pa_w8_kernel(
         def end_root():
             nc.scalar.activation(out=r[:, LASTT : LASTT + 1], in_=end_py["c"][:], func=ACT.Abs_reciprocal_sqrt)
 
-        def warm_tensor(count):
-            unused = psh.tile([P, HALF], F32, name="ph")
-            for i in range(count):
-                nc.tensor.matmul(unused[:], zeros[:, 0:P], zeros[:], start=True, stop=True)
-
-        warm_tensor(3)
         cast(0, 0, (0,), True)
         cast(0, 0, (1,), True)
         turn(0, 0, (0,), "py")
@@ -309,7 +301,6 @@ def tile_geometricmanifoldnetwork_pa_w8_kernel(
         cast(1, 1, (1,))
         turn(1, 0, (0,))
         turn(1, 0, (1,))
-        warm_tensor(2)
         permute_s1()
         scale_x(0, 0, (0,))
         scale_x(0, 0, (1,))
@@ -328,7 +319,6 @@ def tile_geometricmanifoldnetwork_pa_w8_kernel(
         relu(0, 1)
         cast(4, 0)
         scale_x(1, 0, (1,))
-        warm_tensor(2)
         turn(2, 0, (1,))
         quant_x(1, (0,))
         quant_x(1, (1,))

@@ -75,18 +75,27 @@ def tile_geometricmanifoldnetwork_pa_w8_kernel(
                     out=dst[32 * Q : 32 * Q + 8, :].bitcast(I32), in_=src[:, 4 * Q : 4 * Q + 4, :].bitcast(I32)
                 )
 
+        def load_b1():
+            nc.scalar.dma_start(out=b1t[:], in_=b1.rearrange("(g p t) -> p g t", g=2, t=4))
+
+        def load_w2():
+            nc.sync.dma_start(out=w2[:].bitcast(I32), in_=W2_words.rearrange("g p n t -> p g (n t)").bitcast(I32))
+
+        def load_b2():
+            nc.sync.dma_start(out=b2t[:], in_=b2.partition_broadcast(P))
+
         load_x(0)
         load_scales(s1raw, W1_scales)
         load_x(1)
         load_w1(0)
+        load_b1()
         load_x(2)
-        nc.sync.dma_start(out=b1t[:], in_=b1.rearrange("(g p t) -> p g t", g=2, t=4))
-        load_w1(1)
         load_x(3)
+        load_w1(1)
         load_x(4)
-        nc.sync.dma_start(out=w2[:].bitcast(I32), in_=W2_words.rearrange("g p n t -> p g (n t)").bitcast(I32))
-        nc.sync.dma_start(out=b2t[:], in_=b2.partition_broadcast(P))
+        load_w2()
         load_scales(s2, W2_scales)
+        load_b2()
 
         xv = [keep.tile([P, J * K], BF16, name="xv%d" % c, align_bytes=64) for c, (t0, J) in enumerate(CHUNKS)]
         xt, grp, xq, xs, ph, hp, hg, hq, hs, py, v, ssq, over, r, pw, xp = ({} for i in range(16))
@@ -311,27 +320,26 @@ def tile_geometricmanifoldnetwork_pa_w8_kernel(
         cast(2, 1)
         cast(3, 0)
         cast(3, 1)
+        relu(0, 0)
+        cast(4, 0)
         scale_x(1, 0, (0,))
         turn(2, 0, (0,))
-        permute_w1(1)
-        stage1(0, 1)
-        relu(0, 0)
-        relu(0, 1)
-        cast(4, 0)
         scale_x(1, 0, (1,))
         turn(2, 0, (1,))
-        quant_x(1, (0,))
-        quant_x(1, (1,))
+        permute_w1(1)
+        quant_x(1, BOTH)
+        stage1(0, 1)
         stage1(1, 0)
+        relu(0, 1)
         stage1(1, 1)
         scale_x(2, 0, (0,))
-        turn(3, 0, (0,))
-        weave_h(0, BOTH)
         relu(1, 0)
         scale_x(2, 0, (1,))
+        turn(3, 0, (0,))
         turn(3, 0, (1,))
-        quant_h(0, BOTH)
+        weave_h(0, BOTH)
         quant_x(2, BOTH)
+        quant_h(0, BOTH)
         stage2(0)
         relu(1, 1)
         stage1(2, 0)
@@ -352,16 +360,15 @@ def tile_geometricmanifoldnetwork_pa_w8_kernel(
         stage1(3, 1)
         stage2(2)
         scale_x(4, 0, BOTH)
-        weave_h(2, (0,))
-        quant_x(4, BOTH)
-        weave_h(2, (1,))
         bias_v(1)
+        weave_h(2, BOTH)
+        quant_x(4, BOTH)
         quant_h(2, BOTH)
         bias_v(2)
-        relu(3, 0)
         clamp_v(0, 1)
-        relu(3, 1)
+        relu(3, 0)
         root_v(0, 1)
+        relu(3, 1)
         stage1(4, 0)
         stage1(4, 1)
         stage2(3)
@@ -372,9 +379,8 @@ def tile_geometricmanifoldnetwork_pa_w8_kernel(
         relu(4, 1)
         weave_h(3, (0,))
         weave_h(3, (1,))
-        quant_h(3, (0,))
         bias_v(3)
-        quant_h(3, (1,))
+        quant_h(3, BOTH)
         bias_v(4)
         stage2(5, "xt")
         stage2(6, "xt")
@@ -384,9 +390,8 @@ def tile_geometricmanifoldnetwork_pa_w8_kernel(
         square_v(4)
         weave_h(4, BOTH)
         finish_v(0, True)
-        quant_h(4, (0,))
+        quant_h(4, BOTH)
         end_stage2(0)
-        quant_h(4, (1,))
         end_stage2(1)
         bias_v(5)
         bias_v(6)
@@ -395,19 +400,19 @@ def tile_geometricmanifoldnetwork_pa_w8_kernel(
         finish_v(2, False)
         root_v(3, 5)
         square_v(5)
-        end_bias(0)
-        end_bias(1)
         square_v(6)
-        finish_v(3, True)
-        end_square(1, True)
         clamp_v(5, 6)
+        end_bias(0)
+        finish_v(3, True)
+        end_bias(1)
+        finish_v(4, True)
+        end_square(1, True)
         end_square(0, False)
         root_v(5, 6)
         clamp_v(6, 7)
-        finish_v(4, True)
+        finish_v(5, True)
         end_clamp()
         root_v(6, 7)
         end_root()
-        finish_v(5, True)
+        finish_v(6, True)
         finish_v(7, True, 2)
-        finish_v(6, False)

@@ -23,7 +23,7 @@ EPS2 = 1e-24
 CHUNKS = ((0, 1), (128, 2), (384, 2), (640, 2), (896, 1))
 TILES = [(c, j) for c in range(len(CHUNKS)) for j in range(CHUNKS[c][1])]
 BOTH = (0, 1)
-PAIRED = ((0, 0), (0, 1), (1, 0), (1, 1), (2, 0), (2, 1))
+PAIRED = ((0, 0), (0, 1), (2, 1))
 
 
 def tile_geometricmanifoldnetwork_pa_w8_kernel(
@@ -90,8 +90,8 @@ def tile_geometricmanifoldnetwork_pa_w8_kernel(
         load_w1(0)
         load_b1()
         load_x(2)
-        load_x(3)
         load_w1(1)
+        load_x(3)
         load_x(4)
         load_w2()
         load_scales(s2, W2_scales)
@@ -184,7 +184,7 @@ def tile_geometricmanifoldnetwork_pa_w8_kernel(
 
         def weave_h(c, Ts):
             n = P * CHUNKS[c][1]
-            dst = need(hg, c, [P, 2, 4 * n], BF16, "hg", 2)
+            dst = need(hg, c, [P, 2, 4 * n], BF16, "hg", 1)
             part = slice(Ts[0], Ts[-1] + 1)
             if (c, Ts[0]) in PAIRED:
                 nc.vector.tensor_copy(
@@ -196,6 +196,17 @@ def tile_geometricmanifoldnetwork_pa_w8_kernel(
                     out=dst[:, part, :].rearrange("p T (c i t) -> p T c t i", i=4, t=4),
                     in_=hp[c][:, part, :].rearrange("p T (t c i) -> p T c t i", i=4, t=4),
                 )
+
+        def weave_g(c, T):
+            n = P * CHUNKS[c][1]
+            nc.gpsimd.tensor_scalar(
+                out=need(hg, c, [P, 2, 4 * n], BF16, "hg", 1)[:, T, :].rearrange("p (n t) -> p n t", t=4),
+                in0=hp[c][:, T, :].rearrange("p (t n) -> p n t", t=4),
+                scalar1=1.0,
+                scalar2=0.0,
+                op0=ALU.mult,
+                op1=ALU.add,
+            )
 
         def quant_h(c, Ts):
             n = P * CHUNKS[c][1]
@@ -238,10 +249,10 @@ def tile_geometricmanifoldnetwork_pa_w8_kernel(
         def root_v(a, b):
             nc.scalar.activation(out=r[:, a:b], in_=over[:, a:b], func=ACT.Abs_reciprocal_sqrt, bias=EPS2)
 
-        def finish_v(i, on_vector, parts=1):
+        def finish_v(i, on_vector, parts=1, slot=None):
             c, j = TILES[i]
             t0, J = CHUNKS[c]
-            o = work.tile([P, NOUT], F32, name="o", align_bytes=64, bufs=len(TILES))
+            o = work.tile([P, NOUT], F32, name=slot or "o", align_bytes=64, bufs=1 if slot else len(TILES))
             for a in range(parts):
                 cols = slice(NOUT // parts * a, NOUT // parts * (a + 1))
                 if on_vector == "G":
@@ -318,10 +329,9 @@ def tile_geometricmanifoldnetwork_pa_w8_kernel(
         stage1(0, 0)
         cast(2, 0)
         cast(2, 1)
+        relu(0, 0)
         cast(3, 0)
         cast(3, 1)
-        relu(0, 0)
-        cast(4, 0)
         scale_x(1, 0, (0,))
         turn(2, 0, (0,))
         scale_x(1, 0, (1,))
@@ -338,37 +348,41 @@ def tile_geometricmanifoldnetwork_pa_w8_kernel(
         turn(3, 0, (0,))
         turn(3, 0, (1,))
         weave_h(0, BOTH)
-        quant_x(2, BOTH)
+        quant_x(2, (0,))
         quant_h(0, BOTH)
-        stage2(0)
+        quant_x(2, (1,))
+        weave_g(1, 0)
         relu(1, 1)
+        cast(4, 0)
+        weave_g(1, 1)
         stage1(2, 0)
+        stage2(0)
         scale_x(3, 0, (0,))
-        turn(4, 0, BOTH)
-        weave_h(1, (0,))
+        scale_x(3, 0, (1,))
         bias_v(0)
-        weave_h(1, (1,))
         relu(2, 0)
         stage1(2, 1)
-        square_v(0)
+        turn(4, 0, BOTH)
         relu(2, 1)
-        scale_x(3, 0, (1,))
-        quant_h(1, BOTH)
+        square_v(0)
         quant_x(3, BOTH)
+        quant_h(1, BOTH)
+        weave_g(2, 0)
+        stage1(3, 0, (0, 1))
         stage2(1)
-        stage1(3, 0)
+        stage1(3, 0, (2, 3))
         stage1(3, 1)
         stage2(2)
         scale_x(4, 0, BOTH)
         bias_v(1)
-        weave_h(2, BOTH)
+        weave_h(2, (1,))
         quant_x(4, BOTH)
         quant_h(2, BOTH)
         bias_v(2)
-        clamp_v(0, 1)
         relu(3, 0)
-        root_v(0, 1)
+        clamp_v(0, 1)
         relu(3, 1)
+        root_v(0, 1)
         stage1(4, 0)
         stage1(4, 1)
         stage2(3)
@@ -397,7 +411,7 @@ def tile_geometricmanifoldnetwork_pa_w8_kernel(
         bias_v(6)
         finish_v(1, False)
         clamp_v(3, 5)
-        finish_v(2, False)
+        finish_v(2, "G", 1, "hg")
         root_v(3, 5)
         square_v(5)
         square_v(6)
@@ -407,12 +421,12 @@ def tile_geometricmanifoldnetwork_pa_w8_kernel(
         end_bias(1)
         finish_v(4, True)
         end_square(1, True)
-        end_square(0, False)
-        root_v(5, 6)
         clamp_v(6, 7)
+        root_v(5, 6)
+        end_square(0, False)
+        root_v(6, 7)
         finish_v(5, True)
         end_clamp()
-        root_v(6, 7)
         end_root()
         finish_v(6, True)
         finish_v(7, True, 2)

@@ -20,9 +20,11 @@ K = 1024
 HALF = 512
 NOUT = 512
 EPS2 = 1e-24
-CHUNKS = ((0, 1), (128, 2), (384, 2), (640, 2), (896, 1))
-TILES = [(c, j) for c in range(len(CHUNKS)) for j in range(CHUNKS[c][1])]
 BOTH = (0, 1)
+CHUNKS = ((0, 1), (128, 2), (384, 2), (640, 2), (896, 1))
+LAST = len(CHUNKS) - 1
+TILES = [(c, j) for c in range(len(CHUNKS)) for j in range(CHUNKS[c][1])]
+END = len(TILES) - 1
 PAIRED = ((0, 0), (0, 1), (2, 1))
 
 
@@ -32,12 +34,19 @@ def tile_geometricmanifoldnetwork_pa_w8_kernel(
     nc = tc.nc
     with ExitStack() as ctx:
         keep = ctx.enter_context(tc.tile_pool(name="keep", bufs=1))
-        work = ctx.enter_context(tc.tile_pool(name="work", bufs=3))
         psx = ctx.enter_context(tc.psum_pool(name="psx", bufs=2))
         psh = ctx.enter_context(tc.psum_pool(name="psh", bufs=4))
         psy = ctx.enter_context(tc.psum_pool(name="psy", bufs=2))
-        PS = {"xt": psx, "ph": psh, "py": psy}
         ctx.enter_context(tc.manual_schedule())
+
+        def each_chunk(name, dtype, per_token):
+            return [
+                keep.tile([P, 2, per_token * P * J], dtype, name="%s%d" % (name, c), align_bytes=64)
+                for c, (t0, J) in enumerate(CHUNKS)
+            ]
+
+        def each_tile(name, dtype, columns):
+            return [keep.tile([P, columns], dtype, name="%s%d" % (name, i), align_bytes=64) for i in range(len(TILES))]
 
         s1raw = keep.tile([P, K], U8, name="s1raw", align_bytes=64)
         s1 = keep.tile([P, K], U8, name="s1", align_bytes=64)
@@ -55,8 +64,8 @@ def tile_geometricmanifoldnetwork_pa_w8_kernel(
         make_identity(nc, ident[:], nomemset=True)
 
         xbytes = [keep.tile([P, J, K], U8, name="xbytes%d" % c, align_bytes=64) for c, (t0, J) in enumerate(CHUNKS)]
-        w1raw = [keep.tile([P, 2, HALF], I32, name="w1raw%d" % T, align_bytes=64) for T in range(2)]
-        w1 = [keep.tile([P, 2, HALF], U32, name="w1_%d" % T, align_bytes=64) for T in range(2)]
+        w1raw = [keep.tile([P, 2, HALF], I32, name="w1raw%d" % T, align_bytes=64) for T in BOTH]
+        w1 = [keep.tile([P, 2, HALF], U32, name="w1_%d" % T, align_bytes=64) for T in BOTH]
         w2 = keep.tile([P, 2, NOUT], U32, name="w2", align_bytes=64)
         b1t = keep.tile([P, 2, 4], BF16, name="b1t")
         b2t = keep.tile([P, NOUT], BF16, name="b2t")
@@ -64,7 +73,7 @@ def tile_geometricmanifoldnetwork_pa_w8_kernel(
 
         def load_x(c):
             t0, J = CHUNKS[c]
-            nc.sync.dma_start(out=xbytes[c][:], in_=x_bytes[t0 : t0 + P * J, :].rearrange("(p j) k -> p j k", j=J))
+            nc.sync.dma_start(out=xbytes[c][:], in_=x_bytes[t0 : t0 + P * J, :].rearrange("(j p) k -> p j k", j=J))
 
         def load_w1(T):
             nc.sync.dma_start(out=w1raw[T][:], in_=w1i[:, :, HALF * T : HALF * T + HALF])
@@ -75,33 +84,32 @@ def tile_geometricmanifoldnetwork_pa_w8_kernel(
                     out=dst[32 * Q : 32 * Q + 8, :].bitcast(I32), in_=src[:, 4 * Q : 4 * Q + 4, :].bitcast(I32)
                 )
 
-        def load_b1():
-            nc.scalar.dma_start(out=b1t[:], in_=b1.rearrange("(g p t) -> p g t", g=2, t=4))
-
-        def load_w2():
-            nc.sync.dma_start(out=w2[:].bitcast(I32), in_=W2_words.rearrange("g p n t -> p g (n t)").bitcast(I32))
-
-        def load_b2():
-            nc.sync.dma_start(out=b2t[:], in_=b2.partition_broadcast(P))
-
         load_x(0)
         load_scales(s1raw, W1_scales)
         load_x(1)
         load_w1(0)
-        load_b1()
+        nc.scalar.dma_start(out=b1t[:], in_=b1.rearrange("(g p t) -> p g t", g=2, t=4))
         load_x(2)
         load_w1(1)
         load_x(3)
         load_x(4)
-        load_w2()
+        nc.sync.dma_start(out=w2[:].bitcast(I32), in_=W2_words.rearrange("g p n t -> p g (n t)").bitcast(I32))
         load_scales(s2, W2_scales)
-        load_b2()
+        nc.sync.dma_start(out=b2t[:], in_=b2.partition_broadcast(P))
 
-        xv = [keep.tile([P, J * K], BF16, name="xv%d" % c, align_bytes=64) for c, (t0, J) in enumerate(CHUNKS)]
-        xt, grp, xq, xs, ph, hp, hg, hq, hs, py, v, ssq, over, r, pw, xp = ({} for i in range(16))
+        xv = [keep.tile([P, J, K], BF16, name="xv%d" % c, align_bytes=64) for c, (t0, J) in enumerate(CHUNKS)]
+        xg, hp = each_chunk("xg", BF16, 4), each_chunk("hp", BF16, 4)
+        xq, hq = each_chunk("xq", U32, 1), each_chunk("hq", U32, 1)
+        xs, hs = each_chunk("xs", U8, 1), each_chunk("hs", U8, 1)
+        v, squares = each_tile("v", F32, NOUT), each_tile("squares", BF16, NOUT)
+        ssq = keep.tile([P, len(TILES)], F32, name="ssq")
+        over = keep.tile([P, len(TILES)], F32, name="over")
+        r = keep.tile([P, len(TILES)], F32, name="r")
+        end_ssq = [keep.tile([P, 1], F32, name="end_ssq%d" % a) for a in BOTH]
+        xt, ph, hg, py = {}, {}, {}, {}
 
-        def permute_w1(T, eng=None):
-            (eng or nc.vector).tensor_copy(
+        def permute_w1(T):
+            nc.vector.tensor_copy(
                 out=w1[T][:].bitcast(I32).rearrange("p g (t c i) -> p g c t i", t=4, i=2),
                 in_=w1raw[T][:].rearrange("p g (c i t) -> p g c t i", t=4, i=2),
             )
@@ -112,47 +120,43 @@ def tile_geometricmanifoldnetwork_pa_w8_kernel(
                 in_=s1raw[:].rearrange("p (T c i t) -> p T c t i", T=2, t=4, i=8),
             )
 
-        def cast(c, j, gs=BOTH, on_vector=False):
+        def cast(c, gs=BOTH, on_vector=False):
             copy = nc.vector.tensor_copy if on_vector else nc.scalar.copy
-            cols = slice(K * j + HALF * gs[0], K * j + HALF * gs[-1] + HALF)
-            copy(out=xv[c][:, cols], in_=xbytes[c][:].rearrange("p j k -> p (j k)")[:, cols].bitcast(FP8))
+            cols = slice(HALF * gs[0], HALF * gs[-1] + HALF)
+            for j in range(CHUNKS[c][1]):
+                copy(out=xv[c][:, j, cols], in_=xbytes[c][:, j, cols].bitcast(FP8))
 
-        def turn(c, q, gs, pool="xt"):
-            js = (2 * q, 2 * q + 1) if CHUNKS[c][1] > 1 else (0,)
-            bank = PS[pool].tile([P, len(gs), P * len(js), 2], F32, name=pool)
-            xt[c, q, gs] = bank
+        def turn(c, gs, in_v_bank=False):
+            J = CHUNKS[c][1]
+            pool, name = (psy, "py") if in_v_bank else (psx, "xt")
+            xt[c, gs] = pool.tile([P, len(gs), P * J, 2], F32, name=name)
             for a, g in enumerate(gs):
-                for b, j in enumerate(js):
-                    words = xv[c][:, K * j : K * j + K].bitcast(F32)
+                for j in range(J):
+                    words = xv[c][:, j, :].bitcast(F32)
                     for u in range(2):
                         nc.tensor.transpose(
-                            bank[:, a, P * b : P * b + P, u], words[:, 256 * g + u : 256 * (g + 1) : 2], ident[:]
+                            xt[c, gs][:, a, P * j : P * j + P, u], words[:, 256 * g + u : 256 * (g + 1) : 2], ident[:]
                         )
 
-        def need(d, c, shape, dtype, name, bufs=3):
-            if c not in d:
-                d[c] = work.tile(shape, dtype, name=name, align_bytes=64, bufs=bufs)
-            return d[c]
-
-        def scale_x(c, q, gs):
-            n = P * CHUNKS[c][1]
-            m = min(n, 256)
+        def scale_x(c, gs):
             part = slice(gs[0], gs[-1] + 1)
             nc.vector.tensor_tensor(
-                out=need(grp, c, [P, 2, n, 4], BF16, "grp", 2)[:, part, m * q : m * q + m, :],
-                in0=xt[c, q, gs][:].bitcast(BF16),
-                in1=xsc[:, part, :].unsqueeze(2).to_broadcast([P, len(gs), m, 4]),
+                out=xg[c][:, part, :].rearrange("p g (n t) -> p g n t", t=4),
+                in0=xt[c, gs][:].bitcast(BF16),
+                in1=xsc[:, part, :].unsqueeze(2).to_broadcast([P, len(gs), P * CHUNKS[c][1], 4]),
                 op=ALU.mult,
             )
 
-        def quant_x(c, gs):
-            n = P * CHUNKS[c][1]
+        def quantise(codes, scales, values, gs):
             part = slice(gs[0], gs[-1] + 1)
             nc.vector.quantize_mx(
-                out=need(xq, c, [P, 2, n], U32, "xq")[:, part, :].rearrange("p g n -> p (g n)").bitcast(FP8X4),
-                scales=need(xs, c, [P, 2, n], U8, "xs")[:, part, :].rearrange("p g n -> p (g n)"),
-                in_=grp[c][:, part, :, :].rearrange("p g n t -> p (g n t)"),
+                out=codes[:, part, :].rearrange("p g n -> p (g n)").bitcast(FP8X4),
+                scales=scales[:, part, :].rearrange("p g n -> p (g n)"),
+                in_=values[:, part, :].rearrange("p g n -> p (g n)"),
             )
+
+        def quant_x(c, gs=BOTH):
+            quantise(xq[c], xs[c], xg[c], gs)
 
         def stage1(c, T, ts=range(4)):
             n = P * CHUNKS[c][1]
@@ -161,7 +165,7 @@ def tile_geometricmanifoldnetwork_pa_w8_kernel(
                 if t % per_bank == 0:
                     bank = psh.tile([P, per_bank, n], F32, name="ph")
                 ph[c, T, t] = bank[:, t % per_bank, :]
-                for g in range(2):
+                for g in BOTH:
                     nc.tensor.matmul_mx(
                         out=ph[c, T, t],
                         lhsT=w1[T][:, g, P * t : P * t + P].bitcast(FP8X4),
@@ -172,35 +176,36 @@ def tile_geometricmanifoldnetwork_pa_w8_kernel(
                         stop=(g == 1),
                     )
 
-        def relu(c, T, ts=range(4)):
+        def relu(c, T):
             n = P * CHUNKS[c][1]
-            planes = need(hp, c, [P, 2, 4 * n], BF16, "hp", 2)
-            for t in ts:
+            for t in range(4):
                 if (c, T) in PAIRED:
-                    dst = planes[:, T, 2 * n * (t // 2) + t % 2 : 2 * n * (t // 2 + 1) : 2]
+                    dst = hp[c][:, T, 2 * n * (t // 2) + t % 2 : 2 * n * (t // 2 + 1) : 2]
                 else:
-                    dst = planes[:, T, n * t : n * t + n]
+                    dst = hp[c][:, T, n * t : n * t + n]
                 nc.scalar.activation(out=dst, in_=ph[c, T, t], func=ACT.Relu, bias=b1t[:, T, t : t + 1])
 
+        def woven(c):
+            if c not in hg:
+                hg[c] = keep.tile([P, 2, 4 * P * CHUNKS[c][1]], BF16, name="hg%d" % max(c, 2), align_bytes=64)
+            return hg[c]
+
         def weave_h(c, Ts):
-            n = P * CHUNKS[c][1]
-            dst = need(hg, c, [P, 2, 4 * n], BF16, "hg", 1)
             part = slice(Ts[0], Ts[-1] + 1)
             if (c, Ts[0]) in PAIRED:
                 nc.vector.tensor_copy(
-                    out=dst[:, part, :].bitcast(F32).rearrange("p T (n u) -> p T n u", u=2),
+                    out=woven(c)[:, part, :].bitcast(F32).rearrange("p T (n u) -> p T n u", u=2),
                     in_=hp[c][:, part, :].bitcast(F32).rearrange("p T (u n) -> p T n u", u=2),
                 )
             else:
                 nc.vector.tensor_copy(
-                    out=dst[:, part, :].rearrange("p T (c i t) -> p T c t i", i=4, t=4),
+                    out=woven(c)[:, part, :].rearrange("p T (c i t) -> p T c t i", i=4, t=4),
                     in_=hp[c][:, part, :].rearrange("p T (t c i) -> p T c t i", i=4, t=4),
                 )
 
-        def weave_g(c, T):
-            n = P * CHUNKS[c][1]
+        def weave_h_on_gpsimd(c, T):
             nc.gpsimd.tensor_scalar(
-                out=need(hg, c, [P, 2, 4 * n], BF16, "hg", 1)[:, T, :].rearrange("p (n t) -> p n t", t=4),
+                out=woven(c)[:, T, :].rearrange("p (n t) -> p n t", t=4),
                 in0=hp[c][:, T, :].rearrange("p (t n) -> p n t", t=4),
                 scalar1=1.0,
                 scalar2=0.0,
@@ -208,40 +213,32 @@ def tile_geometricmanifoldnetwork_pa_w8_kernel(
                 op1=ALU.add,
             )
 
-        def quant_h(c, Ts):
-            n = P * CHUNKS[c][1]
-            part = slice(Ts[0], Ts[-1] + 1)
-            nc.vector.quantize_mx(
-                out=need(hq, c, [P, 2, n], U32, "hq")[:, part, :].rearrange("p T n -> p (T n)").bitcast(FP8X4),
-                scales=need(hs, c, [P, 2, n], U8, "hs")[:, part, :].rearrange("p T n -> p (T n)"),
-                in_=hg[c][:, part, :].rearrange("p T n -> p (T n)"),
+        def quant_h(c):
+            quantise(hq[c], hs[c], hg[c], BOTH)
+
+        def stage2_pass(dst, i, T, cols):
+            c, j = TILES[i]
+            nc.tensor.matmul_mx(
+                out=dst,
+                lhsT=hq[c][:, T, P * j : P * j + P].bitcast(FP8X4),
+                lhsT_scale=hs[c][:, T, P * j : P * j + P],
+                rhs=w2[:, T, cols].bitcast(FP8X4),
+                rhs_scale=s2[4 * T :, cols],
+                start=(T == 0),
+                stop=(T == 1),
             )
 
-        def stage2(i, pool="py"):
-            c, j = TILES[i]
-            py[i] = PS[pool].tile([P, NOUT], F32, name=pool)
-            for T in range(2):
-                nc.tensor.matmul_mx(
-                    out=py[i][:],
-                    lhsT=hq[c][:, T, P * j : P * j + P].bitcast(FP8X4),
-                    lhsT_scale=hs[c][:, T, P * j : P * j + P],
-                    rhs=w2[:, T, :].bitcast(FP8X4),
-                    rhs_scale=s2[4 * T :, :],
-                    start=(T == 0),
-                    stop=(T == 1),
-                )
-
-        ssq = keep.tile([P, len(TILES) + 1], F32, name="ssq")
-        over = keep.tile([P, len(TILES)], F32, name="over")
-        r = keep.tile([P, len(TILES)], F32, name="r")
+        def stage2(i, in_x_bank=False):
+            pool, name = (psx, "xt") if in_x_bank else (psy, "py")
+            py[i] = pool.tile([P, NOUT], F32, name=name)
+            for T in BOTH:
+                stage2_pass(py[i][:], i, T, slice(0, NOUT))
 
         def bias_v(i):
-            v[i] = work.tile([P, NOUT], F32, name="v", align_bytes=64, bufs=len(TILES))
             nc.vector.tensor_tensor(out=v[i][:], in0=py[i][:], in1=b2t[:], op=ALU.add)
 
         def square_v(i):
-            squares = work.tile([P, NOUT], BF16, name="squares", align_bytes=64)
-            nc.scalar.activation(out=squares[:], in_=v[i][:], func=ACT.Square, accum_out=ssq[:, i : i + 1])
+            nc.scalar.activation(out=squares[i][:], in_=v[i][:], func=ACT.Square, accum_out=ssq[:, i : i + 1])
 
         def clamp_v(a, b):
             nc.scalar.activation(out=over[:, a:b], in_=ssq[:, a:b], func=ACT.Relu, bias=-EPS2)
@@ -249,184 +246,175 @@ def tile_geometricmanifoldnetwork_pa_w8_kernel(
         def root_v(a, b):
             nc.scalar.activation(out=r[:, a:b], in_=over[:, a:b], func=ACT.Abs_reciprocal_sqrt, bias=EPS2)
 
-        def finish_v(i, on_vector, parts=1, slot=None):
-            c, j = TILES[i]
-            t0, J = CHUNKS[c]
-            o = work.tile([P, NOUT], F32, name=slot or "o", align_bytes=64, bufs=1 if slot else len(TILES))
-            for a in range(parts):
-                cols = slice(NOUT // parts * a, NOUT // parts * (a + 1))
-                if on_vector == "G":
-                    nc.gpsimd.tensor_scalar(
-                        out=o[:, cols], in0=v[i][:, cols], scalar1=r[:, i : i + 1], scalar2=0.0, op0=ALU.mult, op1=ALU.add
-                    )
-                elif on_vector:
-                    nc.vector.tensor_scalar(
-                        out=o[:, cols], in0=v[i][:, cols], scalar1=r[:, i : i + 1], scalar2=None, op0=ALU.mult
-                    )
-                else:
-                    nc.scalar.activation(out=o[:, cols], in_=v[i][:, cols], func=ACT.Copy, scale=r[:, i : i + 1])
-                nc.sync.dma_start(
-                    out=out[t0 : t0 + P * J, :].rearrange("(p j) o -> p j o", j=J)[:, j, cols], in_=o[:, cols]
-                )
+        def store(i, scaled):
+            nc.sync.dma_start(out=out[P * i : P * i + P, :], in_=scaled[:])
 
-        end_py = {}
-        LASTT = len(TILES) - 1
+        def finish_v(i):
+            scaled = keep.tile([P, NOUT], F32, name="o%d" % i, align_bytes=64)
+            nc.vector.tensor_scalar(out=scaled[:], in0=v[i][:], scalar1=r[:, i : i + 1], scalar2=None, op0=ALU.mult)
+            store(i, scaled)
 
-        def end_stage2(T):
-            c = len(CHUNKS) - 1
-            for a in range(2):
-                if T == 0:
-                    end_py[a] = psy.tile([P, NOUT // 2], F32, name="py")
-                cols = slice(256 * a, 256 * a + 256)
-                nc.tensor.matmul_mx(
-                    out=end_py[a][:],
-                    lhsT=hq[c][:, T, :].bitcast(FP8X4),
-                    lhsT_scale=hs[c][:, T, :],
-                    rhs=w2[:, T, cols].bitcast(FP8X4),
-                    rhs_scale=s2[4 * T :, cols],
-                    start=(T == 0),
-                    stop=(T == 1),
-                )
+        def finish_v_on_scalar(i):
+            scaled = keep.tile([P, NOUT], F32, name="o%d" % i, align_bytes=64)
+            nc.scalar.activation(out=scaled[:], in_=v[i][:], func=ACT.Copy, scale=r[:, i : i + 1])
+            store(i, scaled)
+
+        def finish_v_on_gpsimd(i):
+            scaled = keep.tile([P, NOUT], F32, name="hg%d" % LAST, align_bytes=64)
+            nc.gpsimd.tensor_scalar(
+                out=scaled[:], in0=v[i][:], scalar1=r[:, i : i + 1], scalar2=0.0, op0=ALU.mult, op1=ALU.add
+            )
+            store(i, scaled)
+
+        sides = [slice(NOUT // 2 * a, NOUT // 2 * (a + 1)) for a in BOTH]
+
+        def end_stage2():
+            for T in BOTH:
+                for a in BOTH:
+                    if T == 0:
+                        py[END, a] = psy.tile([P, NOUT // 2], F32, name="py")
+                    stage2_pass(py[END, a][:], END, T, sides[a])
 
         def end_bias(a):
-            cols = slice(256 * a, 256 * a + 256)
-            nc.vector.tensor_tensor(out=need(v, LASTT, [P, NOUT], F32, "v", len(TILES))[:, cols], in0=end_py[a][:], in1=b2t[:, cols], op=ALU.add)
+            nc.vector.tensor_tensor(out=v[END][:, sides[a]], in0=py[END, a][:], in1=b2t[:, sides[a]], op=ALU.add)
 
-        def end_square(a, on_vector):
-            cols = slice(256 * a, 256 * a + 256)
-            squares = work.tile([P, NOUT // 2], BF16, name="end_squares%d" % a, align_bytes=64)
-            acc = need(end_py, ("s", a), [P, 1], F32, "end_ssq%d" % a, 1)
-            if on_vector:
-                nc.vector.scalar_tensor_tensor(
-                    out=squares[:], in0=v[LASTT][:, cols], scalar=1.0, in1=v[LASTT][:, cols], op0=ALU.mult, op1=ALU.mult, accum_out=acc[:]
-                )
-            else:
-                nc.scalar.activation(out=squares[:], in_=v[LASTT][:, cols], func=ACT.Square, accum_out=acc[:])
+        def end_square_on_scalar(a):
+            nc.scalar.activation(
+                out=squares[END][:, sides[a]], in_=v[END][:, sides[a]], func=ACT.Square, accum_out=end_ssq[a][:]
+            )
 
-        def end_clamp():
+        def end_square_on_vector(a):
+            nc.vector.scalar_tensor_tensor(
+                out=squares[END][:, sides[a]],
+                in0=v[END][:, sides[a]],
+                scalar=1.0,
+                in1=v[END][:, sides[a]],
+                op0=ALU.mult,
+                op1=ALU.mult,
+                accum_out=end_ssq[a][:],
+            )
+
+        def end_sum_and_clamp():
             nc.vector.tensor_scalar(
-                out=need(end_py, "c", [P, 1], F32, "end_c", 1)[:], in0=end_py["s", 0][:], scalar1=end_py["s", 1][:], scalar2=EPS2, op0=ALU.add, op1=ALU.max
+                out=ssq[:, END:], in0=end_ssq[0][:], scalar1=end_ssq[1][:], scalar2=EPS2, op0=ALU.add, op1=ALU.max
             )
 
         def end_root():
-            nc.scalar.activation(out=r[:, LASTT : LASTT + 1], in_=end_py["c"][:], func=ACT.Abs_reciprocal_sqrt)
+            nc.scalar.activation(out=r[:, END:], in_=ssq[:, END:], func=ACT.Abs_reciprocal_sqrt)
 
-        cast(0, 0, (0,), True)
-        cast(0, 0, (1,), True)
-        turn(0, 0, (0,), "py")
-        turn(0, 0, (1,), "py")
-        cast(1, 0, (0,))
-        cast(1, 1, (0,))
-        cast(1, 0, (1,))
-        cast(1, 1, (1,))
-        turn(1, 0, (0,))
-        turn(1, 0, (1,))
+
+        for g in BOTH:
+            cast(0, (g,), on_vector=True)
+        for g in BOTH:
+            turn(0, (g,), in_v_bank=True)
+        for g in BOTH:
+            cast(1, (g,))
+        for g in BOTH:
+            turn(1, (g,))
         permute_s1()
-        scale_x(0, 0, (0,))
-        scale_x(0, 0, (1,))
+        for g in BOTH:
+            scale_x(0, (g,))
         permute_w1(0)
-        quant_x(0, BOTH)
+        quant_x(0)
         stage1(0, 0)
-        cast(2, 0)
-        cast(2, 1)
+        cast(2)
         relu(0, 0)
-        cast(3, 0)
-        cast(3, 1)
-        scale_x(1, 0, (0,))
-        turn(2, 0, (0,))
-        scale_x(1, 0, (1,))
-        turn(2, 0, (1,))
+        cast(3)
+        for g in BOTH:
+            scale_x(1, (g,))
+            turn(2, (g,))
         permute_w1(1)
-        quant_x(1, BOTH)
+        quant_x(1)
         stage1(0, 1)
         stage1(1, 0)
         relu(0, 1)
         stage1(1, 1)
-        scale_x(2, 0, (0,))
+
+        scale_x(2, (0,))
         relu(1, 0)
-        scale_x(2, 0, (1,))
-        turn(3, 0, (0,))
-        turn(3, 0, (1,))
+        scale_x(2, (1,))
+        for g in BOTH:
+            turn(3, (g,))
         weave_h(0, BOTH)
         quant_x(2, (0,))
-        quant_h(0, BOTH)
+        quant_h(0)
         quant_x(2, (1,))
-        weave_g(1, 0)
+        weave_h_on_gpsimd(1, 0)
         relu(1, 1)
-        cast(4, 0)
-        weave_g(1, 1)
+        cast(LAST)
+        weave_h_on_gpsimd(1, 1)
         stage1(2, 0)
         stage2(0)
-        scale_x(3, 0, (0,))
-        scale_x(3, 0, (1,))
+        for g in BOTH:
+            scale_x(3, (g,))
         bias_v(0)
         relu(2, 0)
         stage1(2, 1)
-        turn(4, 0, BOTH)
+        turn(LAST, BOTH)
         relu(2, 1)
         square_v(0)
-        quant_x(3, BOTH)
-        quant_h(1, BOTH)
-        weave_g(2, 0)
+        quant_x(3)
+        quant_h(1)
+        weave_h_on_gpsimd(2, 0)
         stage1(3, 0, (0, 1))
         stage2(1)
         stage1(3, 0, (2, 3))
         stage1(3, 1)
         stage2(2)
-        scale_x(4, 0, BOTH)
+        scale_x(LAST, BOTH)
         bias_v(1)
         weave_h(2, (1,))
-        quant_x(4, BOTH)
-        quant_h(2, BOTH)
+        quant_x(LAST)
+        quant_h(2)
         bias_v(2)
+
         relu(3, 0)
         clamp_v(0, 1)
         relu(3, 1)
         root_v(0, 1)
-        stage1(4, 0)
-        stage1(4, 1)
+        for T in BOTH:
+            stage1(LAST, T)
         stage2(3)
         stage2(4)
         square_v(1)
         square_v(2)
-        relu(4, 0)
-        relu(4, 1)
-        weave_h(3, (0,))
-        weave_h(3, (1,))
+        for T in BOTH:
+            relu(LAST, T)
+        for T in BOTH:
+            weave_h(3, (T,))
         bias_v(3)
-        quant_h(3, BOTH)
+        quant_h(3)
         bias_v(4)
-        stage2(5, "xt")
-        stage2(6, "xt")
+        stage2(5, in_x_bank=True)
+        stage2(6, in_x_bank=True)
+
         clamp_v(1, 3)
         square_v(3)
         root_v(1, 3)
         square_v(4)
-        weave_h(4, BOTH)
-        finish_v(0, True)
-        quant_h(4, BOTH)
-        end_stage2(0)
-        end_stage2(1)
+        weave_h(LAST, BOTH)
+        finish_v(0)
+        quant_h(LAST)
+        end_stage2()
         bias_v(5)
         bias_v(6)
-        finish_v(1, False)
+        finish_v_on_scalar(1)
         clamp_v(3, 5)
-        finish_v(2, "G", 1, "hg")
+        finish_v_on_gpsimd(2)
         root_v(3, 5)
         square_v(5)
         square_v(6)
         clamp_v(5, 6)
-        end_bias(0)
-        finish_v(3, True)
-        end_bias(1)
-        finish_v(4, True)
-        end_square(1, True)
+        for a in BOTH:
+            end_bias(a)
+            finish_v(3 + a)
+        end_square_on_vector(1)
         clamp_v(6, 7)
         root_v(5, 6)
-        end_square(0, False)
+        end_square_on_scalar(0)
         root_v(6, 7)
-        finish_v(5, True)
-        end_clamp()
+        finish_v(5)
+        end_sum_and_clamp()
         end_root()
-        finish_v(6, True)
-        finish_v(7, True, 2)
+        finish_v(6)
+        finish_v(END)

@@ -21,7 +21,7 @@ HALF = 512
 NOUT = 512
 EPS2 = 1e-24
 BOTH = (0, 1)
-CHUNKS = ((0, 1), (128, 2), (384, 2), (640, 2), (896, 1))
+CHUNKS = ((0, 1), (1, 2), (3, 2), (5, 2), (7, 1))
 LAST = len(CHUNKS) - 1
 TILES = [(c, j) for c in range(len(CHUNKS)) for j in range(CHUNKS[c][1])]
 END = len(TILES) - 1
@@ -42,7 +42,7 @@ def tile_geometricmanifoldnetwork_pa_w8_kernel(
         def each_chunk(name, dtype, per_token):
             return [
                 keep.tile([P, 2, per_token * P * J], dtype, name="%s%d" % (name, c), align_bytes=64)
-                for c, (t0, J) in enumerate(CHUNKS)
+                for c, (i0, J) in enumerate(CHUNKS)
             ]
 
         def each_tile(name, dtype, columns):
@@ -63,17 +63,19 @@ def tile_geometricmanifoldnetwork_pa_w8_kernel(
         nc.vector.memset(ident[:], 0.0)
         make_identity(nc, ident[:], nomemset=True)
 
-        xbytes = [keep.tile([P, J, K], U8, name="xbytes%d" % c, align_bytes=64) for c, (t0, J) in enumerate(CHUNKS)]
+        xbytes = [keep.tile([P, J, K], U8, name="xbytes%d" % c, align_bytes=64) for c, (i0, J) in enumerate(CHUNKS)]
         w1raw = [keep.tile([P, 2, HALF], I32, name="w1raw%d" % T, align_bytes=64) for T in BOTH]
         w1 = [keep.tile([P, 2, HALF], U32, name="w1_%d" % T, align_bytes=64) for T in BOTH]
         w2 = keep.tile([P, 2, NOUT], U32, name="w2", align_bytes=64)
         b1t = keep.tile([P, 2, 4], BF16, name="b1t")
         b2t = keep.tile([P, NOUT], BF16, name="b2t")
         w1i = W1_words.rearrange("g p n t -> p g (n t)").bitcast(I32)
+        x_rows = x_bytes.rearrange("(p i) k -> p i k", i=len(TILES))
+        out_rows = out.rearrange("(p i) o -> p i o", i=len(TILES))
 
         def load_x(c):
-            t0, J = CHUNKS[c]
-            nc.sync.dma_start(out=xbytes[c][:], in_=x_bytes[t0 : t0 + P * J, :].rearrange("(j p) k -> p j k", j=J))
+            i0, J = CHUNKS[c]
+            nc.sync.dma_start(out=xbytes[c][:], in_=x_rows[:, i0 : i0 + J, :])
 
         def load_w1(T):
             nc.sync.dma_start(out=w1raw[T][:], in_=w1i[:, :, HALF * T : HALF * T + HALF])
@@ -97,7 +99,7 @@ def tile_geometricmanifoldnetwork_pa_w8_kernel(
         load_scales(s2, W2_scales)
         nc.sync.dma_start(out=b2t[:], in_=b2.partition_broadcast(P))
 
-        xv = [keep.tile([P, J, K], BF16, name="xv%d" % c, align_bytes=64) for c, (t0, J) in enumerate(CHUNKS)]
+        xv = [keep.tile([P, J, K], BF16, name="xv%d" % c, align_bytes=64) for c, (i0, J) in enumerate(CHUNKS)]
         xg, hp = each_chunk("xg", BF16, 4), each_chunk("hp", BF16, 4)
         xq, hq = each_chunk("xq", U32, 1), each_chunk("hq", U32, 1)
         xs, hs = each_chunk("xs", U8, 1), each_chunk("hs", U8, 1)
@@ -246,13 +248,16 @@ def tile_geometricmanifoldnetwork_pa_w8_kernel(
         def root_v(a, b):
             nc.scalar.activation(out=r[:, a:b], in_=over[:, a:b], func=ACT.Abs_reciprocal_sqrt, bias=EPS2)
 
-        def store(i, scaled):
-            nc.sync.dma_start(out=out[P * i : P * i + P, :], in_=scaled[:])
+        def store(i, scaled, cols=slice(0, NOUT)):
+            nc.sync.dma_start(out=out_rows[:, i, cols], in_=scaled[:, cols])
 
-        def finish_v(i):
+        def finish_v(i, parts=(slice(0, NOUT),)):
             scaled = keep.tile([P, NOUT], F32, name="o%d" % i, align_bytes=64)
-            nc.vector.tensor_scalar(out=scaled[:], in0=v[i][:], scalar1=r[:, i : i + 1], scalar2=None, op0=ALU.mult)
-            store(i, scaled)
+            for cols in parts:
+                nc.vector.tensor_scalar(
+                    out=scaled[:, cols], in0=v[i][:, cols], scalar1=r[:, i : i + 1], scalar2=None, op0=ALU.mult
+                )
+                store(i, scaled, cols)
 
         def finish_v_on_scalar(i):
             scaled = keep.tile([P, NOUT], F32, name="o%d" % i, align_bytes=64)
@@ -343,8 +348,8 @@ def tile_geometricmanifoldnetwork_pa_w8_kernel(
         relu(1, 1)
         cast(LAST)
         weave_h_on_gpsimd(1, 1)
-        stage1(2, 0)
         stage2(0)
+        stage1(2, 0)
         for g in BOTH:
             scale_x(3, (g,))
         bias_v(0)
@@ -366,55 +371,53 @@ def tile_geometricmanifoldnetwork_pa_w8_kernel(
         weave_h(2, (1,))
         quant_x(LAST)
         quant_h(2)
-        bias_v(2)
 
         relu(3, 0)
         clamp_v(0, 1)
         relu(3, 1)
         root_v(0, 1)
+        weave_h(3, (0,))
+        bias_v(2)
         for T in BOTH:
             stage1(LAST, T)
-        stage2(3)
-        stage2(4)
-        square_v(1)
-        square_v(2)
-        for T in BOTH:
+            stage2(3 + T)
+            square_v(1 + T)
             relu(LAST, T)
-        for T in BOTH:
-            weave_h(3, (T,))
+        weave_h(3, (1,))
         bias_v(3)
         quant_h(3)
         bias_v(4)
         stage2(5, in_x_bank=True)
         stage2(6, in_x_bank=True)
 
+        finish_v(0)
         clamp_v(1, 3)
         square_v(3)
         root_v(1, 3)
         square_v(4)
         weave_h(LAST, BOTH)
-        finish_v(0)
+        finish_v(1)
         quant_h(LAST)
         end_stage2()
         bias_v(5)
         bias_v(6)
-        finish_v_on_scalar(1)
         clamp_v(3, 5)
-        finish_v_on_gpsimd(2)
+        finish_v_on_scalar(2)
         root_v(3, 5)
+        finish_v_on_gpsimd(3)
         square_v(5)
         square_v(6)
         clamp_v(5, 6)
         for a in BOTH:
             end_bias(a)
-            finish_v(3 + a)
+        finish_v(4)
         end_square_on_vector(1)
-        clamp_v(6, 7)
-        root_v(5, 6)
         end_square_on_scalar(0)
+        root_v(5, 6)
+        clamp_v(6, 7)
         root_v(6, 7)
         finish_v(5)
         end_sum_and_clamp()
         end_root()
         finish_v(6)
-        finish_v(END)
+        finish_v(END, sides)

@@ -73,9 +73,15 @@ def tile_geometricmanifoldnetwork_pa_w8_kernel(
         x_rows = x_bytes.rearrange("(p i) k -> p i k", i=len(TILES))
         out_rows = out.rearrange("(p i) o -> p i o", i=len(TILES))
 
+        x_pairs = x_bytes.rearrange("(i a s) k -> a i s k", i=2, s=len(TILES))
+        out_pairs = out.rearrange("(a i s) o -> a i s o", i=2, s=len(TILES))
+
         def load_x(c):
             i0, J = CHUNKS[c]
-            nc.sync.dma_start(out=xbytes[c][:], in_=x_rows[:, i0 : i0 + J, :])
+            if J == 1:
+                nc.sync.dma_start(out=xbytes[c][:, 0, :], in_=x_pairs[:, :, i0, :])
+            else:
+                nc.sync.dma_start(out=xbytes[c][:], in_=x_rows[:, i0 : i0 + J, :])
 
         def load_w1(T):
             nc.sync.dma_start(out=w1raw[T][:], in_=w1i[:, :, HALF * T : HALF * T + HALF])
@@ -131,23 +137,27 @@ def tile_geometricmanifoldnetwork_pa_w8_kernel(
         def turn(c, gs, in_v_bank=False):
             J = CHUNKS[c][1]
             pool, name = (psy, "py") if in_v_bank else (psx, "xt")
-            xt[c, gs] = pool.tile([P, len(gs), P * J, 2], F32, name=name)
+            xt[c, gs] = pool.tile([P, len(gs), P // 2, J, 2, 2], F32, name=name)
             for a, g in enumerate(gs):
                 for j in range(J):
                     words = xv[c][:, j, :].bitcast(F32)
                     for u in range(2):
                         nc.tensor.transpose(
-                            xt[c, gs][:, a, P * j : P * j + P, u], words[:, 256 * g + u : 256 * (g + 1) : 2], ident[:]
+                            xt[c, gs][:, a, :, j, u, :], words[:, 256 * g + u : 256 * (g + 1) : 2], ident[:]
                         )
 
         def scale_x(c, gs):
             part = slice(gs[0], gs[-1] + 1)
-            nc.vector.tensor_tensor(
-                out=xg[c][:, part, :].rearrange("p g (n t) -> p g n t", t=4),
-                in0=xt[c, gs][:].bitcast(BF16),
-                in1=xsc[:, part, :].unsqueeze(2).to_broadcast([P, len(gs), P * CHUNKS[c][1], 4]),
-                op=ALU.mult,
-            )
+            n = P // 2 * CHUNKS[c][1]
+            turned = xt[c, gs][:].bitcast(BF16).rearrange("p g a j u w -> p g (a j) u w")
+            scales = xsc[:, part, :].rearrange("p g (u e) -> p g u e", u=2).unsqueeze(2)
+            for i in range(2):
+                nc.vector.tensor_tensor(
+                    out=xg[c][:, part, 4 * n * i : 4 * n * (i + 1)].rearrange("p g (n u e) -> p g n u e", u=2, e=2),
+                    in0=turned[:, :, :, :, 2 * i : 2 * i + 2],
+                    in1=scales.to_broadcast([P, len(gs), n, 2, 2]),
+                    op=ALU.mult,
+                )
 
         def quantise(codes, scales, values, gs):
             part = slice(gs[0], gs[-1] + 1)
@@ -249,7 +259,10 @@ def tile_geometricmanifoldnetwork_pa_w8_kernel(
             nc.scalar.activation(out=r[:, a:b], in_=over[:, a:b], func=ACT.Abs_reciprocal_sqrt, bias=EPS2)
 
         def store(i, scaled, cols=slice(0, NOUT)):
-            nc.sync.dma_start(out=out_rows[:, i, cols], in_=scaled[:, cols])
+            c, j = TILES[i]
+            i0, J = CHUNKS[c]
+            rows = out_rows[:, i, cols] if J == 1 else out_pairs[:, j, i0 : i0 + J, cols]
+            nc.sync.dma_start(out=rows, in_=scaled[:, cols])
 
         def finish_v(i, parts=(slice(0, NOUT),)):
             scaled = keep.tile([P, NOUT], F32, name="o%d" % i, align_bytes=64)

@@ -25,7 +25,6 @@ CHUNKS = ((0, 1), (1, 2), (3, 2), (5, 2), (7, 1))
 LAST = len(CHUNKS) - 1
 TILES = [(c, j) for c in range(len(CHUNKS)) for j in range(CHUNKS[c][1])]
 END = len(TILES) - 1
-PAIRED = ((0, 0), (0, 1), (2, 1))
 
 
 def tile_geometricmanifoldnetwork_pa_w8_kernel(
@@ -34,9 +33,7 @@ def tile_geometricmanifoldnetwork_pa_w8_kernel(
     nc = tc.nc
     with ExitStack() as ctx:
         keep = ctx.enter_context(tc.tile_pool(name="keep", bufs=1))
-        psx = ctx.enter_context(tc.psum_pool(name="psx", bufs=2))
-        psh = ctx.enter_context(tc.psum_pool(name="psh", bufs=4))
-        psy = ctx.enter_context(tc.psum_pool(name="psy", bufs=2))
+        psum = ctx.enter_context(tc.psum_pool(name="psum", bufs=1))
         ctx.enter_context(tc.manual_schedule())
 
         def each_chunk(name, dtype, per_token):
@@ -53,6 +50,7 @@ def tile_geometricmanifoldnetwork_pa_w8_kernel(
         s2 = keep.tile([P, NOUT], U8, name="s2", align_bytes=64)
         xsc = keep.tile([P, 2, 4], F32, name="xsc")
         nc.scalar.dma_start(out=xsc[:], in_=x_scale.rearrange("o (g p t) -> p (o g) t", g=2, t=4))
+
         one = keep.tile([P, 2], F32, name="one")
         nc.vector.memset(one[:], 1.0)
         warm = keep.tile([P, 2], F32, name="warm")
@@ -64,7 +62,7 @@ def tile_geometricmanifoldnetwork_pa_w8_kernel(
         make_identity(nc, ident[:], nomemset=True)
 
         xbytes = [keep.tile([P, J, K], U8, name="xbytes%d" % c, align_bytes=64) for c, (i0, J) in enumerate(CHUNKS)]
-        w1raw = [keep.tile([P, 2, HALF], I32, name="w1raw%d" % T, align_bytes=64) for T in BOTH]
+        w1raw = [keep.tile([P, 2, HALF], U32, name="w1raw%d" % T, align_bytes=64) for T in BOTH]
         w1 = [keep.tile([P, 2, HALF], U32, name="w1_%d" % T, align_bytes=64) for T in BOTH]
         w2 = keep.tile([P, 2, NOUT], U32, name="w2", align_bytes=64)
         b1t = keep.tile([P, 2, 4], BF16, name="b1t")
@@ -73,18 +71,14 @@ def tile_geometricmanifoldnetwork_pa_w8_kernel(
         x_rows = x_bytes.rearrange("(p i) k -> p i k", i=len(TILES))
         out_rows = out.rearrange("(p i) o -> p i o", i=len(TILES))
 
-        x_pairs = x_bytes.rearrange("(i a s) k -> a i s k", i=2, s=len(TILES))
         out_pairs = out.rearrange("(a i s) o -> a i s o", i=2, s=len(TILES))
 
         def load_x(c):
             i0, J = CHUNKS[c]
-            if J == 1:
-                nc.sync.dma_start(out=xbytes[c][:, 0, :], in_=x_pairs[:, :, i0, :])
-            else:
-                nc.sync.dma_start(out=xbytes[c][:], in_=x_rows[:, i0 : i0 + J, :])
+            nc.sync.dma_start(out=xbytes[c][:], in_=x_rows[:, i0 : i0 + J, :])
 
         def load_w1(T):
-            nc.sync.dma_start(out=w1raw[T][:], in_=w1i[:, :, HALF * T : HALF * T + HALF])
+            nc.sync.dma_start(out=w1raw[T][:].bitcast(I32), in_=w1i[:, :, HALF * T : HALF * T + HALF])
 
         def load_scales(dst, src):
             for Q in range(4):
@@ -92,20 +86,15 @@ def tile_geometricmanifoldnetwork_pa_w8_kernel(
                     out=dst[32 * Q : 32 * Q + 8, :].bitcast(I32), in_=src[:, 4 * Q : 4 * Q + 4, :].bitcast(I32)
                 )
 
-        load_x(0)
-        load_scales(s1raw, W1_scales)
-        load_x(1)
-        load_w1(0)
-        nc.scalar.dma_start(out=b1t[:], in_=b1.rearrange("(g p t) -> p g t", g=2, t=4))
-        load_x(2)
-        load_w1(1)
-        load_x(3)
-        load_x(4)
-        nc.sync.dma_start(out=w2[:].bitcast(I32), in_=W2_words.rearrange("g p n t -> p g (n t)").bitcast(I32))
-        load_scales(s2, W2_scales)
-        nc.sync.dma_start(out=b2t[:], in_=b2.partition_broadcast(P))
+        def load_b1():
+            nc.scalar.dma_start(out=b1t[:], in_=b1.rearrange("(g p t) -> p g t", g=2, t=4))
 
-        xv = [keep.tile([P, J, K], BF16, name="xv%d" % c, align_bytes=64) for c, (i0, J) in enumerate(CHUNKS)]
+        def load_w2():
+            nc.sync.dma_start(out=w2[:].bitcast(I32), in_=W2_words.rearrange("g p n t -> p g (n t)").bitcast(I32))
+            load_scales(s2, W2_scales)
+            nc.sync.dma_start(out=b2t[:], in_=b2.partition_broadcast(P))
+
+        xv = {}
         xg, hp = each_chunk("xg", BF16, 4), each_chunk("hp", BF16, 4)
         xq, hq = each_chunk("xq", U32, 1), each_chunk("hq", U32, 1)
         xs, hs = each_chunk("xs", U8, 1), each_chunk("hs", U8, 1)
@@ -114,12 +103,26 @@ def tile_geometricmanifoldnetwork_pa_w8_kernel(
         over = keep.tile([P, len(TILES)], F32, name="over")
         r = keep.tile([P, len(TILES)], F32, name="r")
         end_ssq = [keep.tile([P, 1], F32, name="end_ssq%d" % a) for a in BOTH]
-        xt, ph, hg, py = {}, {}, {}, {}
+        xt, xp, ph, hbank, hg, py = {}, {}, {}, {}, {}, {}
+
+        free_banks = ["bank%d" % b for b in range(8)]
+        held = {}
+
+        def take_bank(key, shape, after=None):
+            held[key] = held[after] if after else free_banks[0]
+            if not after:
+                free_banks.remove(held[key])
+            return psum.tile(shape, F32, name=held[key])
+
+        def give_bank(key):
+            free_banks.append(held[key])
+
+        sides = [slice(NOUT // 2 * a, NOUT // 2 * (a + 1)) for a in BOTH]
 
         def permute_w1(T):
             nc.vector.tensor_copy(
                 out=w1[T][:].bitcast(I32).rearrange("p g (t c i) -> p g c t i", t=4, i=2),
-                in_=w1raw[T][:].rearrange("p g (c i t) -> p g c t i", t=4, i=2),
+                in_=w1raw[T][:].bitcast(I32).rearrange("p g (c i t) -> p g c t i", t=4, i=2),
             )
 
         def permute_s1():
@@ -130,34 +133,42 @@ def tile_geometricmanifoldnetwork_pa_w8_kernel(
 
         def cast(c, gs=BOTH, on_vector=False):
             copy = nc.vector.tensor_copy if on_vector else nc.scalar.copy
+            if c not in xv:
+                xv[c] = keep.tile([P, CHUNKS[c][1], K], BF16, name="xv%d" % c, align_bytes=64)
             cols = slice(HALF * gs[0], HALF * gs[-1] + HALF)
             for j in range(CHUNKS[c][1]):
                 copy(out=xv[c][:, j, cols], in_=xbytes[c][:, j, cols].bitcast(FP8))
 
-        def turn(c, gs, in_v_bank=False):
+        def turn(c, gs):
             J = CHUNKS[c][1]
-            pool, name = (psy, "py") if in_v_bank else (psx, "xt")
-            xt[c, gs] = pool.tile([P, len(gs), P // 2, J, 2, 2], F32, name=name)
+            xt[c, gs] = take_bank(("x", c, gs), [P, len(gs), P // 2, 2, 2] if J == 1 else [P, len(gs), P // 2, J, 2, 2])
             for a, g in enumerate(gs):
                 for j in range(J):
                     words = xv[c][:, j, :].bitcast(F32)
                     for u in range(2):
-                        nc.tensor.transpose(
-                            xt[c, gs][:, a, :, j, u, :], words[:, 256 * g + u : 256 * (g + 1) : 2], ident[:]
-                        )
+                        dst = xt[c, gs][:, a, :, :, u] if J == 1 else xt[c, gs][:, a, :, j, u, :]
+                        nc.tensor.transpose(dst, words[:, 256 * g + u : 256 * (g + 1) : 2], ident[:])
 
         def scale_x(c, gs):
             part = slice(gs[0], gs[-1] + 1)
-            n = P // 2 * CHUNKS[c][1]
-            turned = xt[c, gs][:].bitcast(BF16).rearrange("p g a j u w -> p g (a j) u w")
-            scales = xsc[:, part, :].rearrange("p g (u e) -> p g u e", u=2).unsqueeze(2)
-            for i in range(2):
+            if CHUNKS[c][1] == 1:
                 nc.vector.tensor_tensor(
-                    out=xg[c][:, part, 4 * n * i : 4 * n * (i + 1)].rearrange("p g (n u e) -> p g n u e", u=2, e=2),
-                    in0=turned[:, :, :, :, 2 * i : 2 * i + 2],
-                    in1=scales.to_broadcast([P, len(gs), n, 2, 2]),
+                    out=xg[c][:, part, :].rearrange("p g (n t) -> p g n t", t=4),
+                    in0=xt[c, gs][:].rearrange("p g a i u -> p g (a i) u").bitcast(BF16),
+                    in1=xsc[:, part, :].unsqueeze(2).to_broadcast([P, len(gs), P, 4]),
                     op=ALU.mult,
                 )
+            else:
+                turned = xt[c, gs][:].bitcast(BF16).rearrange("p g a j u w -> p g (a j) u w")
+                scales = xsc[:, part, :].rearrange("p g (u e) -> p g u e", u=2).unsqueeze(2)
+                for i in range(2):
+                    nc.vector.tensor_tensor(
+                        out=xg[c][:, part, HALF * i : HALF * (i + 1)].rearrange("p g (n u e) -> p g n u e", u=2, e=2),
+                        in0=turned[:, :, :, :, 2 * i : 2 * i + 2],
+                        in1=scales.to_broadcast([P, len(gs), P, 2, 2]),
+                        op=ALU.mult,
+                    )
+            give_bank(("x", c, gs))
 
         def quantise(codes, scales, values, gs):
             part = slice(gs[0], gs[-1] + 1)
@@ -175,12 +186,12 @@ def tile_geometricmanifoldnetwork_pa_w8_kernel(
             per_bank = HALF // n
             for t in ts:
                 if t % per_bank == 0:
-                    bank = psh.tile([P, per_bank, n], F32, name="ph")
-                ph[c, T, t] = bank[:, t % per_bank, :]
+                    hbank[c, T] = take_bank(("h", c, T, t // per_bank), [P, per_bank, n])
+                ph[c, T, t] = hbank[c, T][:, t % per_bank, :]
                 for g in BOTH:
                     nc.tensor.matmul_mx(
                         out=ph[c, T, t],
-                        lhsT=w1[T][:, g, P * t : P * t + P].bitcast(FP8X4),
+                        lhsT=(late_w1[g] if T else w1[0][:, g, :])[:, P * t : P * t + P].bitcast(FP8X4),
                         lhsT_scale=s1[4 * g :, HALF * T + P * t : HALF * T + P * t + P],
                         rhs=xq[c][:, g, :].bitcast(FP8X4),
                         rhs_scale=xs[c][:, g, :],
@@ -188,45 +199,55 @@ def tile_geometricmanifoldnetwork_pa_w8_kernel(
                         stop=(g == 1),
                     )
 
-        def relu(c, T):
+        def relu(c, T, ts=range(4)):
             n = P * CHUNKS[c][1]
-            for t in range(4):
-                if (c, T) in PAIRED:
-                    dst = hp[c][:, T, 2 * n * (t // 2) + t % 2 : 2 * n * (t // 2 + 1) : 2]
-                else:
-                    dst = hp[c][:, T, n * t : n * t + n]
-                nc.scalar.activation(out=dst, in_=ph[c, T, t], func=ACT.Relu, bias=b1t[:, T, t : t + 1])
+            for t in ts:
+                nc.scalar.activation(
+                    out=hp[c][:, T, n * t : n * t + n], in_=ph[c, T, t], func=ACT.Relu, bias=b1t[:, T, t : t + 1]
+                )
+                if (t + 1) * n % HALF == 0:
+                    give_bank(("h", c, T, t * n // HALF))
 
-        def woven(c):
+        def relu_in_pairs(c, T, ts=range(4)):
+            n = P * CHUNKS[c][1]
+            for t in ts:
+                dst = hp[c][:, T, 2 * n * (t // 2) + t % 2 : 2 * n * (t // 2 + 1) : 2]
+                nc.scalar.activation(out=dst, in_=ph[c, T, t], func=ACT.Relu, bias=b1t[:, T, t : t + 1])
+                if (t + 1) * n % HALF == 0:
+                    give_bank(("h", c, T, t * n // HALF))
+
+        def woven(c, name=None):
             if c not in hg:
-                hg[c] = keep.tile([P, 2, 4 * P * CHUNKS[c][1]], BF16, name="hg%d" % max(c, 2), align_bytes=64)
+                hg[c] = keep.tile([P, 2, 4 * P * CHUNKS[c][1]], BF16, name=name or "hg%d" % c, align_bytes=64)
             return hg[c]
 
-        def weave_h(c, Ts):
+        def weave_h(c, Ts, name=None):
             part = slice(Ts[0], Ts[-1] + 1)
-            if (c, Ts[0]) in PAIRED:
-                nc.vector.tensor_copy(
-                    out=woven(c)[:, part, :].bitcast(F32).rearrange("p T (n u) -> p T n u", u=2),
-                    in_=hp[c][:, part, :].bitcast(F32).rearrange("p T (u n) -> p T n u", u=2),
-                )
-            else:
-                nc.vector.tensor_copy(
-                    out=woven(c)[:, part, :].rearrange("p T (c i t) -> p T c t i", i=4, t=4),
-                    in_=hp[c][:, part, :].rearrange("p T (t c i) -> p T c t i", i=4, t=4),
-                )
+            nc.vector.tensor_copy(
+                out=woven(c, name)[:, part, :].rearrange("p T (c i t) -> p T c t i", i=4, t=4),
+                in_=hp[c][:, part, :].rearrange("p T (t c i) -> p T c t i", i=4, t=4),
+            )
 
-        def weave_h_on_gpsimd(c, T):
+        def weave_pairs(c, Ts, name=None):
+            part = slice(Ts[0], Ts[-1] + 1)
+            nc.vector.tensor_copy(
+                out=woven(c, name)[:, part, :].bitcast(F32).rearrange("p T (n u) -> p T n u", u=2),
+                in_=hp[c][:, part, :].bitcast(F32).rearrange("p T (u n) -> p T n u", u=2),
+            )
+
+        def weave_h_on_gpsimd(c, Ts, name=None):
+            part = slice(Ts[0], Ts[-1] + 1)
             nc.gpsimd.tensor_scalar(
-                out=woven(c)[:, T, :].rearrange("p (n t) -> p n t", t=4),
-                in0=hp[c][:, T, :].rearrange("p (t n) -> p n t", t=4),
+                out=woven(c, name)[:, part, :].rearrange("p T (n t) -> p T n t", t=4),
+                in0=hp[c][:, part, :].rearrange("p T (t n) -> p T n t", t=4),
                 scalar1=1.0,
                 scalar2=0.0,
                 op0=ALU.mult,
                 op1=ALU.add,
             )
 
-        def quant_h(c):
-            quantise(hq[c], hs[c], hg[c], BOTH)
+        def quant_h(c, Ts=BOTH):
+            quantise(hq[c], hs[c], hg[c], Ts)
 
         def stage2_pass(dst, i, T, cols):
             c, j = TILES[i]
@@ -240,14 +261,16 @@ def tile_geometricmanifoldnetwork_pa_w8_kernel(
                 stop=(T == 1),
             )
 
-        def stage2(i, in_x_bank=False):
-            pool, name = (psx, "xt") if in_x_bank else (psy, "py")
-            py[i] = pool.tile([P, NOUT], F32, name=name)
-            for T in BOTH:
+        def stage2(i, Ts=BOTH, after=None):
+            for T in Ts:
+                if T == 0:
+                    py[i] = take_bank(("y", i), [P, NOUT], after)
                 stage2_pass(py[i][:], i, T, slice(0, NOUT))
 
-        def bias_v(i):
+        def bias_v(i, keep_bank=False):
             nc.vector.tensor_tensor(out=v[i][:], in0=py[i][:], in1=b2t[:], op=ALU.add)
+            if not keep_bank:
+                give_bank(("y", i))
 
         def square_v(i):
             nc.scalar.activation(out=squares[i][:], in_=v[i][:], func=ACT.Square, accum_out=ssq[:, i : i + 1])
@@ -277,24 +300,23 @@ def tile_geometricmanifoldnetwork_pa_w8_kernel(
             nc.scalar.activation(out=scaled[:], in_=v[i][:], func=ACT.Copy, scale=r[:, i : i + 1])
             store(i, scaled)
 
-        def finish_v_on_gpsimd(i):
-            scaled = keep.tile([P, NOUT], F32, name="hg%d" % LAST, align_bytes=64)
+        def finish_v_on_gpsimd(i, name=None):
+            scaled = keep.tile([P, NOUT], F32, name=name or "o%d" % i, align_bytes=64)
             nc.gpsimd.tensor_scalar(
                 out=scaled[:], in0=v[i][:], scalar1=r[:, i : i + 1], scalar2=0.0, op0=ALU.mult, op1=ALU.add
             )
             store(i, scaled)
 
-        sides = [slice(NOUT // 2 * a, NOUT // 2 * (a + 1)) for a in BOTH]
-
-        def end_stage2():
-            for T in BOTH:
+        def end_stage2(Ts=BOTH):
+            for T in Ts:
                 for a in BOTH:
                     if T == 0:
-                        py[END, a] = psy.tile([P, NOUT // 2], F32, name="py")
+                        py[END, a] = take_bank(("y", END, a), [P, NOUT // 2])
                     stage2_pass(py[END, a][:], END, T, sides[a])
 
         def end_bias(a):
             nc.vector.tensor_tensor(out=v[END][:, sides[a]], in0=py[END, a][:], in1=b2t[:, sides[a]], op=ALU.add)
+            give_bank(("y", END, a))
 
         def end_square_on_scalar(a):
             nc.scalar.activation(
@@ -320,117 +342,148 @@ def tile_geometricmanifoldnetwork_pa_w8_kernel(
         def end_root():
             nc.scalar.activation(out=r[:, END:], in_=ssq[:, END:], func=ACT.Abs_reciprocal_sqrt)
 
+        def permute_w1_half_on_gpsimd(g):
+            nc.gpsimd.tensor_copy(
+                out=late_w1[g][:].rearrange("p (t m) -> p t m", t=4), in_=late[g][:].rearrange("p (m t) -> p t m", t=4)
+            )
 
-        for g in BOTH:
-            cast(0, (g,), on_vector=True)
-        for g in BOTH:
-            turn(0, (g,), in_v_bank=True)
-        for g in BOTH:
-            cast(1, (g,))
-        for g in BOTH:
-            turn(1, (g,))
+        def permute_w1_half_on_scalar(g):
+            nc.scalar.copy(
+                out=late_w1[g][:].rearrange("p (t c i) -> p c t i", t=4, i=2),
+                in_=late[g][:].rearrange("p (c i t) -> p c t i", t=4, i=2),
+            )
+
+
+        late = [keep.tile([P, HALF], U32, name="late%d" % g, align_bytes=64) for g in BOTH]
+        late_w1 = [keep.tile([P, HALF], U32, name="late_w1_%d" % g, align_bytes=64) for g in BOTH]
+        load_x(0)
+        load_scales(s1raw, W1_scales)
+        load_x(1)
+        load_w1(0)
+        load_b1()
+        nc.sync.dma_start(out=late[0][:].bitcast(I32), in_=w1i[:, 0, HALF:])
+        load_x(2)
+        nc.sync.dma_start(out=late[1][:].bitcast(I32), in_=w1i[:, 1, HALF:])
+        load_x(3)
+        load_x(4)
+        load_w2()
+
+        cast(0, (0,), on_vector=True)
+        cast(0, (1,), on_vector=True)
+        turn(0, (0,))
         permute_s1()
-        for g in BOTH:
-            scale_x(0, (g,))
+        turn(0, (1,))
+        cast(1, (0,))
+        turn(1, (0,))
+        scale_x(0, (0,))
+        cast(1, (1,))
+        scale_x(0, (1,))
         permute_w1(0)
-        quant_x(0)
+        turn(1, (1,))
+        permute_w1_half_on_scalar(0)
+        quant_x(0, BOTH)
         stage1(0, 0)
-        cast(2)
-        relu(0, 0)
-        cast(3)
-        for g in BOTH:
-            scale_x(1, (g,))
-            turn(2, (g,))
-        permute_w1(1)
-        quant_x(1)
+        cast(2, (0,))
+        permute_w1_half_on_gpsimd(1)
+        scale_x(1, (0,))
+        cast(2, (1,))
+        turn(2, (0,))
+        turn(2, (1,))
+        scale_x(1, (1,))
+        quant_x(1, (0,))
         stage1(0, 1)
+        relu(0, 0)
+        cast(3, (0,))
+        quant_x(1, (1,))
         stage1(1, 0)
-        relu(0, 1)
-        stage1(1, 1)
-
+        weave_h_on_gpsimd(0, (0,), "xg1")
+        cast(3, (1,))
         scale_x(2, (0,))
-        relu(1, 0)
+        stage1(1, 1)
+        relu_in_pairs(0, 1)
         scale_x(2, (1,))
-        for g in BOTH:
-            turn(3, (g,))
-        weave_h(0, BOTH)
+        weave_pairs(0, (1,))
+        turn(3, (0,))
         quant_x(2, (0,))
-        quant_h(0)
+        quant_h(0, BOTH)
+        turn(3, (1,))
         quant_x(2, (1,))
-        weave_h_on_gpsimd(1, 0)
-        relu(1, 1)
-        cast(LAST)
-        weave_h_on_gpsimd(1, 1)
-        stage2(0)
+        relu(1, 0)
+        stage2(0, BOTH)
+        weave_h_on_gpsimd(1, (0,), "xg1")
         stage1(2, 0)
-        for g in BOTH:
-            scale_x(3, (g,))
-        bias_v(0)
-        relu(2, 0)
+        relu(1, 1)
+        cast(4, BOTH)
+        scale_x(3, (0,))
+        weave_h_on_gpsimd(1, (1,))
         stage1(2, 1)
-        turn(LAST, BOTH)
-        relu(2, 1)
-        square_v(0)
-        quant_x(3)
-        quant_h(1)
-        weave_h_on_gpsimd(2, 0)
+        scale_x(3, (1,))
+        relu(2, 0)
+        turn(4, BOTH)
+        bias_v(0)
+        quant_x(3, BOTH)
+        quant_h(1, BOTH)
         stage1(3, 0, (0, 1))
-        stage2(1)
+        stage2(1, BOTH)
+        relu_in_pairs(2, 1)
+        square_v(0)
+        weave_h_on_gpsimd(2, (0,), "xg1")
         stage1(3, 0, (2, 3))
+        scale_x(4, BOTH)
         stage1(3, 1)
-        stage2(2)
-        scale_x(LAST, BOTH)
         bias_v(1)
-        weave_h(2, (1,))
-        quant_x(LAST)
-        quant_h(2)
-
+        weave_pairs(2, (1,))
         relu(3, 0)
         clamp_v(0, 1)
+        quant_x(4, BOTH)
+        stage2(2, BOTH)
+        quant_h(2, BOTH)
+        stage1(4, 0)
+        weave_h(3, (0,))
         relu(3, 1)
         root_v(0, 1)
-        weave_h(3, (0,))
+        square_v(1)
+        stage2(3, BOTH)
+        stage1(4, 1)
         bias_v(2)
-        for T in BOTH:
-            stage1(LAST, T)
-            stage2(3 + T)
-            square_v(1 + T)
-            relu(LAST, T)
         weave_h(3, (1,))
+        relu(4, 0)
+        square_v(2)
+        stage2(4, BOTH)
         bias_v(3)
-        quant_h(3)
-        bias_v(4)
-        stage2(5, in_x_bank=True)
-        stage2(6, in_x_bank=True)
-
-        finish_v(0)
+        quant_h(3, BOTH)
+        relu(4, 1)
         clamp_v(1, 3)
         square_v(3)
+        stage2(5, BOTH)
         root_v(1, 3)
+        bias_v(4)
+        finish_v(0)
+        stage2(6, BOTH)
+        weave_h(4, BOTH)
         square_v(4)
-        weave_h(LAST, BOTH)
         finish_v(1)
-        quant_h(LAST)
-        end_stage2()
-        bias_v(5)
-        bias_v(6)
         clamp_v(3, 5)
         finish_v_on_scalar(2)
+        quant_h(4, BOTH)
         root_v(3, 5)
-        finish_v_on_gpsimd(3)
+        end_stage2(BOTH)
+        bias_v(5)
+        finish_v_on_gpsimd(3, "hg4")
         square_v(5)
+        bias_v(6)
+        end_bias(0)
         square_v(6)
-        clamp_v(5, 6)
-        for a in BOTH:
-            end_bias(a)
+        end_bias(1)
         finish_v(4)
+        clamp_v(5, 6)
         end_square_on_vector(1)
         end_square_on_scalar(0)
         root_v(5, 6)
         clamp_v(6, 7)
-        root_v(6, 7)
         finish_v(5)
+        root_v(6, 7)
         end_sum_and_clamp()
-        end_root()
         finish_v(6)
+        end_root()
         finish_v(END, sides)

@@ -25,6 +25,7 @@ CHUNKS = ((0, 1), (1, 2), (3, 2), (5, 2), (7, 1))
 LAST = len(CHUNKS) - 1
 TILES = [(c, j) for c in range(len(CHUNKS)) for j in range(CHUNKS[c][1])]
 END = len(TILES) - 1
+STEPPED = (LAST,)
 
 
 def tile_geometricmanifoldnetwork_pa_w8_kernel(
@@ -71,11 +72,15 @@ def tile_geometricmanifoldnetwork_pa_w8_kernel(
         x_rows = x_bytes.rearrange("(p i) k -> p i k", i=len(TILES))
         out_rows = out.rearrange("(p i) o -> p i o", i=len(TILES))
 
+        x_pairs = x_bytes.rearrange("(i a s) k -> a i s k", i=2, s=len(TILES))
         out_pairs = out.rearrange("(a i s) o -> a i s o", i=2, s=len(TILES))
 
         def load_x(c):
             i0, J = CHUNKS[c]
-            nc.sync.dma_start(out=xbytes[c][:], in_=x_rows[:, i0 : i0 + J, :])
+            if J == 1 and c not in STEPPED:
+                nc.sync.dma_start(out=xbytes[c][:, 0, :], in_=x_pairs[:, :, i0, :])
+            else:
+                nc.sync.dma_start(out=xbytes[c][:], in_=x_rows[:, i0 : i0 + J, :])
 
         def load_w1(T):
             nc.sync.dma_start(out=w1raw[T][:].bitcast(I32), in_=w1i[:, :, HALF * T : HALF * T + HALF])
@@ -141,33 +146,33 @@ def tile_geometricmanifoldnetwork_pa_w8_kernel(
 
         def turn(c, gs):
             J = CHUNKS[c][1]
-            xt[c, gs] = take_bank(("x", c, gs), [P, len(gs), P // 2, 2, 2] if J == 1 else [P, len(gs), P // 2, J, 2, 2])
+            xt[c, gs] = take_bank(("x", c, gs), [P, len(gs), P // 2, J, 2, 2])
             for a, g in enumerate(gs):
                 for j in range(J):
                     words = xv[c][:, j, :].bitcast(F32)
                     for u in range(2):
-                        dst = xt[c, gs][:, a, :, :, u] if J == 1 else xt[c, gs][:, a, :, j, u, :]
+                        dst = xt[c, gs][:, a, :, j, :, u] if c in STEPPED else xt[c, gs][:, a, :, j, u, :]
                         nc.tensor.transpose(dst, words[:, 256 * g + u : 256 * (g + 1) : 2], ident[:])
 
         def scale_x(c, gs):
             part = slice(gs[0], gs[-1] + 1)
-            if CHUNKS[c][1] == 1:
+            J = CHUNKS[c][1]
+            if c in STEPPED:
                 nc.vector.tensor_tensor(
                     out=xg[c][:, part, :].rearrange("p g (n t) -> p g n t", t=4),
-                    in0=xt[c, gs][:].rearrange("p g a i u -> p g (a i) u").bitcast(BF16),
+                    in0=xt[c, gs][:].rearrange("p g a j i u -> p g (a j i) u").bitcast(BF16),
                     in1=xsc[:, part, :].unsqueeze(2).to_broadcast([P, len(gs), P, 4]),
                     op=ALU.mult,
                 )
             else:
-                turned = xt[c, gs][:].bitcast(BF16).rearrange("p g a j u w -> p g (a j) u w")
-                scales = xsc[:, part, :].rearrange("p g (u e) -> p g u e", u=2).unsqueeze(2)
-                for i in range(2):
-                    nc.vector.tensor_tensor(
-                        out=xg[c][:, part, HALF * i : HALF * (i + 1)].rearrange("p g (n u e) -> p g n u e", u=2, e=2),
-                        in0=turned[:, :, :, :, 2 * i : 2 * i + 2],
-                        in1=scales.to_broadcast([P, len(gs), P, 2, 2]),
-                        op=ALU.mult,
-                    )
+                g = gs[0]
+                scales = xsc[:, g, :].rearrange("p (u e) -> p u e", u=2).unsqueeze(1).unsqueeze(1)
+                nc.vector.tensor_tensor(
+                    out=xg[c][:, g, :].rearrange("p (i n u e) -> p i n u e", i=2, u=2, e=2),
+                    in0=xt[c, gs][:, 0].bitcast(BF16).rearrange("p a j u (i e) -> p i (a j) u e", e=2),
+                    in1=scales.to_broadcast([P, 2, P // 2 * J, 2, 2]),
+                    op=ALU.mult,
+                )
             give_bank(("x", c, gs))
 
         def quantise(codes, scales, values, gs):
@@ -353,6 +358,11 @@ def tile_geometricmanifoldnetwork_pa_w8_kernel(
                 in_=late[g][:].rearrange("p (c i t) -> p c t i", t=4, i=2),
             )
 
+        def cast_part(c, j, g, on_gpsimd=False):
+            copy = nc.gpsimd.tensor_copy if on_gpsimd else nc.scalar.copy
+            cols = slice(HALF * g, HALF * g + HALF)
+            copy(out=xv[c][:, j, cols], in_=xbytes[c][:, j, cols].bitcast(FP8))
+
 
         late = [keep.tile([P, HALF], U32, name="late%d" % g, align_bytes=64) for g in BOTH]
         late_w1 = [keep.tile([P, HALF], U32, name="late_w1_%d" % g, align_bytes=64) for g in BOTH]
@@ -385,89 +395,90 @@ def tile_geometricmanifoldnetwork_pa_w8_kernel(
         stage1(0, 0)
         cast(2, (0,))
         permute_w1_half_on_gpsimd(1)
-        scale_x(1, (0,))
         cast(2, (1,))
+        scale_x(1, (0,))
         turn(2, (0,))
         turn(2, (1,))
         scale_x(1, (1,))
         quant_x(1, (0,))
-        stage1(0, 1)
         relu(0, 0)
         cast(3, (0,))
+        stage1(0, 1)
         quant_x(1, (1,))
-        stage1(1, 0)
         weave_h_on_gpsimd(0, (0,), "xg1")
-        cast(3, (1,))
+        cast_part(3, 0, 1)
+        stage1(1, 0)
         scale_x(2, (0,))
+        cast_part(3, 1, 1, on_gpsimd=True)
         stage1(1, 1)
         relu_in_pairs(0, 1)
         scale_x(2, (1,))
-        weave_pairs(0, (1,))
-        turn(3, (0,))
         quant_x(2, (0,))
-        quant_h(0, BOTH)
-        turn(3, (1,))
+        turn(3, (0,))
+        weave_pairs(0, (1,))
         quant_x(2, (1,))
         relu(1, 0)
+        quant_h(0, BOTH)
+        turn(3, (1,))
+        weave_h_on_gpsimd(1, (0,), "xg2")
         stage2(0, BOTH)
-        weave_h_on_gpsimd(1, (0,), "xg1")
-        stage1(2, 0)
         relu(1, 1)
         cast(4, BOTH)
+        stage1(2, 0)
         scale_x(3, (0,))
         weave_h_on_gpsimd(1, (1,))
         stage1(2, 1)
         scale_x(3, (1,))
         relu(2, 0)
-        turn(4, BOTH)
         bias_v(0)
+        turn(4, BOTH)
         quant_x(3, BOTH)
         quant_h(1, BOTH)
         stage1(3, 0, (0, 1))
+        weave_h_on_gpsimd(2, (0,), "xg3")
         stage2(1, BOTH)
         relu_in_pairs(2, 1)
         square_v(0)
-        weave_h_on_gpsimd(2, (0,), "xg1")
         stage1(3, 0, (2, 3))
         scale_x(4, BOTH)
         stage1(3, 1)
         bias_v(1)
         weave_pairs(2, (1,))
+        quant_x(4, BOTH)
         relu(3, 0)
         clamp_v(0, 1)
-        quant_x(4, BOTH)
-        stage2(2, BOTH)
         quant_h(2, BOTH)
-        stage1(4, 0)
+        stage2(2, BOTH)
         weave_h(3, (0,))
+        stage1(4, 0)
         relu(3, 1)
         root_v(0, 1)
         square_v(1)
         stage2(3, BOTH)
-        stage1(4, 1)
         bias_v(2)
         weave_h(3, (1,))
+        stage1(4, 1)
         relu(4, 0)
         square_v(2)
         stage2(4, BOTH)
         bias_v(3)
         quant_h(3, BOTH)
+        stage2(5, BOTH)
         relu(4, 1)
         clamp_v(1, 3)
         square_v(3)
-        stage2(5, BOTH)
-        root_v(1, 3)
         bias_v(4)
         finish_v(0)
         stage2(6, BOTH)
+        root_v(1, 3)
         weave_h(4, BOTH)
         square_v(4)
         finish_v(1)
         clamp_v(3, 5)
-        finish_v_on_scalar(2)
         quant_h(4, BOTH)
-        root_v(3, 5)
+        finish_v_on_scalar(2)
         end_stage2(BOTH)
+        root_v(3, 5)
         bias_v(5)
         finish_v_on_gpsimd(3, "hg4")
         square_v(5)

@@ -25,7 +25,6 @@ CHUNKS = ((0, 1), (1, 2), (3, 2), (5, 2), (7, 1))
 LAST = len(CHUNKS) - 1
 TILES = [(c, j) for c in range(len(CHUNKS)) for j in range(CHUNKS[c][1])]
 END = len(TILES) - 1
-STEPPED = (LAST,)
 
 
 def tile_geometricmanifoldnetwork_pa_w8_kernel(
@@ -63,27 +62,28 @@ def tile_geometricmanifoldnetwork_pa_w8_kernel(
         make_identity(nc, ident[:], nomemset=True)
 
         xbytes = [keep.tile([P, J, K], U8, name="xbytes%d" % c, align_bytes=64) for c, (i0, J) in enumerate(CHUNKS)]
-        w1raw = [keep.tile([P, 2, HALF], U32, name="w1raw%d" % T, align_bytes=64) for T in BOTH]
-        w1 = [keep.tile([P, 2, HALF], U32, name="w1_%d" % T, align_bytes=64) for T in BOTH]
+        early_raw = keep.tile([P, 2, HALF], U32, name="early_raw", align_bytes=64)
+        early = keep.tile([P, 2, HALF], U32, name="early", align_bytes=64)
+        late_raw = [keep.tile([P, HALF], U32, name="late_raw%d" % g, align_bytes=64) for g in BOTH]
+        late = [keep.tile([P, HALF], U32, name="late%d" % g, align_bytes=64) for g in BOTH]
         w2 = keep.tile([P, 2, NOUT], U32, name="w2", align_bytes=64)
         b1t = keep.tile([P, 2, 4], BF16, name="b1t")
         b2t = keep.tile([P, NOUT], BF16, name="b2t")
         w1i = W1_words.rearrange("g p n t -> p g (n t)").bitcast(I32)
         x_rows = x_bytes.rearrange("(p i) k -> p i k", i=len(TILES))
         out_rows = out.rearrange("(p i) o -> p i o", i=len(TILES))
-
         x_pairs = x_bytes.rearrange("(i a s) k -> a i s k", i=2, s=len(TILES))
         out_pairs = out.rearrange("(a i s) o -> a i s o", i=2, s=len(TILES))
 
         def load_x(c):
             i0, J = CHUNKS[c]
-            if J == 1 and c not in STEPPED:
+            if c == 0:
                 nc.sync.dma_start(out=xbytes[c][:, 0, :], in_=x_pairs[:, :, i0, :])
             else:
                 nc.sync.dma_start(out=xbytes[c][:], in_=x_rows[:, i0 : i0 + J, :])
 
-        def load_w1(T):
-            nc.sync.dma_start(out=w1raw[T][:].bitcast(I32), in_=w1i[:, :, HALF * T : HALF * T + HALF])
+        def load_late_w1(g):
+            nc.sync.dma_start(out=late_raw[g][:].bitcast(I32), in_=w1i[:, g, HALF:])
 
         def load_scales(dst, src):
             for Q in range(4):
@@ -91,15 +91,7 @@ def tile_geometricmanifoldnetwork_pa_w8_kernel(
                     out=dst[32 * Q : 32 * Q + 8, :].bitcast(I32), in_=src[:, 4 * Q : 4 * Q + 4, :].bitcast(I32)
                 )
 
-        def load_b1():
-            nc.scalar.dma_start(out=b1t[:], in_=b1.rearrange("(g p t) -> p g t", g=2, t=4))
-
-        def load_w2():
-            nc.sync.dma_start(out=w2[:].bitcast(I32), in_=W2_words.rearrange("g p n t -> p g (n t)").bitcast(I32))
-            load_scales(s2, W2_scales)
-            nc.sync.dma_start(out=b2t[:], in_=b2.partition_broadcast(P))
-
-        xv = {}
+        xv = [keep.tile([P, J, K], BF16, name="xv%d" % c, align_bytes=64) for c, (i0, J) in enumerate(CHUNKS)]
         xg, hp = each_chunk("xg", BF16, 4), each_chunk("hp", BF16, 4)
         xq, hq = each_chunk("xq", U32, 1), each_chunk("hq", U32, 1)
         xs, hs = each_chunk("xs", U8, 1), each_chunk("hs", U8, 1)
@@ -108,26 +100,34 @@ def tile_geometricmanifoldnetwork_pa_w8_kernel(
         over = keep.tile([P, len(TILES)], F32, name="over")
         r = keep.tile([P, len(TILES)], F32, name="r")
         end_ssq = [keep.tile([P, 1], F32, name="end_ssq%d" % a) for a in BOTH]
-        xt, xp, ph, hbank, hg, py = {}, {}, {}, {}, {}, {}
+        xt, ph, hg, py = {}, {}, {}, {}
 
         free_banks = ["bank%d" % b for b in range(8)]
         held = {}
 
-        def take_bank(key, shape, after=None):
-            held[key] = held[after] if after else free_banks[0]
-            if not after:
-                free_banks.remove(held[key])
+        def take_bank(key, shape):
+            held[key] = free_banks[0]
+            free_banks.remove(held[key])
             return psum.tile(shape, F32, name=held[key])
 
         def give_bank(key):
             free_banks.append(held[key])
 
-        sides = [slice(NOUT // 2 * a, NOUT // 2 * (a + 1)) for a in BOTH]
-
-        def permute_w1(T):
+        def permute_early_w1():
             nc.vector.tensor_copy(
-                out=w1[T][:].bitcast(I32).rearrange("p g (t c i) -> p g c t i", t=4, i=2),
-                in_=w1raw[T][:].bitcast(I32).rearrange("p g (c i t) -> p g c t i", t=4, i=2),
+                out=early[:].bitcast(I32).rearrange("p g (t c i) -> p g c t i", t=4, i=2),
+                in_=early_raw[:].bitcast(I32).rearrange("p g (c i t) -> p g c t i", t=4, i=2),
+            )
+
+        def permute_late_w1_on_scalar(g):
+            nc.scalar.copy(
+                out=late[g][:].rearrange("p (t c i) -> p c t i", t=4, i=2),
+                in_=late_raw[g][:].rearrange("p (c i t) -> p c t i", t=4, i=2),
+            )
+
+        def permute_late_w1_on_gpsimd(g):
+            nc.gpsimd.tensor_copy(
+                out=late[g][:].rearrange("p (t m) -> p t m", t=4), in_=late_raw[g][:].rearrange("p (m t) -> p t m", t=4)
             )
 
         def permute_s1():
@@ -136,12 +136,9 @@ def tile_geometricmanifoldnetwork_pa_w8_kernel(
                 in_=s1raw[:].rearrange("p (T c i t) -> p T c t i", T=2, t=4, i=8),
             )
 
-        def cast(c, gs=BOTH, on_vector=False):
-            copy = nc.vector.tensor_copy if on_vector else nc.scalar.copy
-            if c not in xv:
-                xv[c] = keep.tile([P, CHUNKS[c][1], K], BF16, name="xv%d" % c, align_bytes=64)
+        def cast(c, gs, copy=nc.scalar.copy, tiles=None):
             cols = slice(HALF * gs[0], HALF * gs[-1] + HALF)
-            for j in range(CHUNKS[c][1]):
+            for j in tiles or range(CHUNKS[c][1]):
                 copy(out=xv[c][:, j, cols], in_=xbytes[c][:, j, cols].bitcast(FP8))
 
         def turn(c, gs):
@@ -151,13 +148,13 @@ def tile_geometricmanifoldnetwork_pa_w8_kernel(
                 for j in range(J):
                     words = xv[c][:, j, :].bitcast(F32)
                     for u in range(2):
-                        dst = xt[c, gs][:, a, :, j, :, u] if c in STEPPED else xt[c, gs][:, a, :, j, u, :]
+                        dst = xt[c, gs][:, a, :, j, :, u] if c == LAST else xt[c, gs][:, a, :, j, u, :]
                         nc.tensor.transpose(dst, words[:, 256 * g + u : 256 * (g + 1) : 2], ident[:])
 
         def scale_x(c, gs):
             part = slice(gs[0], gs[-1] + 1)
             J = CHUNKS[c][1]
-            if c in STEPPED:
+            if c == LAST:
                 nc.vector.tensor_tensor(
                     out=xg[c][:, part, :].rearrange("p g (n t) -> p g n t", t=4),
                     in0=xt[c, gs][:].rearrange("p g a j i u -> p g (a j i) u").bitcast(BF16),
@@ -191,12 +188,12 @@ def tile_geometricmanifoldnetwork_pa_w8_kernel(
             per_bank = HALF // n
             for t in ts:
                 if t % per_bank == 0:
-                    hbank[c, T] = take_bank(("h", c, T, t // per_bank), [P, per_bank, n])
-                ph[c, T, t] = hbank[c, T][:, t % per_bank, :]
+                    bank = take_bank(("h", c, T, t // per_bank), [P, per_bank, n])
+                ph[c, T, t] = bank[:, t % per_bank, :]
                 for g in BOTH:
                     nc.tensor.matmul_mx(
                         out=ph[c, T, t],
-                        lhsT=(late_w1[g] if T else w1[0][:, g, :])[:, P * t : P * t + P].bitcast(FP8X4),
+                        lhsT=(late[g] if T else early[:, g, :])[:, P * t : P * t + P].bitcast(FP8X4),
                         lhsT_scale=s1[4 * g :, HALF * T + P * t : HALF * T + P * t + P],
                         rhs=xq[c][:, g, :].bitcast(FP8X4),
                         rhs_scale=xs[c][:, g, :],
@@ -204,18 +201,18 @@ def tile_geometricmanifoldnetwork_pa_w8_kernel(
                         stop=(g == 1),
                     )
 
-        def relu(c, T, ts=range(4)):
+        def relu(c, T):
             n = P * CHUNKS[c][1]
-            for t in ts:
+            for t in range(4):
                 nc.scalar.activation(
                     out=hp[c][:, T, n * t : n * t + n], in_=ph[c, T, t], func=ACT.Relu, bias=b1t[:, T, t : t + 1]
                 )
                 if (t + 1) * n % HALF == 0:
                     give_bank(("h", c, T, t * n // HALF))
 
-        def relu_in_pairs(c, T, ts=range(4)):
+        def relu_in_pairs(c, T):
             n = P * CHUNKS[c][1]
-            for t in ts:
+            for t in range(4):
                 dst = hp[c][:, T, 2 * n * (t // 2) + t % 2 : 2 * n * (t // 2 + 1) : 2]
                 nc.scalar.activation(out=dst, in_=ph[c, T, t], func=ACT.Relu, bias=b1t[:, T, t : t + 1])
                 if (t + 1) * n % HALF == 0:
@@ -226,17 +223,17 @@ def tile_geometricmanifoldnetwork_pa_w8_kernel(
                 hg[c] = keep.tile([P, 2, 4 * P * CHUNKS[c][1]], BF16, name=name or "hg%d" % c, align_bytes=64)
             return hg[c]
 
-        def weave_h(c, Ts, name=None):
+        def weave_h(c, Ts):
             part = slice(Ts[0], Ts[-1] + 1)
             nc.vector.tensor_copy(
-                out=woven(c, name)[:, part, :].rearrange("p T (c i t) -> p T c t i", i=4, t=4),
+                out=woven(c)[:, part, :].rearrange("p T (c i t) -> p T c t i", i=4, t=4),
                 in_=hp[c][:, part, :].rearrange("p T (t c i) -> p T c t i", i=4, t=4),
             )
 
-        def weave_pairs(c, Ts, name=None):
+        def weave_pairs(c, Ts):
             part = slice(Ts[0], Ts[-1] + 1)
             nc.vector.tensor_copy(
-                out=woven(c, name)[:, part, :].bitcast(F32).rearrange("p T (n u) -> p T n u", u=2),
+                out=woven(c)[:, part, :].bitcast(F32).rearrange("p T (n u) -> p T n u", u=2),
                 in_=hp[c][:, part, :].bitcast(F32).rearrange("p T (u n) -> p T n u", u=2),
             )
 
@@ -251,8 +248,8 @@ def tile_geometricmanifoldnetwork_pa_w8_kernel(
                 op1=ALU.add,
             )
 
-        def quant_h(c, Ts=BOTH):
-            quantise(hq[c], hs[c], hg[c], Ts)
+        def quant_h(c):
+            quantise(hq[c], hs[c], hg[c], BOTH)
 
         def stage2_pass(dst, i, T, cols):
             c, j = TILES[i]
@@ -266,16 +263,14 @@ def tile_geometricmanifoldnetwork_pa_w8_kernel(
                 stop=(T == 1),
             )
 
-        def stage2(i, Ts=BOTH, after=None):
-            for T in Ts:
-                if T == 0:
-                    py[i] = take_bank(("y", i), [P, NOUT], after)
+        def stage2(i):
+            py[i] = take_bank(("y", i), [P, NOUT])
+            for T in BOTH:
                 stage2_pass(py[i][:], i, T, slice(0, NOUT))
 
-        def bias_v(i, keep_bank=False):
+        def bias_v(i):
             nc.vector.tensor_tensor(out=v[i][:], in0=py[i][:], in1=b2t[:], op=ALU.add)
-            if not keep_bank:
-                give_bank(("y", i))
+            give_bank(("y", i))
 
         def square_v(i):
             nc.scalar.activation(out=squares[i][:], in_=v[i][:], func=ACT.Square, accum_out=ssq[:, i : i + 1])
@@ -305,15 +300,17 @@ def tile_geometricmanifoldnetwork_pa_w8_kernel(
             nc.scalar.activation(out=scaled[:], in_=v[i][:], func=ACT.Copy, scale=r[:, i : i + 1])
             store(i, scaled)
 
-        def finish_v_on_gpsimd(i, name=None):
-            scaled = keep.tile([P, NOUT], F32, name=name or "o%d" % i, align_bytes=64)
+        def finish_v_on_gpsimd(i):
+            scaled = keep.tile([P, NOUT], F32, name="hg%d" % LAST, align_bytes=64)
             nc.gpsimd.tensor_scalar(
                 out=scaled[:], in0=v[i][:], scalar1=r[:, i : i + 1], scalar2=0.0, op0=ALU.mult, op1=ALU.add
             )
             store(i, scaled)
 
-        def end_stage2(Ts=BOTH):
-            for T in Ts:
+        sides = [slice(NOUT // 2 * a, NOUT // 2 * (a + 1)) for a in BOTH]
+
+        def end_stage2():
+            for T in BOTH:
                 for a in BOTH:
                     if T == 0:
                         py[END, a] = take_bank(("y", END, a), [P, NOUT // 2])
@@ -347,39 +344,23 @@ def tile_geometricmanifoldnetwork_pa_w8_kernel(
         def end_root():
             nc.scalar.activation(out=r[:, END:], in_=ssq[:, END:], func=ACT.Abs_reciprocal_sqrt)
 
-        def permute_w1_half_on_gpsimd(g):
-            nc.gpsimd.tensor_copy(
-                out=late_w1[g][:].rearrange("p (t m) -> p t m", t=4), in_=late[g][:].rearrange("p (m t) -> p t m", t=4)
-            )
-
-        def permute_w1_half_on_scalar(g):
-            nc.scalar.copy(
-                out=late_w1[g][:].rearrange("p (t c i) -> p c t i", t=4, i=2),
-                in_=late[g][:].rearrange("p (c i t) -> p c t i", t=4, i=2),
-            )
-
-        def cast_part(c, j, g, on_gpsimd=False):
-            copy = nc.gpsimd.tensor_copy if on_gpsimd else nc.scalar.copy
-            cols = slice(HALF * g, HALF * g + HALF)
-            copy(out=xv[c][:, j, cols], in_=xbytes[c][:, j, cols].bitcast(FP8))
-
-
-        late = [keep.tile([P, HALF], U32, name="late%d" % g, align_bytes=64) for g in BOTH]
-        late_w1 = [keep.tile([P, HALF], U32, name="late_w1_%d" % g, align_bytes=64) for g in BOTH]
         load_x(0)
         load_scales(s1raw, W1_scales)
         load_x(1)
-        load_w1(0)
-        load_b1()
-        nc.sync.dma_start(out=late[0][:].bitcast(I32), in_=w1i[:, 0, HALF:])
+        nc.sync.dma_start(out=early_raw[:].bitcast(I32), in_=w1i[:, :, :HALF])
+        nc.scalar.dma_start(out=b1t[:], in_=b1.rearrange("(g p t) -> p g t", g=2, t=4))
+        load_late_w1(0)
         load_x(2)
-        nc.sync.dma_start(out=late[1][:].bitcast(I32), in_=w1i[:, 1, HALF:])
+        load_late_w1(1)
         load_x(3)
         load_x(4)
-        load_w2()
+        nc.sync.dma_start(out=w2[:].bitcast(I32), in_=W2_words.rearrange("g p n t -> p g (n t)").bitcast(I32))
+        load_scales(s2, W2_scales)
+        nc.sync.dma_start(out=b2t[:], in_=b2.partition_broadcast(P))
 
-        cast(0, (0,), on_vector=True)
-        cast(0, (1,), on_vector=True)
+
+        cast(0, (0,), nc.vector.tensor_copy)
+        cast(0, (1,), nc.vector.tensor_copy)
         turn(0, (0,))
         permute_s1()
         turn(0, (1,))
@@ -388,13 +369,13 @@ def tile_geometricmanifoldnetwork_pa_w8_kernel(
         scale_x(0, (0,))
         cast(1, (1,))
         scale_x(0, (1,))
-        permute_w1(0)
+        permute_early_w1()
         turn(1, (1,))
-        permute_w1_half_on_scalar(0)
-        quant_x(0, BOTH)
+        permute_late_w1_on_scalar(0)
+        quant_x(0)
         stage1(0, 0)
         cast(2, (0,))
-        permute_w1_half_on_gpsimd(1)
+        permute_late_w1_on_gpsimd(1)
         cast(2, (1,))
         scale_x(1, (0,))
         turn(2, (0,))
@@ -406,10 +387,10 @@ def tile_geometricmanifoldnetwork_pa_w8_kernel(
         stage1(0, 1)
         quant_x(1, (1,))
         weave_h_on_gpsimd(0, (0,), "xg1")
-        cast_part(3, 0, 1)
+        cast(3, (1,), tiles=(0,))
         stage1(1, 0)
         scale_x(2, (0,))
-        cast_part(3, 1, 1, on_gpsimd=True)
+        cast(3, (1,), nc.gpsimd.tensor_copy, tiles=(1,))
         stage1(1, 1)
         relu_in_pairs(0, 1)
         scale_x(2, (1,))
@@ -418,10 +399,10 @@ def tile_geometricmanifoldnetwork_pa_w8_kernel(
         weave_pairs(0, (1,))
         quant_x(2, (1,))
         relu(1, 0)
-        quant_h(0, BOTH)
+        quant_h(0)
         turn(3, (1,))
         weave_h_on_gpsimd(1, (0,), "xg2")
-        stage2(0, BOTH)
+        stage2(0)
         relu(1, 1)
         cast(4, BOTH)
         stage1(2, 0)
@@ -432,11 +413,11 @@ def tile_geometricmanifoldnetwork_pa_w8_kernel(
         relu(2, 0)
         bias_v(0)
         turn(4, BOTH)
-        quant_x(3, BOTH)
-        quant_h(1, BOTH)
+        quant_x(3)
+        quant_h(1)
         stage1(3, 0, (0, 1))
         weave_h_on_gpsimd(2, (0,), "xg3")
-        stage2(1, BOTH)
+        stage2(1)
         relu_in_pairs(2, 1)
         square_v(0)
         stage1(3, 0, (2, 3))
@@ -444,43 +425,43 @@ def tile_geometricmanifoldnetwork_pa_w8_kernel(
         stage1(3, 1)
         bias_v(1)
         weave_pairs(2, (1,))
-        quant_x(4, BOTH)
+        quant_x(4)
         relu(3, 0)
         clamp_v(0, 1)
-        quant_h(2, BOTH)
-        stage2(2, BOTH)
+        quant_h(2)
+        stage2(2)
         weave_h(3, (0,))
         stage1(4, 0)
         relu(3, 1)
         root_v(0, 1)
         square_v(1)
-        stage2(3, BOTH)
+        stage2(3)
         bias_v(2)
         weave_h(3, (1,))
         stage1(4, 1)
         relu(4, 0)
         square_v(2)
-        stage2(4, BOTH)
+        stage2(4)
         bias_v(3)
-        quant_h(3, BOTH)
-        stage2(5, BOTH)
+        quant_h(3)
+        stage2(5)
         relu(4, 1)
         clamp_v(1, 3)
         square_v(3)
         bias_v(4)
         finish_v(0)
-        stage2(6, BOTH)
+        stage2(6)
         root_v(1, 3)
         weave_h(4, BOTH)
         square_v(4)
         finish_v(1)
         clamp_v(3, 5)
-        quant_h(4, BOTH)
+        quant_h(4)
         finish_v_on_scalar(2)
-        end_stage2(BOTH)
+        end_stage2()
         root_v(3, 5)
         bias_v(5)
-        finish_v_on_gpsimd(3, "hg4")
+        finish_v_on_gpsimd(3)
         square_v(5)
         bias_v(6)
         end_bias(0)

@@ -61,29 +61,27 @@ def tile_geometricmanifoldnetwork_pa_w8_kernel(
         nc.vector.memset(ident[:], 0.0)
         make_identity(nc, ident[:], nomemset=True)
 
-        xbytes = [keep.tile([P, J, K], U8, name="xbytes%d" % c, align_bytes=64) for c, (i0, J) in enumerate(CHUNKS)]
+        xbytes = [keep.tile([P, J * K], U8, name="xbytes%d" % c, align_bytes=64) for c, (i0, J) in enumerate(CHUNKS)]
+        w1raw = {(1, g): keep.tile([P, HALF], U32, name="late_raw%d" % g, align_bytes=64) for g in BOTH}
+        w1 = {(1, g): keep.tile([P, HALF], U32, name="late%d" % g, align_bytes=64) for g in BOTH}
         early_raw = keep.tile([P, 2, HALF], U32, name="early_raw", align_bytes=64)
         early = keep.tile([P, 2, HALF], U32, name="early", align_bytes=64)
-        late_raw = [keep.tile([P, HALF], U32, name="late_raw%d" % g, align_bytes=64) for g in BOTH]
-        late = [keep.tile([P, HALF], U32, name="late%d" % g, align_bytes=64) for g in BOTH]
         w2 = keep.tile([P, 2, NOUT], U32, name="w2", align_bytes=64)
         b1t = keep.tile([P, 2, 4], BF16, name="b1t")
         b2t = keep.tile([P, NOUT], BF16, name="b2t")
         w1i = W1_words.rearrange("g p n t -> p g (n t)").bitcast(I32)
-        x_rows = x_bytes.rearrange("(p i) k -> p i k", i=len(TILES))
+        x_rows = x_bytes.rearrange("(p i) k -> p (i k)", i=len(TILES))
         out_rows = out.rearrange("(p i) o -> p i o", i=len(TILES))
-        x_pairs = x_bytes.rearrange("(i a s) k -> a i s k", i=2, s=len(TILES))
-        out_pairs = out.rearrange("(a i s) o -> a i s o", i=2, s=len(TILES))
 
         def load_x(c):
             i0, J = CHUNKS[c]
-            if c == 0:
-                nc.sync.dma_start(out=xbytes[c][:, 0, :], in_=x_pairs[:, :, i0, :])
-            else:
-                nc.sync.dma_start(out=xbytes[c][:], in_=x_rows[:, i0 : i0 + J, :])
+            nc.sync.dma_start(out=xbytes[c][:], in_=x_rows[:, K * i0 : K * (i0 + J)])
 
-        def load_late_w1(g):
-            nc.sync.dma_start(out=late_raw[g][:].bitcast(I32), in_=w1i[:, g, HALF:])
+        def load_w1(T, g):
+            nc.sync.dma_start(out=w1raw[T, g][:].bitcast(I32), in_=w1i[:, g, HALF * T : HALF * T + HALF])
+
+        def load_early_w1():
+            nc.sync.dma_start(out=early_raw[:].bitcast(I32), in_=w1i[:, :, :HALF])
 
         def load_scales(dst, src):
             for Q in range(4):
@@ -91,7 +89,15 @@ def tile_geometricmanifoldnetwork_pa_w8_kernel(
                     out=dst[32 * Q : 32 * Q + 8, :].bitcast(I32), in_=src[:, 4 * Q : 4 * Q + 4, :].bitcast(I32)
                 )
 
-        xv = [keep.tile([P, J, K], BF16, name="xv%d" % c, align_bytes=64) for c, (i0, J) in enumerate(CHUNKS)]
+        def load_b1():
+            nc.scalar.dma_start(out=b1t[:], in_=b1.rearrange("(g p t) -> p g t", g=2, t=4))
+
+        def load_w2():
+            nc.sync.dma_start(out=w2[:].bitcast(I32), in_=W2_words.rearrange("g p n t -> p g (n t)").bitcast(I32))
+
+        def load_b2():
+            nc.sync.dma_start(out=b2t[:], in_=b2.partition_broadcast(P))
+
         xg, hp = each_chunk("xg", BF16, 4), each_chunk("hp", BF16, 4)
         xq, hq = each_chunk("xq", U32, 1), each_chunk("hq", U32, 1)
         xs, hs = each_chunk("xs", U8, 1), each_chunk("hs", U8, 1)
@@ -100,7 +106,7 @@ def tile_geometricmanifoldnetwork_pa_w8_kernel(
         over = keep.tile([P, len(TILES)], F32, name="over")
         r = keep.tile([P, len(TILES)], F32, name="r")
         end_ssq = [keep.tile([P, 1], F32, name="end_ssq%d" % a) for a in BOTH]
-        xt, ph, hg, py = {}, {}, {}, {}
+        xv, xt, hbank, hg, py = {}, {}, {}, {}, {}
 
         free_banks = ["bank%d" % b for b in range(8)]
         held = {}
@@ -119,15 +125,15 @@ def tile_geometricmanifoldnetwork_pa_w8_kernel(
                 in_=early_raw[:].bitcast(I32).rearrange("p g (c i t) -> p g c t i", t=4, i=2),
             )
 
-        def permute_late_w1_on_scalar(g):
+        def permute_w1_on_scalar(T, g):
             nc.scalar.copy(
-                out=late[g][:].rearrange("p (t c i) -> p c t i", t=4, i=2),
-                in_=late_raw[g][:].rearrange("p (c i t) -> p c t i", t=4, i=2),
+                out=w1[T, g][:].rearrange("p (t c i) -> p c t i", t=4, i=2),
+                in_=w1raw[T, g][:].rearrange("p (c i t) -> p c t i", t=4, i=2),
             )
 
-        def permute_late_w1_on_gpsimd(g):
+        def permute_w1_on_gpsimd(T, g):
             nc.gpsimd.tensor_copy(
-                out=late[g][:].rearrange("p (t m) -> p t m", t=4), in_=late_raw[g][:].rearrange("p (m t) -> p t m", t=4)
+                out=w1[T, g][:].rearrange("p (t m) -> p t m", t=4), in_=w1raw[T, g][:].rearrange("p (m t) -> p t m", t=4)
             )
 
         def permute_s1():
@@ -136,41 +142,41 @@ def tile_geometricmanifoldnetwork_pa_w8_kernel(
                 in_=s1raw[:].rearrange("p (T c i t) -> p T c t i", T=2, t=4, i=8),
             )
 
-        def cast(c, gs, copy=nc.scalar.copy, tiles=None):
-            cols = slice(HALF * gs[0], HALF * gs[-1] + HALF)
-            for j in tiles or range(CHUNKS[c][1]):
-                copy(out=xv[c][:, j, cols], in_=xbytes[c][:, j, cols].bitcast(FP8))
+        def cast(c, g, tiles=None):
+            tiles = tiles or range(CHUNKS[c][1])
+            wide = keep.tile([P, len(tiles), 2, P], F32, name="xv%d%d%d" % (c, g, tiles[0]), align_bytes=64)
+            codes = xbytes[c][:].bitcast(FP8).rearrange("p (j g m u e) -> p j g u m e", g=2, m=P, u=2, e=2)
+            nc.scalar.copy(
+                out=wide[:].bitcast(BF16).rearrange("p j u (m e) -> p j u m e", e=2),
+                in_=codes[:, tiles[0] : tiles[-1] + 1, g],
+            )
+            for a, j in enumerate(tiles):
+                for u in BOTH:
+                    xv[c, g, j, u] = wide[:, a, u, :]
 
-        def turn(c, gs):
-            J = CHUNKS[c][1]
-            xt[c, gs] = take_bank(("x", c, gs), [P, len(gs), P // 2, J, 2, 2])
-            for a, g in enumerate(gs):
-                for j in range(J):
-                    words = xv[c][:, j, :].bitcast(F32)
-                    for u in range(2):
-                        dst = xt[c, gs][:, a, :, j, :, u] if c == LAST else xt[c, gs][:, a, :, j, u, :]
-                        nc.tensor.transpose(dst, words[:, 256 * g + u : 256 * (g + 1) : 2], ident[:])
+        def cast_plain(c, g, j, copy):
+            wide = keep.tile([P, HALF], BF16, name="xv%d%d%d" % (c, g, j), align_bytes=64)
+            first = K * j + HALF * g
+            copy(out=wide[:], in_=xbytes[c][:, first : first + HALF].bitcast(FP8))
+            for u in BOTH:
+                xv[c, g, j, u] = wide[:].bitcast(F32)[:, u::2]
 
-        def scale_x(c, gs):
-            part = slice(gs[0], gs[-1] + 1)
+        def turn(c, g):
             J = CHUNKS[c][1]
-            if c == LAST:
-                nc.vector.tensor_tensor(
-                    out=xg[c][:, part, :].rearrange("p g (n t) -> p g n t", t=4),
-                    in0=xt[c, gs][:].rearrange("p g a j i u -> p g (a j i) u").bitcast(BF16),
-                    in1=xsc[:, part, :].unsqueeze(2).to_broadcast([P, len(gs), P, 4]),
-                    op=ALU.mult,
-                )
-            else:
-                g = gs[0]
-                scales = xsc[:, g, :].rearrange("p (u e) -> p u e", u=2).unsqueeze(1).unsqueeze(1)
-                nc.vector.tensor_tensor(
-                    out=xg[c][:, g, :].rearrange("p (i n u e) -> p i n u e", i=2, u=2, e=2),
-                    in0=xt[c, gs][:, 0].bitcast(BF16).rearrange("p a j u (i e) -> p i (a j) u e", e=2),
-                    in1=scales.to_broadcast([P, 2, P // 2 * J, 2, 2]),
-                    op=ALU.mult,
-                )
-            give_bank(("x", c, gs))
+            xt[c, g] = take_bank(("x", c, g), [P, 2, J * P])
+            for j in range(J):
+                for u in BOTH:
+                    nc.tensor.transpose(xt[c, g][:, u, P * j : P * j + P], xv[c, g, j, u], ident[:])
+
+        def scale_x(c, g):
+            scales = xsc[:, g, :].rearrange("p (u e) -> p u e", u=2).unsqueeze(1)
+            nc.vector.tensor_tensor(
+                out=xg[c][:, g, :].rearrange("p (n u e) -> p n u e", u=2, e=2),
+                in0=xt[c, g][:].bitcast(BF16).rearrange("p u (n e) -> p n u e", e=2),
+                in1=scales.to_broadcast([P, P * CHUNKS[c][1], 2, 2]),
+                op=ALU.mult,
+            )
+            give_bank(("x", c, g))
 
         def quantise(codes, scales, values, gs):
             part = slice(gs[0], gs[-1] + 1)
@@ -188,12 +194,11 @@ def tile_geometricmanifoldnetwork_pa_w8_kernel(
             per_bank = HALF // n
             for t in ts:
                 if t % per_bank == 0:
-                    bank = take_bank(("h", c, T, t // per_bank), [P, per_bank, n])
-                ph[c, T, t] = bank[:, t % per_bank, :]
+                    hbank[c, T, t // per_bank] = take_bank(("h", c, T, t // per_bank), [P, per_bank, n])
                 for g in BOTH:
                     nc.tensor.matmul_mx(
-                        out=ph[c, T, t],
-                        lhsT=(late[g] if T else early[:, g, :])[:, P * t : P * t + P].bitcast(FP8X4),
+                        out=hbank[c, T, t // per_bank][:, t % per_bank, :],
+                        lhsT=(w1[T, g] if T else early[:, g, :])[:, P * t : P * t + P].bitcast(FP8X4),
                         lhsT_scale=s1[4 * g :, HALF * T + P * t : HALF * T + P * t + P],
                         rhs=xq[c][:, g, :].bitcast(FP8X4),
                         rhs_scale=xs[c][:, g, :],
@@ -201,27 +206,45 @@ def tile_geometricmanifoldnetwork_pa_w8_kernel(
                         stop=(g == 1),
                     )
 
-        def relu(c, T):
+        def relu(c, T, ts=range(4)):
             n = P * CHUNKS[c][1]
-            for t in range(4):
+            per_bank = HALF // n
+            for t in ts:
                 nc.scalar.activation(
-                    out=hp[c][:, T, n * t : n * t + n], in_=ph[c, T, t], func=ACT.Relu, bias=b1t[:, T, t : t + 1]
+                    out=hp[c][:, T, n * t : n * t + n],
+                    in_=hbank[c, T, t // per_bank][:, t % per_bank, :],
+                    func=ACT.Relu,
+                    bias=b1t[:, T, t : t + 1],
                 )
-                if (t + 1) * n % HALF == 0:
-                    give_bank(("h", c, T, t * n // HALF))
+                if (t + 1) % per_bank == 0:
+                    give_bank(("h", c, T, t // per_bank))
 
         def relu_in_pairs(c, T):
             n = P * CHUNKS[c][1]
+            per_bank = HALF // n
             for t in range(4):
                 dst = hp[c][:, T, 2 * n * (t // 2) + t % 2 : 2 * n * (t // 2 + 1) : 2]
-                nc.scalar.activation(out=dst, in_=ph[c, T, t], func=ACT.Relu, bias=b1t[:, T, t : t + 1])
-                if (t + 1) * n % HALF == 0:
-                    give_bank(("h", c, T, t * n // HALF))
+                src = hbank[c, T, t // per_bank][:, t % per_bank, :]
+                nc.scalar.activation(out=dst, in_=src, func=ACT.Relu, bias=b1t[:, T, t : t + 1])
+                if (t + 1) % per_bank == 0:
+                    give_bank(("h", c, T, t // per_bank))
 
         def woven(c, name=None):
             if c not in hg:
                 hg[c] = keep.tile([P, 2, 4 * P * CHUNKS[c][1]], BF16, name=name or "hg%d" % c, align_bytes=64)
             return hg[c]
+
+        def bias_h(c, T):
+            nc.vector.tensor_tensor(
+                out=hp[c][:, T, :].rearrange("p (n t) -> p n t", t=4),
+                in0=hbank[c, T, 0][:].rearrange("p t n -> p n t"),
+                in1=b1t[:, T, :].unsqueeze(1).to_broadcast([P, P, 4]),
+                op=ALU.add,
+            )
+            give_bank(("h", c, T, 0))
+
+        def relu_on_vector(c):
+            nc.vector.tensor_scalar(out=woven(c)[:], in0=hp[c][:], scalar1=0.0, scalar2=None, op0=ALU.max)
 
         def weave_h(c, Ts):
             part = slice(Ts[0], Ts[-1] + 1)
@@ -282,10 +305,7 @@ def tile_geometricmanifoldnetwork_pa_w8_kernel(
             nc.scalar.activation(out=r[:, a:b], in_=over[:, a:b], func=ACT.Abs_reciprocal_sqrt, bias=EPS2)
 
         def store(i, scaled, cols=slice(0, NOUT)):
-            c, j = TILES[i]
-            i0, J = CHUNKS[c]
-            rows = out_rows[:, i, cols] if J == 1 else out_pairs[:, j, i0 : i0 + J, cols]
-            nc.sync.dma_start(out=rows, in_=scaled[:, cols])
+            nc.sync.dma_start(out=out_rows[:, i, cols], in_=scaled[:, cols])
 
         def finish_v(i, parts=(slice(0, NOUT),)):
             scaled = keep.tile([P, NOUT], F32, name="o%d" % i, align_bytes=64)
@@ -300,8 +320,8 @@ def tile_geometricmanifoldnetwork_pa_w8_kernel(
             nc.scalar.activation(out=scaled[:], in_=v[i][:], func=ACT.Copy, scale=r[:, i : i + 1])
             store(i, scaled)
 
-        def finish_v_on_gpsimd(i):
-            scaled = keep.tile([P, NOUT], F32, name="hg%d" % LAST, align_bytes=64)
+        def finish_v_on_gpsimd(i, name=None):
+            scaled = keep.tile([P, NOUT], F32, name=name or "o%d" % i, align_bytes=64)
             nc.gpsimd.tensor_scalar(
                 out=scaled[:], in0=v[i][:], scalar1=r[:, i : i + 1], scalar2=0.0, op0=ALU.mult, op1=ALU.add
             )
@@ -347,72 +367,72 @@ def tile_geometricmanifoldnetwork_pa_w8_kernel(
         load_x(0)
         load_scales(s1raw, W1_scales)
         load_x(1)
-        nc.sync.dma_start(out=early_raw[:].bitcast(I32), in_=w1i[:, :, :HALF])
-        nc.scalar.dma_start(out=b1t[:], in_=b1.rearrange("(g p t) -> p g t", g=2, t=4))
-        load_late_w1(0)
+        load_early_w1()
+        load_b1()
+        load_w1(1, 0)
         load_x(2)
-        load_late_w1(1)
+        load_w1(1, 1)
         load_x(3)
         load_x(4)
-        nc.sync.dma_start(out=w2[:].bitcast(I32), in_=W2_words.rearrange("g p n t -> p g (n t)").bitcast(I32))
+        load_w2()
         load_scales(s2, W2_scales)
-        nc.sync.dma_start(out=b2t[:], in_=b2.partition_broadcast(P))
-
-
-        cast(0, (0,), nc.vector.tensor_copy)
-        cast(0, (1,), nc.vector.tensor_copy)
-        turn(0, (0,))
+        load_b2()
+        cast_plain(0, 0, 0, nc.vector.tensor_copy)
+        cast_plain(0, 1, 0, nc.vector.tensor_copy)
+        turn(0, 0)
         permute_s1()
-        turn(0, (1,))
-        cast(1, (0,))
-        turn(1, (0,))
-        scale_x(0, (0,))
-        cast(1, (1,))
-        scale_x(0, (1,))
+        turn(0, 1)
+        cast(1, 0)
+        turn(1, 0)
+        scale_x(0, 0)
+        cast(1, 1)
+        scale_x(0, 1)
         permute_early_w1()
-        turn(1, (1,))
-        permute_late_w1_on_scalar(0)
+        turn(1, 1)
+        permute_w1_on_scalar(1, 0)
         quant_x(0)
         stage1(0, 0)
-        cast(2, (0,))
-        permute_late_w1_on_gpsimd(1)
-        cast(2, (1,))
-        scale_x(1, (0,))
-        turn(2, (0,))
-        turn(2, (1,))
-        scale_x(1, (1,))
+        cast(2, 0)
+        permute_w1_on_gpsimd(1, 1)
+        cast(2, 1)
+        scale_x(1, 0)
+        turn(2, 0)
+        turn(2, 1)
+        scale_x(1, 1)
         quant_x(1, (0,))
         relu(0, 0)
-        cast(3, (0,))
+        cast(3, 0)
         stage1(0, 1)
         quant_x(1, (1,))
         weave_h_on_gpsimd(0, (0,), "xg1")
-        cast(3, (1,), tiles=(0,))
+        cast(3, 1, (0,))
         stage1(1, 0)
-        scale_x(2, (0,))
-        cast(3, (1,), nc.gpsimd.tensor_copy, tiles=(1,))
+        scale_x(2, 0)
+        cast_plain(3, 1, 1, nc.gpsimd.tensor_copy)
         stage1(1, 1)
         relu_in_pairs(0, 1)
-        scale_x(2, (1,))
+        scale_x(2, 1)
         quant_x(2, (0,))
-        turn(3, (0,))
+        turn(3, 0)
         weave_pairs(0, (1,))
         quant_x(2, (1,))
         relu(1, 0)
         quant_h(0)
-        turn(3, (1,))
+        turn(3, 1)
         weave_h_on_gpsimd(1, (0,), "xg2")
         stage2(0)
         relu(1, 1)
-        cast(4, BOTH)
+        cast(4, 0)
+        cast(4, 1)
         stage1(2, 0)
-        scale_x(3, (0,))
+        scale_x(3, 0)
         weave_h_on_gpsimd(1, (1,))
         stage1(2, 1)
-        scale_x(3, (1,))
+        scale_x(3, 1)
         relu(2, 0)
         bias_v(0)
-        turn(4, BOTH)
+        turn(4, 0)
+        turn(4, 1)
         quant_x(3)
         quant_h(1)
         stage1(3, 0, (0, 1))
@@ -421,7 +441,8 @@ def tile_geometricmanifoldnetwork_pa_w8_kernel(
         relu_in_pairs(2, 1)
         square_v(0)
         stage1(3, 0, (2, 3))
-        scale_x(4, BOTH)
+        scale_x(4, 0)
+        scale_x(4, 1)
         stage1(3, 1)
         bias_v(1)
         weave_pairs(2, (1,))
@@ -461,7 +482,7 @@ def tile_geometricmanifoldnetwork_pa_w8_kernel(
         end_stage2()
         root_v(3, 5)
         bias_v(5)
-        finish_v_on_gpsimd(3)
+        finish_v_on_gpsimd(3, "hg4")
         square_v(5)
         bias_v(6)
         end_bias(0)

@@ -49,12 +49,12 @@ def tile_geometricmanifoldnetwork_pa_w8_kernel(
         s1 = keep.tile([P, K], U8, name="s1", align_bytes=64)
         s2 = keep.tile([P, NOUT], U8, name="s2", align_bytes=64)
         xsc = keep.tile([P, 2, 4], F32, name="xsc")
-        nc.scalar.dma_start(out=xsc[:], in_=x_scale.rearrange("o (g p t) -> p (o g) t", g=2, t=4))
 
         one = keep.tile([P, 2], F32, name="one")
         nc.vector.memset(one[:], 1.0)
         warm = keep.tile([P, 2], F32, name="warm")
         nc.scalar.activation(out=warm[:], in_=one[:], func=ACT.Abs_reciprocal_sqrt)
+        nc.scalar.dma_start(out=xsc[:], in_=x_scale.rearrange("o (g p t) -> p (o g) t", g=2, t=4))
         nc.vector.memset(s1raw[:].bitcast(I32), 0)
         nc.vector.memset(s2[:].bitcast(I32), 0)
         ident = keep.tile([P, P], F32, name="ident", align_bytes=64)

@@ -46,7 +46,7 @@ def tile_geometricmanifoldnetwork_pa_w8_kernel(
             return [keep.tile([P, columns], dtype, name="%s%d" % (name, i), align_bytes=64) for i in range(len(TILES))]
 
         s1raw = keep.tile([P, K], U8, name="s1raw", align_bytes=64)
-        s1 = keep.tile([P, K], U8, name="s1", align_bytes=64)
+        s1 = {}
         s2 = keep.tile([P, NOUT], U8, name="s2", align_bytes=64)
         xsc = keep.tile([P, 2, 4], F32, name="xsc")
 
@@ -54,12 +54,13 @@ def tile_geometricmanifoldnetwork_pa_w8_kernel(
         nc.vector.memset(one[:], 1.0)
         warm = keep.tile([P, 2], F32, name="warm")
         nc.scalar.activation(out=warm[:], in_=one[:], func=ACT.Abs_reciprocal_sqrt)
-        nc.scalar.dma_start(out=xsc[:], in_=x_scale.rearrange("o (g p t) -> p (o g) t", g=2, t=4))
         nc.vector.memset(s1raw[:].bitcast(I32), 0)
-        nc.vector.memset(s2[:].bitcast(I32), 0)
         ident = keep.tile([P, P], F32, name="ident", align_bytes=64)
         nc.vector.memset(ident[:], 0.0)
         make_identity(nc, ident[:], nomemset=True)
+        nc.vector.memset(s2[:].bitcast(I32), 0)
+        b1rows = keep.tile([P, 2 * P], F32, name="b1rows", align_bytes=64)
+        nc.vector.memset(b1rows[:], 0.0)
 
         xbytes = [keep.tile([P, J * K], U8, name="xbytes%d" % c, align_bytes=64) for c, (i0, J) in enumerate(CHUNKS)]
         w1raw = {(1, g): keep.tile([P, HALF], U32, name="late_raw%d" % g, align_bytes=64) for g in BOTH}
@@ -89,8 +90,13 @@ def tile_geometricmanifoldnetwork_pa_w8_kernel(
                     out=dst[32 * Q : 32 * Q + 8, :].bitcast(I32), in_=src[:, 4 * Q : 4 * Q + 4, :].bitcast(I32)
                 )
 
+        def load_xsc():
+            nc.scalar.dma_start(out=xsc[:], in_=x_scale.rearrange("o (g p t) -> p (o g) t", g=2, t=4))
+
         def load_b1():
-            nc.scalar.dma_start(out=b1t[:], in_=b1.rearrange("(g p t) -> p g t", g=2, t=4))
+            words = b1.rearrange("(T k) -> T k", T=2).bitcast(F32)
+            for u in BOTH:
+                nc.scalar.dma_start(out=b1rows[2 * u : 2 * u + 2, : 2 * P - 1], in_=words[:, u : u + 2 * P - 1])
 
         def load_w2():
             nc.sync.dma_start(out=w2[:].bitcast(I32), in_=W2_words.rearrange("g p n t -> p g (n t)").bitcast(I32))
@@ -125,6 +131,12 @@ def tile_geometricmanifoldnetwork_pa_w8_kernel(
                 in_=early_raw[:].bitcast(I32).rearrange("p g (c i t) -> p g c t i", t=4, i=2),
             )
 
+        def permute_w1_on_vector(T, g):
+            nc.vector.tensor_copy(
+                out=w1[T, g][:].bitcast(I32).rearrange("p (t c i) -> p c t i", t=4, i=2),
+                in_=w1raw[T, g][:].bitcast(I32).rearrange("p (c i t) -> p c t i", t=4, i=2),
+            )
+
         def permute_w1_on_scalar(T, g):
             nc.scalar.copy(
                 out=w1[T, g][:].rearrange("p (t c i) -> p c t i", t=4, i=2),
@@ -136,11 +148,20 @@ def tile_geometricmanifoldnetwork_pa_w8_kernel(
                 out=w1[T, g][:].rearrange("p (t m) -> p t m", t=4), in_=w1raw[T, g][:].rearrange("p (m t) -> p t m", t=4)
             )
 
-        def permute_s1():
-            nc.vector.tensor_copy(
-                out=s1[:].rearrange("p (T t c i) -> p T c t i", T=2, t=4, i=8),
-                in_=s1raw[:].rearrange("p (T c i t) -> p T c t i", T=2, t=4, i=8),
+        def permute_s1(T, name):
+            s1[T] = keep.tile([P, HALF], U8, name=name, align_bytes=64)
+            nc.gpsimd.tensor_copy(
+                out=s1[T][:].rearrange("p (t m) -> p t m", t=4),
+                in_=s1raw[:, HALF * T : HALF * T + HALF].rearrange("p (m t) -> p t m", t=4),
             )
+
+        def turn_b1():
+            xt["b1"] = take_bank("b1", [P, P])
+            nc.tensor.transpose(xt["b1"][:], b1rows[:, : 2 * P - 1 : 2], ident[:])
+
+        def empty_b1():
+            nc.scalar.copy(out=b1t[:].bitcast(F32), in_=xt["b1"][:, :4].rearrange("p (u T) -> p T u", u=2))
+            give_bank("b1")
 
         def cast(c, g, tiles=None):
             tiles = tiles or range(CHUNKS[c][1])
@@ -158,6 +179,23 @@ def tile_geometricmanifoldnetwork_pa_w8_kernel(
             wide = keep.tile([P, HALF], BF16, name="xv%d%d%d" % (c, g, j), align_bytes=64)
             first = K * j + HALF * g
             copy(out=wide[:], in_=xbytes[c][:, first : first + HALF].bitcast(FP8))
+            for u in BOTH:
+                xv[c, g, j, u] = wide[:].bitcast(F32)[:, u::2]
+
+        def cast_apart(c, g, j, copy):
+            wide = keep.tile([P, 2, P], F32, name="xv%d%d%d" % (c, g, j), align_bytes=64)
+            first = K * j + HALF * g
+            copy(
+                out=wide[:].bitcast(BF16).rearrange("p u (m e) -> p m u e", e=2),
+                in_=xbytes[c][:, first : first + HALF].bitcast(FP8).rearrange("p (m u e) -> p m u e", u=2, e=2),
+            )
+            for u in BOTH:
+                xv[c, g, j, u] = wide[:, u, :]
+
+        def cast_held(c, g, j, name):
+            wide = keep.tile([P, HALF], BF16, name=name, align_bytes=64)
+            first = K * j + HALF * g
+            nc.gpsimd.tensor_copy(out=wide[:], in_=xbytes[c][:, first : first + HALF].bitcast(FP8))
             for u in BOTH:
                 xv[c, g, j, u] = wide[:].bitcast(F32)[:, u::2]
 
@@ -199,7 +237,7 @@ def tile_geometricmanifoldnetwork_pa_w8_kernel(
                     nc.tensor.matmul_mx(
                         out=hbank[c, T, t // per_bank][:, t % per_bank, :],
                         lhsT=(w1[T, g] if T else early[:, g, :])[:, P * t : P * t + P].bitcast(FP8X4),
-                        lhsT_scale=s1[4 * g :, HALF * T + P * t : HALF * T + P * t + P],
+                        lhsT_scale=s1[T][4 * g :, P * t : P * t + P],
                         rhs=xq[c][:, g, :].bitcast(FP8X4),
                         rhs_scale=xs[c][:, g, :],
                         start=(g == 0),
@@ -251,6 +289,24 @@ def tile_geometricmanifoldnetwork_pa_w8_kernel(
             nc.vector.tensor_copy(
                 out=woven(c)[:, part, :].rearrange("p T (c i t) -> p T c t i", i=4, t=4),
                 in_=hp[c][:, part, :].rearrange("p T (t c i) -> p T c t i", i=4, t=4),
+            )
+
+        def weave_tile(c, T, j):
+            nc.vector.tensor_copy(
+                out=woven(c)[:, T, HALF * j : HALF * j + HALF].rearrange("p (c i t) -> p c t i", i=4, t=4),
+                in_=hp[c][:, T, :].rearrange("p (t n) -> p t n", t=4)[:, :, P * j : P * j + P].rearrange(
+                    "p t (c i) -> p c t i", i=4
+                ),
+            )
+
+        def weave_tile_on_gpsimd(c, T, j, name=None):
+            nc.gpsimd.tensor_scalar(
+                out=woven(c, name)[:, T, HALF * j : HALF * j + HALF].rearrange("p (n t) -> p n t", t=4),
+                in0=hp[c][:, T, :].rearrange("p (t n) -> p n t", t=4)[:, P * j : P * j + P, :],
+                scalar1=1.0,
+                scalar2=0.0,
+                op0=ALU.mult,
+                op1=ALU.add,
             )
 
         def weave_pairs(c, Ts):
@@ -365,55 +421,59 @@ def tile_geometricmanifoldnetwork_pa_w8_kernel(
             nc.scalar.activation(out=r[:, END:], in_=ssq[:, END:], func=ACT.Abs_reciprocal_sqrt)
 
         load_x(0)
-        load_scales(s1raw, W1_scales)
         load_x(1)
-        load_early_w1()
-        load_b1()
-        load_w1(1, 0)
+        load_scales(s1raw, W1_scales)
+        load_xsc()
         load_x(2)
+        load_early_w1()
+        load_w1(1, 0)
         load_w1(1, 1)
+        cast_apart(0, 0, 0, nc.vector.tensor_copy)
+        cast_apart(0, 1, 0, nc.vector.tensor_copy)
+        turn(0, 0)
+        turn(0, 1)
+        permute_s1(0, "xv010")
+        cast(1, 0)
+        turn(1, 0)
+        scale_x(0, 0)
+        cast(1, 1)
+        load_b1()
         load_x(3)
         load_x(4)
         load_w2()
         load_scales(s2, W2_scales)
         load_b2()
-        cast_plain(0, 0, 0, nc.vector.tensor_copy)
-        cast_plain(0, 1, 0, nc.vector.tensor_copy)
-        turn(0, 0)
-        permute_s1()
-        turn(0, 1)
-        cast(1, 0)
-        turn(1, 0)
-        scale_x(0, 0)
-        cast(1, 1)
         scale_x(0, 1)
-        permute_early_w1()
         turn(1, 1)
-        permute_w1_on_scalar(1, 0)
-        quant_x(0)
-        stage1(0, 0)
-        cast(2, 0)
-        permute_w1_on_gpsimd(1, 1)
-        cast(2, 1)
         scale_x(1, 0)
+        cast(2, 0)
+        cast(2, 1)
+        quant_x(0)
+        permute_early_w1()
         turn(2, 0)
         turn(2, 1)
+        turn_b1()
+        permute_w1_on_scalar(1, 0)
+        stage1(0, 0)
+        permute_s1(1, "xg0")
         scale_x(1, 1)
+        permute_w1_on_scalar(1, 1)
+        empty_b1()
         quant_x(1, (0,))
-        relu(0, 0)
         cast(3, 0)
         stage1(0, 1)
         quant_x(1, (1,))
-        weave_h_on_gpsimd(0, (0,), "xg1")
-        cast(3, 1, (0,))
+        cast_held(3, 1, 1, "xg1")
+        relu(0, 0)
         stage1(1, 0)
         scale_x(2, 0)
-        cast_plain(3, 1, 1, nc.gpsimd.tensor_copy)
-        stage1(1, 1)
-        relu_in_pairs(0, 1)
+        cast(3, 1, (0,))
+        weave_h_on_gpsimd(0, (0,))
         scale_x(2, 1)
-        quant_x(2, (0,))
+        relu_in_pairs(0, 1)
+        stage1(1, 1)
         turn(3, 0)
+        quant_x(2, (0,))
         weave_pairs(0, (1,))
         quant_x(2, (1,))
         relu(1, 0)

@@ -163,6 +163,11 @@ def tile_geometricmanifoldnetwork_pa_w8_kernel(
             nc.scalar.copy(out=b1t[:].bitcast(F32), in_=xt["b1"][:, :4].rearrange("p (u T) -> p T u", u=2))
             give_bank("b1")
 
+        def warm_pe(count):
+            sink = psum.tile([P, P], F32, name="bank7")
+            for a in range(count):
+                nc.tensor.matmul(sink[:], lhsT=ident[:], rhs=ident[:], start=True, stop=True)
+
         def cast(c, g, tiles=None):
             tiles = tiles or range(CHUNKS[c][1])
             wide = keep.tile([P, len(tiles), 2, P], F32, name="xv%d%d%d" % (c, g, tiles[0]), align_bytes=64)
@@ -428,13 +433,16 @@ def tile_geometricmanifoldnetwork_pa_w8_kernel(
         load_early_w1()
         load_w1(1, 0)
         load_w1(1, 1)
+        warm_pe(2)
         cast_apart(0, 0, 0, nc.vector.tensor_copy)
         cast_apart(0, 1, 0, nc.vector.tensor_copy)
         turn(0, 0)
         turn(0, 1)
+        warm_pe(1)
         permute_s1(0, "xv010")
         cast(1, 0)
         turn(1, 0)
+        warm_pe(1)
         scale_x(0, 0)
         cast(1, 1)
         load_b1()
@@ -445,6 +453,7 @@ def tile_geometricmanifoldnetwork_pa_w8_kernel(
         load_b2()
         scale_x(0, 1)
         turn(1, 1)
+        warm_pe(2)
         scale_x(1, 0)
         cast(2, 0)
         cast(2, 1)

@@ -155,6 +155,13 @@ def tile_geometricmanifoldnetwork_pa_w8_kernel(
                 in_=s1raw[:, HALF * T : HALF * T + HALF].rearrange("p (m t) -> p t m", t=4),
             )
 
+        def permute_s1_on_vector(T):
+            s1[T] = keep.tile([P, HALF], U8, name="s1_%d" % T, align_bytes=64)
+            nc.vector.tensor_copy(
+                out=s1[T][:].rearrange("p (t c i) -> p c t i", t=4, i=8),
+                in_=s1raw[:, HALF * T : HALF * T + HALF].rearrange("p (c i t) -> p c t i", t=4, i=8),
+            )
+
         def turn_b1():
             xt["b1"] = take_bank("b1", [P, P])
             nc.tensor.transpose(xt["b1"][:], b1rows[:, : 2 * P - 1 : 2], ident[:])
@@ -458,13 +465,13 @@ def tile_geometricmanifoldnetwork_pa_w8_kernel(
         cast(2, 0)
         cast(2, 1)
         quant_x(0)
+        permute_s1_on_vector(1)
         permute_early_w1()
         turn(2, 0)
         turn(2, 1)
         turn_b1()
         permute_w1_on_scalar(1, 0)
         stage1(0, 0)
-        permute_s1(1, "xg0")
         scale_x(1, 1)
         permute_w1_on_scalar(1, 1)
         empty_b1()

@@ -63,8 +63,8 @@ def tile_geometricmanifoldnetwork_pa_w8_kernel(
         nc.vector.memset(b1rows[:], 0.0)
 
         xbytes = [keep.tile([P, J * K], U8, name="xbytes%d" % c, align_bytes=64) for c, (i0, J) in enumerate(CHUNKS)]
-        w1raw = {(1, g): keep.tile([P, HALF], U32, name="late_raw%d" % g, align_bytes=64) for g in BOTH}
-        w1 = {(1, g): keep.tile([P, HALF], U32, name="late%d" % g, align_bytes=64) for g in BOTH}
+        late_raw = [keep.tile([P, HALF], U32, name="late_raw%d" % g, align_bytes=64) for g in BOTH]
+        late = [keep.tile([P, HALF], U32, name="late%d" % g, align_bytes=64) for g in BOTH]
         early_raw = keep.tile([P, 2, HALF], U32, name="early_raw", align_bytes=64)
         early = keep.tile([P, 2, HALF], U32, name="early", align_bytes=64)
         w2 = keep.tile([P, 2, NOUT], U32, name="w2", align_bytes=64)
@@ -78,8 +78,8 @@ def tile_geometricmanifoldnetwork_pa_w8_kernel(
             i0, J = CHUNKS[c]
             nc.sync.dma_start(out=xbytes[c][:], in_=x_rows[:, K * i0 : K * (i0 + J)])
 
-        def load_w1(T, g):
-            nc.sync.dma_start(out=w1raw[T, g][:].bitcast(I32), in_=w1i[:, g, HALF * T : HALF * T + HALF])
+        def load_late_w1(g):
+            nc.sync.dma_start(out=late_raw[g][:].bitcast(I32), in_=w1i[:, g, HALF:])
 
         def load_early_w1():
             nc.sync.dma_start(out=early_raw[:].bitcast(I32), in_=w1i[:, :, :HALF])
@@ -90,13 +90,13 @@ def tile_geometricmanifoldnetwork_pa_w8_kernel(
                     out=dst[32 * Q : 32 * Q + 8, :].bitcast(I32), in_=src[:, 4 * Q : 4 * Q + 4, :].bitcast(I32)
                 )
 
-        def load_xsc():
+        def load_x_scale():
             nc.scalar.dma_start(out=xsc[:], in_=x_scale.rearrange("o (g p t) -> p (o g) t", g=2, t=4))
 
         def load_b1():
             words = b1.rearrange("(T k) -> T k", T=2).bitcast(F32)
             for u in BOTH:
-                nc.scalar.dma_start(out=b1rows[2 * u : 2 * u + 2, : 2 * P - 1], in_=words[:, u : u + 2 * P - 1])
+                nc.sync.dma_start(out=b1rows[2 * u : 2 * u + 2, : 2 * P - 1], in_=words[:, u : u + 2 * P - 1])
 
         def load_w2():
             nc.sync.dma_start(out=w2[:].bitcast(I32), in_=W2_words.rearrange("g p n t -> p g (n t)").bitcast(I32))
@@ -110,9 +110,10 @@ def tile_geometricmanifoldnetwork_pa_w8_kernel(
         v, squares = each_tile("v", F32, NOUT), each_tile("squares", BF16, NOUT)
         ssq = keep.tile([P, len(TILES)], F32, name="ssq")
         over = keep.tile([P, len(TILES)], F32, name="over")
+        floored = keep.tile([P, len(TILES)], F32, name="floored")
         r = keep.tile([P, len(TILES)], F32, name="r")
         end_ssq = [keep.tile([P, 1], F32, name="end_ssq%d" % a) for a in BOTH]
-        xv, xt, hbank, hg, py = {}, {}, {}, {}, {}
+        xv, xt, turned_b1, hbank, hg, py = {}, {}, {}, {}, {}, {}
 
         free_banks = ["bank%d" % b for b in range(8)]
         held = {}
@@ -131,46 +132,34 @@ def tile_geometricmanifoldnetwork_pa_w8_kernel(
                 in_=early_raw[:].bitcast(I32).rearrange("p g (c i t) -> p g c t i", t=4, i=2),
             )
 
-        def permute_w1_on_vector(T, g):
-            nc.vector.tensor_copy(
-                out=w1[T, g][:].bitcast(I32).rearrange("p (t c i) -> p c t i", t=4, i=2),
-                in_=w1raw[T, g][:].bitcast(I32).rearrange("p (c i t) -> p c t i", t=4, i=2),
-            )
-
-        def permute_w1_on_scalar(T, g):
+        def permute_late_w1(g):
             nc.scalar.copy(
-                out=w1[T, g][:].rearrange("p (t c i) -> p c t i", t=4, i=2),
-                in_=w1raw[T, g][:].rearrange("p (c i t) -> p c t i", t=4, i=2),
+                out=late[g][:].rearrange("p (t c i) -> p c t i", t=4, i=2),
+                in_=late_raw[g][:].rearrange("p (c i t) -> p c t i", t=4, i=2),
             )
 
-        def permute_w1_on_gpsimd(T, g):
+        def permute_early_s1():
+            s1[0] = keep.tile([P, HALF], U8, name="xv010", align_bytes=64)
             nc.gpsimd.tensor_copy(
-                out=w1[T, g][:].rearrange("p (t m) -> p t m", t=4), in_=w1raw[T, g][:].rearrange("p (m t) -> p t m", t=4)
+                out=s1[0][:].rearrange("p (t m) -> p t m", t=4), in_=s1raw[:, :HALF].rearrange("p (m t) -> p t m", t=4)
             )
 
-        def permute_s1(T, name):
-            s1[T] = keep.tile([P, HALF], U8, name=name, align_bytes=64)
-            nc.gpsimd.tensor_copy(
-                out=s1[T][:].rearrange("p (t m) -> p t m", t=4),
-                in_=s1raw[:, HALF * T : HALF * T + HALF].rearrange("p (m t) -> p t m", t=4),
-            )
-
-        def permute_s1_on_vector(T):
-            s1[T] = keep.tile([P, HALF], U8, name="s1_%d" % T, align_bytes=64)
+        def permute_late_s1():
+            s1[1] = keep.tile([P, HALF], U8, name="s1_1", align_bytes=64)
             nc.vector.tensor_copy(
-                out=s1[T][:].rearrange("p (t c i) -> p c t i", t=4, i=8),
-                in_=s1raw[:, HALF * T : HALF * T + HALF].rearrange("p (c i t) -> p c t i", t=4, i=8),
+                out=s1[1][:].rearrange("p (t c i) -> p c t i", t=4, i=8),
+                in_=s1raw[:, HALF:].rearrange("p (c i t) -> p c t i", t=4, i=8),
             )
 
         def turn_b1():
-            xt["b1"] = take_bank("b1", [P, P])
-            nc.tensor.transpose(xt["b1"][:], b1rows[:, : 2 * P - 1 : 2], ident[:])
+            turned_b1[0] = take_bank("b1", [P, P])
+            nc.tensor.transpose(turned_b1[0][:], b1rows[:, : 2 * P - 1 : 2], ident[:])
 
         def empty_b1():
-            nc.scalar.copy(out=b1t[:].bitcast(F32), in_=xt["b1"][:, :4].rearrange("p (u T) -> p T u", u=2))
+            nc.scalar.copy(out=b1t[:].bitcast(F32), in_=turned_b1[0][:, :4].rearrange("p (u T) -> p T u", u=2))
             give_bank("b1")
 
-        def warm_pe(count):
+        def warm_tensor(count):
             sink = psum.tile([P, P], F32, name="bank7")
             for a in range(count):
                 nc.tensor.matmul(sink[:], lhsT=ident[:], rhs=ident[:], start=True, stop=True)
@@ -187,24 +176,16 @@ def tile_geometricmanifoldnetwork_pa_w8_kernel(
                 for u in BOTH:
                     xv[c, g, j, u] = wide[:, a, u, :]
 
-        def cast_plain(c, g, j, copy):
-            wide = keep.tile([P, HALF], BF16, name="xv%d%d%d" % (c, g, j), align_bytes=64)
-            first = K * j + HALF * g
-            copy(out=wide[:], in_=xbytes[c][:, first : first + HALF].bitcast(FP8))
-            for u in BOTH:
-                xv[c, g, j, u] = wide[:].bitcast(F32)[:, u::2]
-
-        def cast_apart(c, g, j, copy):
-            wide = keep.tile([P, 2, P], F32, name="xv%d%d%d" % (c, g, j), align_bytes=64)
-            first = K * j + HALF * g
-            copy(
+        def cast_first_tile(g):
+            wide = keep.tile([P, 2, P], F32, name="xv0%d0" % g, align_bytes=64)
+            nc.vector.tensor_copy(
                 out=wide[:].bitcast(BF16).rearrange("p u (m e) -> p m u e", e=2),
-                in_=xbytes[c][:, first : first + HALF].bitcast(FP8).rearrange("p (m u e) -> p m u e", u=2, e=2),
+                in_=xbytes[0][:, HALF * g : HALF * g + HALF].bitcast(FP8).rearrange("p (m u e) -> p m u e", u=2, e=2),
             )
             for u in BOTH:
-                xv[c, g, j, u] = wide[:, u, :]
+                xv[0, g, 0, u] = wide[:, u, :]
 
-        def cast_held(c, g, j, name):
+        def cast_on_gpsimd(c, g, j, name):
             wide = keep.tile([P, HALF], BF16, name=name, align_bytes=64)
             first = K * j + HALF * g
             nc.gpsimd.tensor_copy(out=wide[:], in_=xbytes[c][:, first : first + HALF].bitcast(FP8))
@@ -248,7 +229,7 @@ def tile_geometricmanifoldnetwork_pa_w8_kernel(
                 for g in BOTH:
                     nc.tensor.matmul_mx(
                         out=hbank[c, T, t // per_bank][:, t % per_bank, :],
-                        lhsT=(w1[T, g] if T else early[:, g, :])[:, P * t : P * t + P].bitcast(FP8X4),
+                        lhsT=(late[g] if T else early[:, g, :])[:, P * t : P * t + P].bitcast(FP8X4),
                         lhsT_scale=s1[T][4 * g :, P * t : P * t + P],
                         rhs=xq[c][:, g, :].bitcast(FP8X4),
                         rhs_scale=xs[c][:, g, :],
@@ -256,10 +237,10 @@ def tile_geometricmanifoldnetwork_pa_w8_kernel(
                         stop=(g == 1),
                     )
 
-        def relu(c, T, ts=range(4)):
+        def relu(c, T):
             n = P * CHUNKS[c][1]
             per_bank = HALF // n
-            for t in ts:
+            for t in range(4):
                 nc.scalar.activation(
                     out=hp[c][:, T, n * t : n * t + n],
                     in_=hbank[c, T, t // per_bank][:, t % per_bank, :],
@@ -284,41 +265,11 @@ def tile_geometricmanifoldnetwork_pa_w8_kernel(
                 hg[c] = keep.tile([P, 2, 4 * P * CHUNKS[c][1]], BF16, name=name or "hg%d" % c, align_bytes=64)
             return hg[c]
 
-        def bias_h(c, T):
-            nc.vector.tensor_tensor(
-                out=hp[c][:, T, :].rearrange("p (n t) -> p n t", t=4),
-                in0=hbank[c, T, 0][:].rearrange("p t n -> p n t"),
-                in1=b1t[:, T, :].unsqueeze(1).to_broadcast([P, P, 4]),
-                op=ALU.add,
-            )
-            give_bank(("h", c, T, 0))
-
-        def relu_on_vector(c):
-            nc.vector.tensor_scalar(out=woven(c)[:], in0=hp[c][:], scalar1=0.0, scalar2=None, op0=ALU.max)
-
         def weave_h(c, Ts):
             part = slice(Ts[0], Ts[-1] + 1)
             nc.vector.tensor_copy(
                 out=woven(c)[:, part, :].rearrange("p T (c i t) -> p T c t i", i=4, t=4),
                 in_=hp[c][:, part, :].rearrange("p T (t c i) -> p T c t i", i=4, t=4),
-            )
-
-        def weave_tile(c, T, j):
-            nc.vector.tensor_copy(
-                out=woven(c)[:, T, HALF * j : HALF * j + HALF].rearrange("p (c i t) -> p c t i", i=4, t=4),
-                in_=hp[c][:, T, :].rearrange("p (t n) -> p t n", t=4)[:, :, P * j : P * j + P].rearrange(
-                    "p t (c i) -> p c t i", i=4
-                ),
-            )
-
-        def weave_tile_on_gpsimd(c, T, j, name=None):
-            nc.gpsimd.tensor_scalar(
-                out=woven(c, name)[:, T, HALF * j : HALF * j + HALF].rearrange("p (n t) -> p n t", t=4),
-                in0=hp[c][:, T, :].rearrange("p (t n) -> p n t", t=4)[:, P * j : P * j + P, :],
-                scalar1=1.0,
-                scalar2=0.0,
-                op0=ALU.mult,
-                op1=ALU.add,
             )
 
         def weave_pairs(c, Ts):
@@ -372,6 +323,14 @@ def tile_geometricmanifoldnetwork_pa_w8_kernel(
         def root_v(a, b):
             nc.scalar.activation(out=r[:, a:b], in_=over[:, a:b], func=ACT.Abs_reciprocal_sqrt, bias=EPS2)
 
+        def clamp_on_vector(i):
+            nc.vector.tensor_scalar(
+                out=floored[:, i : i + 1], in0=ssq[:, i : i + 1], scalar1=EPS2, scalar2=None, op0=ALU.max
+            )
+
+        def root_of_floored(i):
+            nc.scalar.activation(out=r[:, i : i + 1], in_=floored[:, i : i + 1], func=ACT.Abs_reciprocal_sqrt)
+
         def store(i, scaled, cols=slice(0, NOUT)):
             nc.sync.dma_start(out=out_rows[:, i, cols], in_=scaled[:, cols])
 
@@ -388,8 +347,8 @@ def tile_geometricmanifoldnetwork_pa_w8_kernel(
             nc.scalar.activation(out=scaled[:], in_=v[i][:], func=ACT.Copy, scale=r[:, i : i + 1])
             store(i, scaled)
 
-        def finish_v_on_gpsimd(i, name=None):
-            scaled = keep.tile([P, NOUT], F32, name=name or "o%d" % i, align_bytes=64)
+        def finish_v_on_gpsimd(i):
+            scaled = keep.tile([P, NOUT], F32, name="hg%d" % LAST, align_bytes=64)
             nc.gpsimd.tensor_scalar(
                 out=scaled[:], in0=v[i][:], scalar1=r[:, i : i + 1], scalar2=0.0, op0=ALU.mult, op1=ALU.add
             )
@@ -432,27 +391,30 @@ def tile_geometricmanifoldnetwork_pa_w8_kernel(
         def end_root():
             nc.scalar.activation(out=r[:, END:], in_=ssq[:, END:], func=ACT.Abs_reciprocal_sqrt)
 
+
         load_x(0)
         load_x(1)
         load_scales(s1raw, W1_scales)
-        load_xsc()
+        load_x_scale()
         load_x(2)
         load_early_w1()
-        load_w1(1, 0)
-        load_w1(1, 1)
-        warm_pe(2)
-        cast_apart(0, 0, 0, nc.vector.tensor_copy)
-        cast_apart(0, 1, 0, nc.vector.tensor_copy)
+        load_b1()
+        load_late_w1(0)
+        load_late_w1(1)
+
+
+        warm_tensor(2)
+        cast_first_tile(0)
+        cast_first_tile(1)
         turn(0, 0)
         turn(0, 1)
-        warm_pe(1)
-        permute_s1(0, "xv010")
+        warm_tensor(1)
+        permute_early_s1()
         cast(1, 0)
         turn(1, 0)
-        warm_pe(1)
+        warm_tensor(1)
         scale_x(0, 0)
         cast(1, 1)
-        load_b1()
         load_x(3)
         load_x(4)
         load_w2()
@@ -460,26 +422,27 @@ def tile_geometricmanifoldnetwork_pa_w8_kernel(
         load_b2()
         scale_x(0, 1)
         turn(1, 1)
-        warm_pe(2)
+        warm_tensor(2)
         scale_x(1, 0)
         cast(2, 0)
         cast(2, 1)
         quant_x(0)
-        permute_s1_on_vector(1)
+        permute_late_s1()
         permute_early_w1()
         turn(2, 0)
-        turn(2, 1)
         turn_b1()
-        permute_w1_on_scalar(1, 0)
+        warm_tensor(1)
+        turn(2, 1)
+        permute_late_w1(0)
         stage1(0, 0)
         scale_x(1, 1)
-        permute_w1_on_scalar(1, 1)
+        permute_late_w1(1)
         empty_b1()
         quant_x(1, (0,))
         cast(3, 0)
         stage1(0, 1)
         quant_x(1, (1,))
-        cast_held(3, 1, 1, "xg1")
+        cast_on_gpsimd(3, 1, 1, "xg1")
         relu(0, 0)
         stage1(1, 0)
         scale_x(2, 0)
@@ -496,11 +459,11 @@ def tile_geometricmanifoldnetwork_pa_w8_kernel(
         quant_h(0)
         turn(3, 1)
         weave_h_on_gpsimd(1, (0,), "xg2")
-        stage2(0)
         relu(1, 1)
         cast(4, 0)
         cast(4, 1)
         stage1(2, 0)
+        stage2(0)
         scale_x(3, 0)
         weave_h_on_gpsimd(1, (1,))
         stage1(2, 1)
@@ -554,24 +517,24 @@ def tile_geometricmanifoldnetwork_pa_w8_kernel(
         finish_v(1)
         clamp_v(3, 5)
         quant_h(4)
+        root_v(3, 5)
         finish_v_on_scalar(2)
         end_stage2()
-        root_v(3, 5)
         bias_v(5)
-        finish_v_on_gpsimd(3, "hg4")
+        finish_v_on_gpsimd(3)
         square_v(5)
         bias_v(6)
         end_bias(0)
         square_v(6)
         end_bias(1)
+        clamp_on_vector(5)
         finish_v(4)
-        clamp_v(5, 6)
+        root_of_floored(5)
         end_square_on_vector(1)
         end_square_on_scalar(0)
-        root_v(5, 6)
-        clamp_v(6, 7)
+        clamp_on_vector(6)
         finish_v(5)
-        root_v(6, 7)
+        root_of_floored(6)
         end_sum_and_clamp()
         finish_v(6)
         end_root()

@@ -38,16 +38,16 @@ def tile_geometricmanifoldnetwork_pa_w8_kernel(
 
         def each_chunk(name, dtype, per_token):
             return [
-                keep.tile([P, 2, per_token * P * J], dtype, name="%s%d" % (name, c), align_bytes=64)
+                keep.tile([P, 2, per_token * P * J], dtype, name="%s%d" % (name, c), align_bytes=256)
                 for c, (i0, J) in enumerate(CHUNKS)
             ]
 
         def each_tile(name, dtype, columns):
-            return [keep.tile([P, columns], dtype, name="%s%d" % (name, i), align_bytes=64) for i in range(len(TILES))]
+            return [keep.tile([P, columns], dtype, name="%s%d" % (name, i), align_bytes=256) for i in range(len(TILES))]
 
-        s1raw = keep.tile([P, K], U8, name="s1raw", align_bytes=64)
+        s1raw = keep.tile([P, K], U8, name="s1raw", align_bytes=256)
         s1 = {}
-        s2 = keep.tile([P, NOUT], U8, name="s2", align_bytes=64)
+        s2 = keep.tile([P, NOUT], U8, name="s2", align_bytes=256)
         xsc = keep.tile([P, 2, 4], F32, name="xsc")
 
         one = keep.tile([P, 2], F32, name="one")
@@ -55,21 +55,21 @@ def tile_geometricmanifoldnetwork_pa_w8_kernel(
         warm = keep.tile([P, 2], F32, name="warm")
         nc.scalar.activation(out=warm[:], in_=one[:], func=ACT.Abs_reciprocal_sqrt)
         nc.vector.memset(s1raw[:].bitcast(I32), 0)
-        ident = keep.tile([P, P], F32, name="ident", align_bytes=64)
+        ident = keep.tile([P, P], F32, name="ident", align_bytes=256)
         nc.vector.memset(ident[:], 0.0)
         make_identity(nc, ident[:], nomemset=True)
         nc.vector.memset(s2[:].bitcast(I32), 0)
-        b1rows = keep.tile([P, 2 * P], F32, name="b1rows", align_bytes=64)
+        b1rows = keep.tile([P, 2 * P], F32, name="b1rows", align_bytes=256)
         nc.vector.memset(b1rows[:], 0.0)
 
-        xbytes = [keep.tile([P, J * K], U8, name="xbytes%d" % c, align_bytes=64) for c, (i0, J) in enumerate(CHUNKS)]
-        late_raw = [keep.tile([P, HALF], U32, name="late_raw%d" % g, align_bytes=64) for g in BOTH]
-        late = [keep.tile([P, HALF], U32, name="late%d" % g, align_bytes=64) for g in BOTH]
-        early_raw = keep.tile([P, 2, HALF], U32, name="early_raw", align_bytes=64)
-        early = keep.tile([P, 2, HALF], U32, name="early", align_bytes=64)
-        w2 = keep.tile([P, 2, NOUT], U32, name="w2", align_bytes=64)
+        xbytes = [keep.tile([P, J * K], U8, name="xbytes%d" % c, align_bytes=256) for c, (i0, J) in enumerate(CHUNKS)]
+        late_raw = [keep.tile([P, HALF], U32, name="late_raw%d" % g, align_bytes=256) for g in BOTH]
+        late = [keep.tile([P, HALF], U32, name="late%d" % g, align_bytes=256) for g in BOTH]
+        early_raw = keep.tile([P, 2, HALF], U32, name="early_raw", align_bytes=256)
+        early = keep.tile([P, 2, HALF], U32, name="early", align_bytes=256)
+        w2 = keep.tile([P, 2, NOUT], U32, name="w2", align_bytes=256)
         b1t = keep.tile([P, 2, 4], BF16, name="b1t")
-        b2t = keep.tile([P, NOUT], BF16, name="b2t")
+        b2t = keep.tile([P, NOUT], BF16, name="b2t", align_bytes=256)
         w1i = W1_words.rearrange("g p n t -> p g (n t)").bitcast(I32)
         x_rows = x_bytes.rearrange("(p i) k -> p (i k)", i=len(TILES))
         out_rows = out.rearrange("(p i) o -> p i o", i=len(TILES))
@@ -139,13 +139,13 @@ def tile_geometricmanifoldnetwork_pa_w8_kernel(
             )
 
         def permute_early_s1():
-            s1[0] = keep.tile([P, HALF], U8, name="xv010", align_bytes=64)
+            s1[0] = keep.tile([P, HALF], U8, name="xv010", align_bytes=256)
             nc.gpsimd.tensor_copy(
                 out=s1[0][:].rearrange("p (t m) -> p t m", t=4), in_=s1raw[:, :HALF].rearrange("p (m t) -> p t m", t=4)
             )
 
         def permute_late_s1():
-            s1[1] = keep.tile([P, HALF], U8, name="s1_1", align_bytes=64)
+            s1[1] = keep.tile([P, HALF], U8, name="s1_1", align_bytes=256)
             nc.vector.tensor_copy(
                 out=s1[1][:].rearrange("p (t c i) -> p c t i", t=4, i=8),
                 in_=s1raw[:, HALF:].rearrange("p (c i t) -> p c t i", t=4, i=8),
@@ -166,7 +166,7 @@ def tile_geometricmanifoldnetwork_pa_w8_kernel(
 
         def cast(c, g, tiles=None):
             tiles = tiles or range(CHUNKS[c][1])
-            wide = keep.tile([P, len(tiles), 2, P], F32, name="xv%d%d%d" % (c, g, tiles[0]), align_bytes=64)
+            wide = keep.tile([P, len(tiles), 2, P], F32, name="xv%d%d%d" % (c, g, tiles[0]), align_bytes=256)
             codes = xbytes[c][:].bitcast(FP8).rearrange("p (j g m u e) -> p j g u m e", g=2, m=P, u=2, e=2)
             nc.scalar.copy(
                 out=wide[:].bitcast(BF16).rearrange("p j u (m e) -> p j u m e", e=2),
@@ -177,7 +177,7 @@ def tile_geometricmanifoldnetwork_pa_w8_kernel(
                     xv[c, g, j, u] = wide[:, a, u, :]
 
         def cast_first_tile(g):
-            wide = keep.tile([P, 2, P], F32, name="xv0%d0" % g, align_bytes=64)
+            wide = keep.tile([P, 2, P], F32, name="xv0%d0" % g, align_bytes=256)
             nc.vector.tensor_copy(
                 out=wide[:].bitcast(BF16).rearrange("p u (m e) -> p m u e", e=2),
                 in_=xbytes[0][:, HALF * g : HALF * g + HALF].bitcast(FP8).rearrange("p (m u e) -> p m u e", u=2, e=2),
@@ -186,7 +186,7 @@ def tile_geometricmanifoldnetwork_pa_w8_kernel(
                 xv[0, g, 0, u] = wide[:, u, :]
 
         def cast_on_gpsimd(c, g, j, name):
-            wide = keep.tile([P, HALF], BF16, name=name, align_bytes=64)
+            wide = keep.tile([P, HALF], BF16, name=name, align_bytes=256)
             first = K * j + HALF * g
             nc.gpsimd.tensor_copy(out=wide[:], in_=xbytes[c][:, first : first + HALF].bitcast(FP8))
             for u in BOTH:
@@ -262,7 +262,7 @@ def tile_geometricmanifoldnetwork_pa_w8_kernel(
 
         def woven(c, name=None):
             if c not in hg:
-                hg[c] = keep.tile([P, 2, 4 * P * CHUNKS[c][1]], BF16, name=name or "hg%d" % c, align_bytes=64)
+                hg[c] = keep.tile([P, 2, 4 * P * CHUNKS[c][1]], BF16, name=name or "hg%d" % c, align_bytes=256)
             return hg[c]
 
         def weave_h(c, Ts):
@@ -335,7 +335,7 @@ def tile_geometricmanifoldnetwork_pa_w8_kernel(
             nc.sync.dma_start(out=out_rows[:, i, cols], in_=scaled[:, cols])
 
         def finish_v(i, parts=(slice(0, NOUT),)):
-            scaled = keep.tile([P, NOUT], F32, name="o%d" % i, align_bytes=64)
+            scaled = keep.tile([P, NOUT], F32, name="o%d" % i, align_bytes=256)
             for cols in parts:
                 nc.vector.tensor_scalar(
                     out=scaled[:, cols], in0=v[i][:, cols], scalar1=r[:, i : i + 1], scalar2=None, op0=ALU.mult
@@ -343,12 +343,12 @@ def tile_geometricmanifoldnetwork_pa_w8_kernel(
                 store(i, scaled, cols)
 
         def finish_v_on_scalar(i):
-            scaled = keep.tile([P, NOUT], F32, name="o%d" % i, align_bytes=64)
+            scaled = keep.tile([P, NOUT], F32, name="o%d" % i, align_bytes=256)
             nc.scalar.activation(out=scaled[:], in_=v[i][:], func=ACT.Copy, scale=r[:, i : i + 1])
             store(i, scaled)
 
         def finish_v_on_gpsimd(i):
-            scaled = keep.tile([P, NOUT], F32, name="hg%d" % LAST, align_bytes=64)
+            scaled = keep.tile([P, NOUT], F32, name="hg%d" % LAST, align_bytes=256)
             nc.gpsimd.tensor_scalar(
                 out=scaled[:], in0=v[i][:], scalar1=r[:, i : i + 1], scalar2=0.0, op0=ALU.mult, op1=ALU.add
             )

@@ -91,7 +91,7 @@ def tile_geometricmanifoldnetwork_pa_w8_kernel(
                 )
 
         def load_x_scale():
-            nc.scalar.dma_start(out=xsc[:], in_=x_scale.rearrange("o (g p t) -> p (o g) t", g=2, t=4))
+            nc.sync.dma_start(out=xsc[:], in_=x_scale.rearrange("o (g p t) -> p (o g) t", g=2, t=4))
 
         def load_b1():
             words = b1.rearrange("(T k) -> T k", T=2).bitcast(F32)
@@ -105,6 +105,7 @@ def tile_geometricmanifoldnetwork_pa_w8_kernel(
             nc.sync.dma_start(out=b2t[:], in_=b2.partition_broadcast(P))
 
         xg, hp = each_chunk("xg", BF16, 4), each_chunk("hp", BF16, 4)
+        xg1 = [keep.tile([P, 1, 8 * P], BF16, name="xg1%d" % g, align_bytes=256) for g in BOTH]
         xq, hq = each_chunk("xq", U32, 1), each_chunk("hq", U32, 1)
         xs, hs = each_chunk("xs", U8, 1), each_chunk("hs", U8, 1)
         v, squares = each_tile("v", F32, NOUT), each_tile("squares", BF16, NOUT)
@@ -112,6 +113,7 @@ def tile_geometricmanifoldnetwork_pa_w8_kernel(
         over = keep.tile([P, len(TILES)], F32, name="over")
         floored = keep.tile([P, len(TILES)], F32, name="floored")
         r = keep.tile([P, len(TILES)], F32, name="r")
+        scaled_on_scalar = {}
         end_ssq = [keep.tile([P, 1], F32, name="end_ssq%d" % a) for a in BOTH]
         xv, xt, turned_b1, hbank, hg, py = {}, {}, {}, {}, {}, {}
 
@@ -126,10 +128,11 @@ def tile_geometricmanifoldnetwork_pa_w8_kernel(
         def give_bank(key):
             free_banks.append(held[key])
 
-        def permute_early_w1():
+        def permute_early_w1(gs=BOTH):
+            part = slice(gs[0], gs[-1] + 1)
             nc.vector.tensor_copy(
-                out=early[:].bitcast(I32).rearrange("p g (t c i) -> p g c t i", t=4, i=2),
-                in_=early_raw[:].bitcast(I32).rearrange("p g (c i t) -> p g c t i", t=4, i=2),
+                out=early[:, part].bitcast(I32).rearrange("p g (t c i) -> p g c t i", t=4, i=2),
+                in_=early_raw[:, part].bitcast(I32).rearrange("p g (c i t) -> p g c t i", t=4, i=2),
             )
 
         def permute_late_w1(g):
@@ -176,14 +179,15 @@ def tile_geometricmanifoldnetwork_pa_w8_kernel(
                 for u in BOTH:
                     xv[c, g, j, u] = wide[:, a, u, :]
 
-        def cast_first_tile(g):
-            wide = keep.tile([P, 2, P], F32, name="xv0%d0" % g, align_bytes=256)
+        def cast_on_vector(c, g, j):
+            wide = keep.tile([P, 2, P], F32, name="xv%d%d%d" % (c, g, j), align_bytes=256)
+            first = K * j + HALF * g
             nc.vector.tensor_copy(
                 out=wide[:].bitcast(BF16).rearrange("p u (m e) -> p m u e", e=2),
-                in_=xbytes[0][:, HALF * g : HALF * g + HALF].bitcast(FP8).rearrange("p (m u e) -> p m u e", u=2, e=2),
+                in_=xbytes[c][:, first : first + HALF].bitcast(FP8).rearrange("p (m u e) -> p m u e", u=2, e=2),
             )
             for u in BOTH:
-                xv[0, g, 0, u] = wide[:, u, :]
+                xv[c, g, j, u] = wide[:, u, :]
 
         def cast_on_gpsimd(c, g, j, name):
             wide = keep.tile([P, HALF], BF16, name=name, align_bytes=256)
@@ -199,26 +203,29 @@ def tile_geometricmanifoldnetwork_pa_w8_kernel(
                 for u in BOTH:
                     nc.tensor.transpose(xt[c, g][:, u, P * j : P * j + P], xv[c, g, j, u], ident[:])
 
-        def scale_x(c, g):
+        def scale_x(c, g, tiles=None):
+            tiles = tiles or range(CHUNKS[c][1])
+            part = slice(P * tiles[0], P * tiles[-1] + P)
             scales = xsc[:, g, :].rearrange("p (u e) -> p u e", u=2).unsqueeze(1)
             nc.vector.tensor_tensor(
-                out=xg[c][:, g, :].rearrange("p (n u e) -> p n u e", u=2, e=2),
-                in0=xt[c, g][:].bitcast(BF16).rearrange("p u (n e) -> p n u e", e=2),
-                in1=scales.to_broadcast([P, P * CHUNKS[c][1], 2, 2]),
+                out=(xg[c][:, g, :] if c != 1 else xg1[g][:, 0, :]).rearrange("p (n u e) -> p n u e", u=2, e=2)[:, part],
+                in0=xt[c, g][:].bitcast(BF16).rearrange("p u (n e) -> p n u e", e=2)[:, part],
+                in1=scales.to_broadcast([P, P * len(tiles), 2, 2]),
                 op=ALU.mult,
             )
-            give_bank(("x", c, g))
+            if tiles[-1] == CHUNKS[c][1] - 1:
+                give_bank(("x", c, g))
 
         def quantise(codes, scales, values, gs):
             part = slice(gs[0], gs[-1] + 1)
             nc.vector.quantize_mx(
                 out=codes[:, part, :].rearrange("p g n -> p (g n)").bitcast(FP8X4),
                 scales=scales[:, part, :].rearrange("p g n -> p (g n)"),
-                in_=values[:, part, :].rearrange("p g n -> p (g n)"),
+                in_=values.rearrange("p g n -> p (g n)"),
             )
 
         def quant_x(c, gs=BOTH):
-            quantise(xq[c], xs[c], xg[c], gs)
+            quantise(xq[c], xs[c], xg[c][:, gs[0] : gs[-1] + 1, :] if c != 1 else xg1[gs[0]][:], gs)
 
         def stage1(c, T, ts=range(4)):
             n = P * CHUNKS[c][1]
@@ -237,10 +244,10 @@ def tile_geometricmanifoldnetwork_pa_w8_kernel(
                         stop=(g == 1),
                     )
 
-        def relu(c, T):
+        def relu(c, T, ts=range(4)):
             n = P * CHUNKS[c][1]
             per_bank = HALF // n
-            for t in range(4):
+            for t in ts:
                 nc.scalar.activation(
                     out=hp[c][:, T, n * t : n * t + n],
                     in_=hbank[c, T, t // per_bank][:, t % per_bank, :],
@@ -250,48 +257,54 @@ def tile_geometricmanifoldnetwork_pa_w8_kernel(
                 if (t + 1) % per_bank == 0:
                     give_bank(("h", c, T, t // per_bank))
 
-        def relu_in_pairs(c, T):
+        def relu_in_pairs(c, T, ts=range(4)):
             n = P * CHUNKS[c][1]
             per_bank = HALF // n
-            for t in range(4):
+            for t in ts:
                 dst = hp[c][:, T, 2 * n * (t // 2) + t % 2 : 2 * n * (t // 2 + 1) : 2]
                 src = hbank[c, T, t // per_bank][:, t % per_bank, :]
                 nc.scalar.activation(out=dst, in_=src, func=ACT.Relu, bias=b1t[:, T, t : t + 1])
                 if (t + 1) % per_bank == 0:
                     give_bank(("h", c, T, t // per_bank))
 
-        def woven(c, name=None):
-            if c not in hg:
-                hg[c] = keep.tile([P, 2, 4 * P * CHUNKS[c][1]], BF16, name=name or "hg%d" % c, align_bytes=256)
-            return hg[c]
+        def woven(c, Ts, name=None, both=True):
+            if (c, Ts[0]) not in hg:
+                held_Ts = BOTH if both else Ts
+                whole = keep.tile(
+                    [P, len(held_Ts), 4 * P * CHUNKS[c][1]], BF16, name=name or "hg%d%d" % (c, Ts[0]), align_bytes=256
+                )
+                for a, T in enumerate(held_Ts):
+                    hg[c, T] = (whole, a)
+            whole, a = hg[c, Ts[0]]
+            return whole[:, a : a + len(Ts), :]
 
-        def weave_h(c, Ts):
+        def weave_h(c, Ts, first=0, both=True):
             part = slice(Ts[0], Ts[-1] + 1)
             nc.vector.tensor_copy(
-                out=woven(c)[:, part, :].rearrange("p T (c i t) -> p T c t i", i=4, t=4),
-                in_=hp[c][:, part, :].rearrange("p T (t c i) -> p T c t i", i=4, t=4),
+                out=woven(c, Ts, None, both).rearrange("p T (c i t) -> p T c t i", i=4, t=4)[:, :, first // 4 :],
+                in_=hp[c][:, part, :].rearrange("p T (t c i) -> p T c t i", i=4, t=4)[:, :, first // 4 :],
             )
 
-        def weave_pairs(c, Ts):
+        def weave_pairs(c, Ts, both=True):
             part = slice(Ts[0], Ts[-1] + 1)
             nc.vector.tensor_copy(
-                out=woven(c)[:, part, :].bitcast(F32).rearrange("p T (n u) -> p T n u", u=2),
+                out=woven(c, Ts, None, both).bitcast(F32).rearrange("p T (n u) -> p T n u", u=2),
                 in_=hp[c][:, part, :].bitcast(F32).rearrange("p T (u n) -> p T n u", u=2),
             )
 
-        def weave_h_on_gpsimd(c, Ts, name=None):
+        def weave_h_on_gpsimd(c, Ts, name=None, tokens=None, both=True):
             part = slice(Ts[0], Ts[-1] + 1)
             nc.gpsimd.tensor_scalar(
-                out=woven(c, name)[:, part, :].rearrange("p T (n t) -> p T n t", t=4),
-                in0=hp[c][:, part, :].rearrange("p T (t n) -> p T n t", t=4),
+                out=woven(c, Ts, name, both).rearrange("p T (n t) -> p T n t", t=4)[:, :, :tokens],
+                in0=hp[c][:, part, :].rearrange("p T (t n) -> p T n t", t=4)[:, :, :tokens],
                 scalar1=1.0,
                 scalar2=0.0,
                 op0=ALU.mult,
                 op1=ALU.add,
             )
 
-        def quant_h(c):
-            quantise(hq[c], hs[c], hg[c], BOTH)
+        def quant_h(c, Ts=BOTH):
+            quantise(hq[c], hs[c], woven(c, Ts), Ts)
 
         def stage2_pass(dst, i, T, cols):
             c, j = TILES[i]
@@ -305,9 +318,10 @@ def tile_geometricmanifoldnetwork_pa_w8_kernel(
                 stop=(T == 1),
             )
 
-        def stage2(i):
-            py[i] = take_bank(("y", i), [P, NOUT])
-            for T in BOTH:
+        def stage2(i, Ts=BOTH):
+            if 0 in Ts:
+                py[i] = take_bank(("y", i), [P, NOUT])
+            for T in Ts:
                 stage2_pass(py[i][:], i, T, slice(0, NOUT))
 
         def bias_v(i):
@@ -342,13 +356,16 @@ def tile_geometricmanifoldnetwork_pa_w8_kernel(
                 )
                 store(i, scaled, cols)
 
-        def finish_v_on_scalar(i):
-            scaled = keep.tile([P, NOUT], F32, name="o%d" % i, align_bytes=256)
-            nc.scalar.activation(out=scaled[:], in_=v[i][:], func=ACT.Copy, scale=r[:, i : i + 1])
-            store(i, scaled)
+        def finish_v_on_scalar(i, cols=slice(0, NOUT)):
+            if i not in scaled_on_scalar:
+                scaled_on_scalar[i] = keep.tile([P, NOUT], F32, name="o%d" % i, align_bytes=256)
+            scaled = scaled_on_scalar[i]
+            nc.scalar.activation(out=scaled[:, cols], in_=v[i][:, cols], func=ACT.Copy, scale=r[:, i : i + 1])
+            if cols.stop == NOUT:
+                store(i, scaled)
 
-        def finish_v_on_gpsimd(i):
-            scaled = keep.tile([P, NOUT], F32, name="hg%d" % LAST, align_bytes=256)
+        def finish_v_on_gpsimd(i, name="hg%d0" % LAST):
+            scaled = keep.tile([P, NOUT], F32, name=name, align_bytes=256)
             nc.gpsimd.tensor_scalar(
                 out=scaled[:], in0=v[i][:], scalar1=r[:, i : i + 1], scalar2=0.0, op0=ALU.mult, op1=ALU.add
             )
@@ -356,8 +373,8 @@ def tile_geometricmanifoldnetwork_pa_w8_kernel(
 
         sides = [slice(NOUT // 2 * a, NOUT // 2 * (a + 1)) for a in BOTH]
 
-        def end_stage2():
-            for T in BOTH:
+        def end_stage2(Ts=BOTH):
+            for T in Ts:
                 for a in BOTH:
                     if T == 0:
                         py[END, a] = take_bank(("y", END, a), [P, NOUT // 2])
@@ -391,21 +408,18 @@ def tile_geometricmanifoldnetwork_pa_w8_kernel(
         def end_root():
             nc.scalar.activation(out=r[:, END:], in_=ssq[:, END:], func=ACT.Abs_reciprocal_sqrt)
 
-
         load_x(0)
         load_x(1)
-        load_scales(s1raw, W1_scales)
         load_x_scale()
+        load_scales(s1raw, W1_scales)
         load_x(2)
         load_early_w1()
         load_b1()
         load_late_w1(0)
         load_late_w1(1)
-
-
         warm_tensor(2)
-        cast_first_tile(0)
-        cast_first_tile(1)
+        cast(0,0)
+        cast_on_vector(0,1,0)
         turn(0, 0)
         turn(0, 1)
         warm_tensor(1)
@@ -442,7 +456,7 @@ def tile_geometricmanifoldnetwork_pa_w8_kernel(
         cast(3, 0)
         stage1(0, 1)
         quant_x(1, (1,))
-        cast_on_gpsimd(3, 1, 1, "xg1")
+        cast_on_gpsimd(3, 1, 1, "xg10")
         relu(0, 0)
         stage1(1, 0)
         scale_x(2, 0)

@@ -135,6 +135,12 @@ def tile_geometricmanifoldnetwork_pa_w8_kernel(
                 in_=early_raw[:, part].bitcast(I32).rearrange("p g (c i t) -> p g c t i", t=4, i=2),
             )
 
+        def permute_early_w1_on_scalar(g):
+            nc.scalar.copy(
+                out=early[:, g].rearrange("p (t c i) -> p c t i", t=4, i=2),
+                in_=early_raw[:, g].rearrange("p (c i t) -> p c t i", t=4, i=2),
+            )
+
         def permute_late_w1(g):
             nc.scalar.copy(
                 out=late[g][:].rearrange("p (t c i) -> p c t i", t=4, i=2),
@@ -441,37 +447,38 @@ def tile_geometricmanifoldnetwork_pa_w8_kernel(
         cast(2, 0)
         cast(2, 1)
         quant_x(0)
+        permute_early_w1_on_scalar(1)
         permute_late_s1()
-        permute_early_w1()
+        permute_early_w1((0,))
         turn(2, 0)
         turn_b1()
         warm_tensor(1)
         turn(2, 1)
         permute_late_w1(0)
+        empty_b1()
         stage1(0, 0)
         scale_x(1, 1)
         permute_late_w1(1)
-        empty_b1()
         quant_x(1, (0,))
-        cast(3, 0)
         stage1(0, 1)
         quant_x(1, (1,))
-        cast_on_gpsimd(3, 1, 1, "xg10")
-        relu(0, 0)
-        stage1(1, 0)
-        scale_x(2, 0)
-        cast(3, 1, (0,))
-        weave_h_on_gpsimd(0, (0,))
-        scale_x(2, 1)
-        relu_in_pairs(0, 1)
-        stage1(1, 1)
-        turn(3, 0)
-        quant_x(2, (0,))
-        weave_pairs(0, (1,))
-        quant_x(2, (1,))
-        relu(1, 0)
+        cast_on_gpsimd(3,1,1,"xg10")
+        relu(0,0)
+        cast(3,0)
+        stage1(1,0)
+        scale_x(2,0)
+        weave_h_on_gpsimd(0,(0,))
+        relu(0,1)
+        cast(3,1,(0,))
+        scale_x(2,1)
+        stage1(1,1)
+        turn(3,0)
+        relu(1,0)
+        quant_x(2,(0,))
+        weave_h(0,(1,))
+        quant_x(2,(1,))
         quant_h(0)
-        turn(3, 1)
+        turn(3,1)
         weave_h_on_gpsimd(1, (0,), "xg2")
         relu(1, 1)
         cast(4, 0)
@@ -479,13 +486,14 @@ def tile_geometricmanifoldnetwork_pa_w8_kernel(
         stage1(2, 0)
         stage2(0)
         scale_x(3, 0)
-        weave_h_on_gpsimd(1, (1,))
+        weave_h_on_gpsimd(1,(1,),None,192)
         stage1(2, 1)
         scale_x(3, 1)
         relu(2, 0)
         bias_v(0)
         turn(4, 0)
         turn(4, 1)
+        weave_h(1,(1,),192)
         quant_x(3)
         quant_h(1)
         stage1(3, 0, (0, 1))

@@ -474,9 +474,8 @@ def tile_geometricmanifoldnetwork_pa_w8_kernel(
         stage1(1,1)
         turn(3,0)
         relu(1,0)
-        quant_x(2,(0,))
         weave_h(0,(1,))
-        quant_x(2,(1,))
+        quant_x(2)
         quant_h(0)
         turn(3,1)
         weave_h_on_gpsimd(1, (0,), "xg2")
@@ -486,14 +485,13 @@ def tile_geometricmanifoldnetwork_pa_w8_kernel(
         stage1(2, 0)
         stage2(0)
         scale_x(3, 0)
-        weave_h_on_gpsimd(1,(1,),None,192)
+        weave_h_on_gpsimd(1, (1,))
         stage1(2, 1)
         scale_x(3, 1)
         relu(2, 0)
         bias_v(0)
         turn(4, 0)
         turn(4, 1)
-        weave_h(1,(1,),192)
         quant_x(3)
         quant_h(1)
         stage1(3, 0, (0, 1))
@@ -527,30 +525,33 @@ def tile_geometricmanifoldnetwork_pa_w8_kernel(
         bias_v(3)
         quant_h(3)
         stage2(5)
-        relu(4, 1)
-        clamp_v(1, 3)
+        relu(4,1)
+        clamp_v(1,3)
         square_v(3)
         bias_v(4)
         finish_v(0)
         stage2(6)
-        root_v(1, 3)
-        weave_h(4, BOTH)
+        root_v(1,3)
+        weave_h(4,BOTH)
         square_v(4)
         finish_v(1)
-        clamp_v(3, 5)
+        clamp_v(3,4)
+        finish_v_on_scalar(2,sides[0])
+        root_v(3,4)
+        clamp_v(4,5)
+        finish_v_on_scalar(2,sides[1])
         quant_h(4)
-        root_v(3, 5)
-        finish_v_on_scalar(2)
+        root_v(4,5)
+        finish_v_on_scalar(3)
         end_stage2()
         bias_v(5)
-        finish_v_on_gpsimd(3)
+        finish_v_on_gpsimd(4)
         square_v(5)
         bias_v(6)
         end_bias(0)
         square_v(6)
         end_bias(1)
         clamp_on_vector(5)
-        finish_v(4)
         root_of_floored(5)
         end_square_on_vector(1)
         end_square_on_scalar(0)

from contextlib import ExitStack

import concourse.mybir as mybir
from concourse.masks import make_identity

FLOPS = 2 * 1024 * 1024 * 1024 + 2 * 1024 * 1024 * 512

F32 = mybir.dt.float32
BF16 = mybir.dt.bfloat16
U32 = mybir.dt.uint32
I32 = mybir.dt.int32
U8 = mybir.dt.uint8
FP8 = mybir.dt.float8_e4m3fn
FP8X4 = mybir.dt.float8_e4m3fn_x4
ACT = mybir.ActivationFunctionType
ALU = mybir.AluOpType

P = 128
K = 1024
HALF = 512
NOUT = 512
EPS2 = 1e-24
BOTH = (0, 1)
CHUNKS = ((0, 1), (1, 2), (3, 2), (5, 2), (7, 1))
LAST = len(CHUNKS) - 1
TILES = [(c, j) for c in range(len(CHUNKS)) for j in range(CHUNKS[c][1])]
END = len(TILES) - 1


def tile_geometricmanifoldnetwork_pa_w8_kernel(
    tc, x_bytes, x_scale, W1_words, W1_scales, b1, W2_words, W2_scales, b2, out
):
    nc = tc.nc
    with ExitStack() as ctx:
        keep = ctx.enter_context(tc.tile_pool(name="keep", bufs=1))
        psum = ctx.enter_context(tc.psum_pool(name="psum", bufs=1))
        ctx.enter_context(tc.manual_schedule())

        def each_chunk(name, dtype, per_token):
            return [
                keep.tile([P, 2, per_token * P * J], dtype, name="%s%d" % (name, c), align_bytes=256)
                for c, (i0, J) in enumerate(CHUNKS)
            ]

        def each_tile(name, dtype, columns):
            return [keep.tile([P, columns], dtype, name="%s%d" % (name, i), align_bytes=256) for i in range(len(TILES))]

        s1raw = keep.tile([P, K], U8, name="s1raw", align_bytes=256)
        s1 = {}
        s2 = keep.tile([P, NOUT], U8, name="s2", align_bytes=256)
        xsc = keep.tile([P, 2, 4], F32, name="xsc")

        one = keep.tile([P, 2], F32, name="one")
        nc.vector.memset(one[:], 1.0)
        warm = keep.tile([P, 2], F32, name="warm")
        nc.scalar.activation(out=warm[:], in_=one[:], func=ACT.Abs_reciprocal_sqrt)
        nc.vector.memset(s1raw[:].bitcast(I32), 0)
        ident = keep.tile([P, P], F32, name="ident", align_bytes=256)
        nc.vector.memset(ident[:], 0.0)
        make_identity(nc, ident[:], nomemset=True)
        nc.vector.memset(s2[:].bitcast(I32), 0)
        b1rows = keep.tile([P, 2 * P], F32, name="b1rows", align_bytes=256)
        nc.vector.memset(b1rows[:], 0.0)

        xbytes = [keep.tile([P, J * K], U8, name="xbytes%d" % c, align_bytes=256) for c, (i0, J) in enumerate(CHUNKS)]
        late_raw = [keep.tile([P, HALF], U32, name="late_raw%d" % g, align_bytes=256) for g in BOTH]
        late = [keep.tile([P, HALF], U32, name="late%d" % g, align_bytes=256) for g in BOTH]
        early_raw = keep.tile([P, 2, HALF], U32, name="early_raw", align_bytes=256)
        early = keep.tile([P, 2, HALF], U32, name="early", align_bytes=256)
        w2 = keep.tile([P, 2, NOUT], U32, name="w2", align_bytes=256)
        b1t = keep.tile([P, 2, 4], BF16, name="b1t")
        b2t = keep.tile([P, NOUT], BF16, name="b2t", align_bytes=256)
        w1i = W1_words.rearrange("g p n t -> p g (n t)").bitcast(I32)
        x_rows = x_bytes.rearrange("(p i) k -> p (i k)", i=len(TILES))
        out_rows = out.rearrange("(p i) o -> p i o", i=len(TILES))

        def load_x(c):
            i0, J = CHUNKS[c]
            nc.sync.dma_start(out=xbytes[c][:], in_=x_rows[:, K * i0 : K * (i0 + J)])

        def load_late_w1(g):
            nc.sync.dma_start(out=late_raw[g][:].bitcast(I32), in_=w1i[:, g, HALF:])

        def load_early_w1():
            nc.sync.dma_start(out=early_raw[:].bitcast(I32), in_=w1i[:, :, :HALF])

        def load_scales(dst, src):
            for Q in range(4):
                nc.sync.dma_start(
                    out=dst[32 * Q : 32 * Q + 8, :].bitcast(I32), in_=src[:, 4 * Q : 4 * Q + 4, :].bitcast(I32)
                )

        def load_x_scale():
            nc.sync.dma_start(out=xsc[:], in_=x_scale.rearrange("o (g p t) -> p (o g) t", g=2, t=4))

        def load_b1():
            words = b1.rearrange("(T k) -> T k", T=2).bitcast(F32)
            for u in BOTH:
                nc.sync.dma_start(out=b1rows[2 * u : 2 * u + 2, : 2 * P - 1], in_=words[:, u : u + 2 * P - 1])

        def load_w2():
            nc.sync.dma_start(out=w2[:].bitcast(I32), in_=W2_words.rearrange("g p n t -> p g (n t)").bitcast(I32))

        def load_b2():
            nc.sync.dma_start(out=b2t[:], in_=b2.partition_broadcast(P))

        xg, hp = each_chunk("xg", BF16, 4), each_chunk("hp", BF16, 4)
        xg1 = [keep.tile([P, 1, 8 * P], BF16, name="xg1%d" % g, align_bytes=256) for g in BOTH]
        xq, hq = each_chunk("xq", U32, 1), each_chunk("hq", U32, 1)
        xs, hs = each_chunk("xs", U8, 1), each_chunk("hs", U8, 1)
        v, squares = each_tile("v", F32, NOUT), each_tile("squares", BF16, NOUT)
        ssq = keep.tile([P, len(TILES)], F32, name="ssq")
        over = keep.tile([P, len(TILES)], F32, name="over")
        floored = keep.tile([P, len(TILES)], F32, name="floored")
        r = keep.tile([P, len(TILES)], F32, name="r")
        scaled_on_scalar = {}
        end_ssq = [keep.tile([P, 1], F32, name="end_ssq%d" % a) for a in BOTH]
        xv, xt, turned_b1, hbank, hg, py = {}, {}, {}, {}, {}, {}

        free_banks = ["bank%d" % b for b in range(8)]
        held = {}

        def take_bank(key, shape):
            held[key] = free_banks[0]
            free_banks.remove(held[key])
            return psum.tile(shape, F32, name=held[key])

        def give_bank(key):
            free_banks.append(held[key])

        def permute_early_w1(gs=BOTH):
            part = slice(gs[0], gs[-1] + 1)
            nc.vector.tensor_copy(
                out=early[:, part].bitcast(I32).rearrange("p g (t c i) -> p g c t i", t=4, i=2),
                in_=early_raw[:, part].bitcast(I32).rearrange("p g (c i t) -> p g c t i", t=4, i=2),
            )

        def permute_early_w1_on_scalar(g):
            nc.scalar.copy(
                out=early[:, g].rearrange("p (t c i) -> p c t i", t=4, i=2),
                in_=early_raw[:, g].rearrange("p (c i t) -> p c t i", t=4, i=2),
            )

        def permute_late_w1(g):
            nc.scalar.copy(
                out=late[g][:].rearrange("p (t c i) -> p c t i", t=4, i=2),
                in_=late_raw[g][:].rearrange("p (c i t) -> p c t i", t=4, i=2),
            )

        def permute_early_s1():
            s1[0] = keep.tile([P, HALF], U8, name="xv010", align_bytes=256)
            nc.gpsimd.tensor_copy(
                out=s1[0][:].rearrange("p (t m) -> p t m", t=4), in_=s1raw[:, :HALF].rearrange("p (m t) -> p t m", t=4)
            )

        def permute_late_s1():
            s1[1] = keep.tile([P, HALF], U8, name="s1_1", align_bytes=256)
            nc.vector.tensor_copy(
                out=s1[1][:].rearrange("p (t c i) -> p c t i", t=4, i=8),
                in_=s1raw[:, HALF:].rearrange("p (c i t) -> p c t i", t=4, i=8),
            )

        def turn_b1():
            turned_b1[0] = take_bank("b1", [P, P])
            nc.tensor.transpose(turned_b1[0][:], b1rows[:, : 2 * P - 1 : 2], ident[:])

        def empty_b1():
            nc.scalar.copy(out=b1t[:].bitcast(F32), in_=turned_b1[0][:, :4].rearrange("p (u T) -> p T u", u=2))
            give_bank("b1")

        def warm_tensor(count):
            sink = psum.tile([P, P], F32, name="bank7")
            for a in range(count):
                nc.tensor.matmul(sink[:], lhsT=ident[:], rhs=ident[:], start=True, stop=True)

        def cast(c, g, tiles=None):
            tiles = tiles or range(CHUNKS[c][1])
            wide = keep.tile([P, len(tiles), 2, P], F32, name="xv%d%d%d" % (c, g, tiles[0]), align_bytes=256)
            codes = xbytes[c][:].bitcast(FP8).rearrange("p (j g m u e) -> p j g u m e", g=2, m=P, u=2, e=2)
            nc.scalar.copy(
                out=wide[:].bitcast(BF16).rearrange("p j u (m e) -> p j u m e", e=2),
                in_=codes[:, tiles[0] : tiles[-1] + 1, g],
            )
            for a, j in enumerate(tiles):
                for u in BOTH:
                    xv[c, g, j, u] = wide[:, a, u, :]

        def cast_on_vector(c, g, j):
            wide = keep.tile([P, 2, P], F32, name="xv%d%d%d" % (c, g, j), align_bytes=256)
            first = K * j + HALF * g
            nc.vector.tensor_copy(
                out=wide[:].bitcast(BF16).rearrange("p u (m e) -> p m u e", e=2),
                in_=xbytes[c][:, first : first + HALF].bitcast(FP8).rearrange("p (m u e) -> p m u e", u=2, e=2),
            )
            for u in BOTH:
                xv[c, g, j, u] = wide[:, u, :]

        def cast_on_gpsimd(c, g, j, name):
            wide = keep.tile([P, HALF], BF16, name=name, align_bytes=256)
            first = K * j + HALF * g
            nc.gpsimd.tensor_copy(out=wide[:], in_=xbytes[c][:, first : first + HALF].bitcast(FP8))
            for u in BOTH:
                xv[c, g, j, u] = wide[:].bitcast(F32)[:, u::2]

        def turn(c, g):
            J = CHUNKS[c][1]
            xt[c, g] = take_bank(("x", c, g), [P, 2, J * P])
            for j in range(J):
                for u in BOTH:
                    nc.tensor.transpose(xt[c, g][:, u, P * j : P * j + P], xv[c, g, j, u], ident[:])

        def scale_x(c, g, tiles=None):
            tiles = tiles or range(CHUNKS[c][1])
            part = slice(P * tiles[0], P * tiles[-1] + P)
            scales = xsc[:, g, :].rearrange("p (u e) -> p u e", u=2).unsqueeze(1)
            nc.vector.tensor_tensor(
                out=(xg[c][:, g, :] if c != 1 else xg1[g][:, 0, :]).rearrange("p (n u e) -> p n u e", u=2, e=2)[:, part],
                in0=xt[c, g][:].bitcast(BF16).rearrange("p u (n e) -> p n u e", e=2)[:, part],
                in1=scales.to_broadcast([P, P * len(tiles), 2, 2]),
                op=ALU.mult,
            )
            if tiles[-1] == CHUNKS[c][1] - 1:
                give_bank(("x", c, g))

        def quantise(codes, scales, values, gs):
            part = slice(gs[0], gs[-1] + 1)
            nc.vector.quantize_mx(
                out=codes[:, part, :].rearrange("p g n -> p (g n)").bitcast(FP8X4),
                scales=scales[:, part, :].rearrange("p g n -> p (g n)"),
                in_=values.rearrange("p g n -> p (g n)"),
            )

        def quant_x(c, gs=BOTH):
            quantise(xq[c], xs[c], xg[c][:, gs[0] : gs[-1] + 1, :] if c != 1 else xg1[gs[0]][:], gs)

        def stage1(c, T, ts=range(4)):
            n = P * CHUNKS[c][1]
            per_bank = HALF // n
            for t in ts:
                if t % per_bank == 0:
                    hbank[c, T, t // per_bank] = take_bank(("h", c, T, t // per_bank), [P, per_bank, n])
                for g in BOTH:
                    nc.tensor.matmul_mx(
                        out=hbank[c, T, t // per_bank][:, t % per_bank, :],
                        lhsT=(late[g] if T else early[:, g, :])[:, P * t : P * t + P].bitcast(FP8X4),
                        lhsT_scale=s1[T][4 * g :, P * t : P * t + P],
                        rhs=xq[c][:, g, :].bitcast(FP8X4),
                        rhs_scale=xs[c][:, g, :],
                        start=(g == 0),
                        stop=(g == 1),
                    )

        def relu(c, T, ts=range(4)):
            n = P * CHUNKS[c][1]
            per_bank = HALF // n
            for t in ts:
                nc.scalar.activation(
                    out=hp[c][:, T, n * t : n * t + n],
                    in_=hbank[c, T, t // per_bank][:, t % per_bank, :],
                    func=ACT.Relu,
                    bias=b1t[:, T, t : t + 1],
                )
                if (t + 1) % per_bank == 0:
                    give_bank(("h", c, T, t // per_bank))

        def relu_in_pairs(c, T, ts=range(4)):
            n = P * CHUNKS[c][1]
            per_bank = HALF // n
            for t in ts:
                dst = hp[c][:, T, 2 * n * (t // 2) + t % 2 : 2 * n * (t // 2 + 1) : 2]
                src = hbank[c, T, t // per_bank][:, t % per_bank, :]
                nc.scalar.activation(out=dst, in_=src, func=ACT.Relu, bias=b1t[:, T, t : t + 1])
                if (t + 1) % per_bank == 0:
                    give_bank(("h", c, T, t // per_bank))

        def woven(c, Ts, name=None, both=True):
            if (c, Ts[0]) not in hg:
                held_Ts = BOTH if both else Ts
                whole = keep.tile(
                    [P, len(held_Ts), 4 * P * CHUNKS[c][1]], BF16, name=name or "hg%d%d" % (c, Ts[0]), align_bytes=256
                )
                for a, T in enumerate(held_Ts):
                    hg[c, T] = (whole, a)
            whole, a = hg[c, Ts[0]]
            return whole[:, a : a + len(Ts), :]

        def weave_h(c, Ts, first=0, both=True):
            part = slice(Ts[0], Ts[-1] + 1)
            nc.vector.tensor_copy(
                out=woven(c, Ts, None, both).rearrange("p T (c i t) -> p T c t i", i=4, t=4)[:, :, first // 4 :],
                in_=hp[c][:, part, :].rearrange("p T (t c i) -> p T c t i", i=4, t=4)[:, :, first // 4 :],
            )

        def weave_pairs(c, Ts, both=True):
            part = slice(Ts[0], Ts[-1] + 1)
            nc.vector.tensor_copy(
                out=woven(c, Ts, None, both).bitcast(F32).rearrange("p T (n u) -> p T n u", u=2),
                in_=hp[c][:, part, :].bitcast(F32).rearrange("p T (u n) -> p T n u", u=2),
            )

        def weave_h_on_gpsimd(c, Ts, name=None, tokens=None, both=True):
            part = slice(Ts[0], Ts[-1] + 1)
            nc.gpsimd.tensor_scalar(
                out=woven(c, Ts, name, both).rearrange("p T (n t) -> p T n t", t=4)[:, :, :tokens],
                in0=hp[c][:, part, :].rearrange("p T (t n) -> p T n t", t=4)[:, :, :tokens],
                scalar1=1.0,
                scalar2=0.0,
                op0=ALU.mult,
                op1=ALU.add,
            )

        def quant_h(c, Ts=BOTH):
            quantise(hq[c], hs[c], woven(c, Ts), Ts)

        def stage2_pass(dst, i, T, cols):
            c, j = TILES[i]
            nc.tensor.matmul_mx(
                out=dst,
                lhsT=hq[c][:, T, P * j : P * j + P].bitcast(FP8X4),
                lhsT_scale=hs[c][:, T, P * j : P * j + P],
                rhs=w2[:, T, cols].bitcast(FP8X4),
                rhs_scale=s2[4 * T :, cols],
                start=(T == 0),
                stop=(T == 1),
            )

        def stage2(i, Ts=BOTH):
            if 0 in Ts:
                py[i] = take_bank(("y", i), [P, NOUT])
            for T in Ts:
                stage2_pass(py[i][:], i, T, slice(0, NOUT))

        def bias_v(i):
            nc.vector.tensor_tensor(out=v[i][:], in0=py[i][:], in1=b2t[:], op=ALU.add)
            give_bank(("y", i))

        def square_v(i):
            nc.scalar.activation(out=squares[i][:], in_=v[i][:], func=ACT.Square, accum_out=ssq[:, i : i + 1])

        def clamp_v(a, b):
            nc.scalar.activation(out=over[:, a:b], in_=ssq[:, a:b], func=ACT.Relu, bias=-EPS2)

        def root_v(a, b):
            nc.scalar.activation(out=r[:, a:b], in_=over[:, a:b], func=ACT.Abs_reciprocal_sqrt, bias=EPS2)

        def clamp_on_vector(i):
            nc.vector.tensor_scalar(
                out=floored[:, i : i + 1], in0=ssq[:, i : i + 1], scalar1=EPS2, scalar2=None, op0=ALU.max
            )

        def root_of_floored(i):
            nc.scalar.activation(out=r[:, i : i + 1], in_=floored[:, i : i + 1], func=ACT.Abs_reciprocal_sqrt)

        def store(i, scaled, cols=slice(0, NOUT)):
            nc.sync.dma_start(out=out_rows[:, i, cols], in_=scaled[:, cols])

        def finish_v(i, parts=(slice(0, NOUT),)):
            scaled = keep.tile([P, NOUT], F32, name="o%d" % i, align_bytes=256)
            for cols in parts:
                nc.vector.tensor_scalar(
                    out=scaled[:, cols], in0=v[i][:, cols], scalar1=r[:, i : i + 1], scalar2=None, op0=ALU.mult
                )
                store(i, scaled, cols)

        def finish_v_on_scalar(i, cols=slice(0, NOUT)):
            if i not in scaled_on_scalar:
                scaled_on_scalar[i] = keep.tile([P, NOUT], F32, name="o%d" % i, align_bytes=256)
            scaled = scaled_on_scalar[i]
            nc.scalar.activation(out=scaled[:, cols], in_=v[i][:, cols], func=ACT.Copy, scale=r[:, i : i + 1])
            if cols.stop == NOUT:
                store(i, scaled)

        def finish_v_on_gpsimd(i, name="hg%d0" % LAST):
            scaled = keep.tile([P, NOUT], F32, name=name, align_bytes=256)
            nc.gpsimd.tensor_scalar(
                out=scaled[:], in0=v[i][:], scalar1=r[:, i : i + 1], scalar2=0.0, op0=ALU.mult, op1=ALU.add
            )
            store(i, scaled)

        sides = [slice(NOUT // 2 * a, NOUT // 2 * (a + 1)) for a in BOTH]

        def end_stage2(Ts=BOTH):
            for T in Ts:
                for a in BOTH:
                    if T == 0:
                        py[END, a] = take_bank(("y", END, a), [P, NOUT // 2])
                    stage2_pass(py[END, a][:], END, T, sides[a])

        def end_bias(a):
            nc.vector.tensor_tensor(out=v[END][:, sides[a]], in0=py[END, a][:], in1=b2t[:, sides[a]], op=ALU.add)
            give_bank(("y", END, a))

        def end_square_on_scalar(a):
            nc.scalar.activation(
                out=squares[END][:, sides[a]], in_=v[END][:, sides[a]], func=ACT.Square, accum_out=end_ssq[a][:]
            )

        def end_square_on_vector(a):
            nc.vector.scalar_tensor_tensor(
                out=squares[END][:, sides[a]],
                in0=v[END][:, sides[a]],
                scalar=1.0,
                in1=v[END][:, sides[a]],
                op0=ALU.mult,
                op1=ALU.mult,
                accum_out=end_ssq[a][:],
            )

        def end_sum_and_clamp():
            nc.vector.tensor_scalar(
                out=ssq[:, END:], in0=end_ssq[0][:], scalar1=end_ssq[1][:], scalar2=EPS2, op0=ALU.add, op1=ALU.max
            )

        def end_root():
            nc.scalar.activation(out=r[:, END:], in_=ssq[:, END:], func=ACT.Abs_reciprocal_sqrt)

        load_x(0)
        load_x(1)
        load_x_scale()
        load_scales(s1raw, W1_scales)
        load_x(2)
        load_early_w1()
        load_b1()
        load_late_w1(0)
        load_late_w1(1)
        warm_tensor(2)
        cast(0,0)
        cast_on_vector(0,1,0)
        turn(0, 0)
        turn(0, 1)
        warm_tensor(1)
        permute_early_s1()
        cast(1, 0)
        turn(1, 0)
        warm_tensor(1)
        scale_x(0, 0)
        cast(1, 1)
        load_x(3)
        load_x(4)
        load_w2()
        load_scales(s2, W2_scales)
        load_b2()
        scale_x(0, 1)
        turn(1, 1)
        warm_tensor(2)
        scale_x(1, 0)
        cast(2, 0)
        cast(2, 1)
        quant_x(0)
        permute_early_w1_on_scalar(1)
        permute_late_s1()
        permute_early_w1((0,))
        turn(2, 0)
        turn_b1()
        warm_tensor(1)
        turn(2, 1)
        permute_late_w1(0)
        empty_b1()
        stage1(0, 0)
        scale_x(1, 1)
        permute_late_w1(1)
        quant_x(1, (0,))
        stage1(0, 1)
        quant_x(1, (1,))
        cast_on_gpsimd(3,1,1,"xg10")
        relu(0,0)
        cast(3,0)
        stage1(1,0)
        scale_x(2,0)
        weave_h_on_gpsimd(0,(0,))
        relu(0,1)
        cast(3,1,(0,))
        scale_x(2,1)
        stage1(1,1)
        turn(3,0)
        relu(1,0)
        weave_h(0,(1,))
        quant_x(2)
        quant_h(0)
        turn(3,1)
        weave_h_on_gpsimd(1, (0,), "xg2")
        relu(1, 1)
        cast(4, 0)
        cast(4, 1)
        stage1(2, 0)
        stage2(0)
        scale_x(3, 0)
        weave_h_on_gpsimd(1, (1,))
        stage1(2, 1)
        scale_x(3, 1)
        relu(2, 0)
        bias_v(0)
        turn(4, 0)
        turn(4, 1)
        quant_x(3)
        quant_h(1)
        stage1(3, 0, (0, 1))
        weave_h_on_gpsimd(2, (0,), "xg3")
        stage2(1)
        relu_in_pairs(2, 1)
        square_v(0)
        stage1(3, 0, (2, 3))
        scale_x(4, 0)
        scale_x(4, 1)
        stage1(3, 1)
        bias_v(1)
        weave_pairs(2, (1,))
        quant_x(4)
        relu(3, 0)
        clamp_v(0, 1)
        quant_h(2)
        stage2(2)
        weave_h(3, (0,))
        stage1(4, 0)
        relu(3, 1)
        root_v(0, 1)
        square_v(1)
        stage2(3)
        bias_v(2)
        weave_h(3, (1,))
        stage1(4, 1)
        relu(4, 0)
        square_v(2)
        stage2(4)
        bias_v(3)
        quant_h(3)
        stage2(5)
        relu(4,1)
        clamp_v(1,3)
        square_v(3)
        bias_v(4)
        finish_v(0)
        stage2(6)
        root_v(1,3)
        weave_h(4,BOTH)
        square_v(4)
        finish_v(1)
        clamp_v(3,4)
        finish_v_on_scalar(2,sides[0])
        root_v(3,4)
        clamp_v(4,5)
        finish_v_on_scalar(2,sides[1])
        quant_h(4)
        root_v(4,5)
        finish_v_on_scalar(3)
        end_stage2()
        bias_v(5)
        finish_v_on_gpsimd(4)
        square_v(5)
        bias_v(6)
        end_bias(0)
        square_v(6)
        end_bias(1)
        clamp_on_vector(5)
        root_of_floored(5)
        end_square_on_vector(1)
        end_square_on_scalar(0)
        clamp_on_vector(6)
        finish_v(5)
        root_of_floored(6)
        end_sum_and_clamp()
        finish_v(6)
        end_root()
        finish_v(END, sides)
